import numpy as np
import ml_dtypes


def mxq(x, axis, fmt="e4m3"):
    dtype, down = {"e4m3": (ml_dtypes.float8_e4m3fn, 7), "e5m2": (ml_dtypes.float8_e5m2, 14)}[fmt]
    v = np.moveaxis(np.asarray(x, np.float32).astype(ml_dtypes.bfloat16).astype(np.float64), axis, -1)
    blocks = v.reshape(v.shape[:-1] + (-1, 32))
    amax = np.abs(blocks).max(-1, keepdims=True)
    byte = np.maximum(np.where(amax > 0, np.frexp(amax)[1] - 1 + 127, 0) - down, 1)
    scale = np.exp2(byte - 127.0)
    codes = (blocks / scale).astype(np.float32).astype(dtype).astype(np.float64)
    return np.moveaxis((codes * scale).reshape(v.shape), -1, axis)


WIDE = False


def mx_kscale(k):
    if not WIDE:
        return np.ones(k)
    levels = np.array([10, -10, 5, -5, 0])
    if k % 512:
        return np.exp2(np.random.permutation(np.resize(levels, k // 32))).repeat(32)
    a = np.empty((k // 512, 16))
    for p in range(k // 512):
        a[p, :8] = np.random.permutation(np.resize(levels, 8))
        for g in range(8):
            far = levels[np.abs(levels - a[p, g]) >= 10]
            a[p, g + 8] = far[np.random.randint(len(far))]
    return np.exp2(a.ravel()).repeat(32)


BF16 = ml_dtypes.bfloat16


def bf(x):
    return np.asarray(x, np.float32).astype(BF16)


def f64(x):
    return np.asarray(x).astype(np.float64)


B, S, D, H, C = 1, 1024, 1024, 1024, 512


def draw0():
    s, t = mx_kscale(H), mx_kscale(S)
    return {"q": bf(np.random.standard_normal((B, S, H)) * 0.6 * s),
            "k": bf(np.random.standard_normal((B, S, H)) * 0.6 / s * t[:, None]),
            "v": bf(np.random.standard_normal((B, S, H)) * 0.6 / t[:, None]),
            "decay": bf(np.random.uniform(0.5, 1.5, S) * 2.0 / S)}


def core(q, k, v, decay):
    qq = mxq(f64(q), 2, "e4m3")
    kq = mxq(f64(k), 2, "e4m3")
    vq = mxq(f64(v), 1, "e4m3")
    idx = np.arange(S)
    diff = f64(np.abs(idx[None, :] - idx[:, None]))
    dm = np.exp(-f64(decay)[None, :] * diff) * np.tril(np.ones((S, S)))
    out = np.zeros((B, S, H))
    for r in range(0, S, C):
        e = r + C
        sc = (qq[:, r:e] @ kq[:, :e].transpose(0, 2, 1)) * dm[r:e, :e]
        sc = sc / np.sqrt(H)
        out[:, r:e] = mxq(sc, 2, "e4m3") @ vq[:, :e]
    return out


def e4m3fn_bytes(y):
    return np.clip(np.asarray(y, np.float64), -448.0, 448.0).astype(np.float32).astype(ml_dtypes.float8_e4m3fn).view(np.uint8)


def e4m3fn_values(b):
    return np.asarray(b, np.uint8).view(ml_dtypes.float8_e4m3fn).astype(np.float64)


def setup_inputs():
    d = draw0()
    x0 = np.asarray(d['v']).astype(np.float64)
    s = (np.max(np.abs(x0), axis=(0, 2), keepdims=True) / 448.0).astype(np.float32)
    out = {}
    for k, v in d.items():
        if k == 'v':
            out['v_bytes'] = e4m3fn_bytes(x0 / s.astype(np.float64))
            out['v_scale'] = s
        else:
            out[k] = v
    return out


def reference(q, k, v_bytes, v_scale, decay):
    return core(q, k, e4m3fn_values(v_bytes) * v_scale.astype(np.float64), decay)

@@ -1,0 +1,352 @@
+import math
+from contextlib import ExitStack
+
+import concourse.mybir as mybir
+from concourse.masks import make_identity
+
+F32 = mybir.dt.float32
+BF16 = mybir.dt.bfloat16
+U32 = mybir.dt.uint32
+U8 = mybir.dt.uint8
+E4M3FN = mybir.dt.float8_e4m3fn
+FP8X4 = mybir.dt.float8_e4m3fn_x4
+ALU = mybir.AluOpType
+ACT = mybir.ActivationFunctionType
+
+FLOPS = 2 * 1024 * (512 * 512 + 512 * 1024) * 2
+BIG = 2.0**100
+LOG_SCALE = -5.0 * math.log(2.0)
+
+
+def tile_simplifiedretnet_pa_kernel(tc, q, k, v_bytes, v_scale, decay, out):
+    nc = tc.nc
+    x_rows = {
+        "q": q.rearrange("o (c m b) f -> (o c) m b f", c=2, b=4),
+        "k": k.rearrange("o (c m b) f -> (o c) m b f", c=2, b=4),
+    }
+    v_rows = v_bytes.rearrange("o (g p t) n -> (o g) p t n", g=2, t=4)
+    o_rows = out.rearrange("o (c m b) n -> (o c) m b n", c=2, b=4)
+
+    with ExitStack() as ctx:
+        keep = ctx.enter_context(tc.tile_pool(name="keep", bufs=1))
+        ps_tp = ctx.enter_context(tc.psum_pool(name="ps_tp", bufs=3))
+        ps_sc = ctx.enter_context(tc.psum_pool(name="ps_sc", bufs=2))
+        ps_po = ctx.enter_context(tc.psum_pool(name="ps_po", bufs=3))
+        ctx.enter_context(tc.manual_schedule())
+
+        def sb(name, shape, dtype):
+            return keep.tile(shape, dtype, name=name, align_bytes=64)
+
+        raw = {(x, c): sb("raw_%s_%s" % (x, c,), [128, 4, 1024], BF16) for x in "qk" for c in range(2)}
+        grouped = {(x, c, b): sb("grp_%s_%s_%s" % (x, c, b,), [128, 2, 128, 2], F32) for x in "qk" for c in range(2) for b in range(4)}
+        codes = {(x, c, b): sb("cod_%s_%s_%s" % (x, c, b,), [128, 256], U32) for x in "qk" for c in range(2) for b in range(4)}
+        scales = {(x, c, b): sb("scl_%s_%s_%s" % (x, c, b,), [128, 256], U8) for x in "qk" for c in range(2) for b in range(4)}
+        vb = [sb("vb%s" % (g,), [128, 4, 1024], U8) for g in range(2)]
+        wide = [sb("wide%s" % (g,), [128, 4, 1024], BF16) for g in range(2)]
+        vi = {(g, h): sb("vi%s_%s" % (g, h,), [128, 512, 4], BF16) for g in range(2) for h in range(2)}
+        v_codes = {(g, h): sb("vc%s_%s" % (g, h,), [128, 512], U32) for g in range(2) for h in range(2)}
+        v_scl = {(g, h): sb("vx%s_%s" % (g, h,), [128, 512], U8) for g in range(2) for h in range(2)}
+        gain = [sb("gain%s" % (e,), [128, 128, 16], F32) for e in range(3)]
+        pairs = [(0, 0), (0, 1), (1, 1)]
+        s_bf = {(g, c, b): sb("s%s_%s_%s" % (g, c, b,), [128, 128, 4], BF16) for g, c in pairs for b in range(4)}
+        s_codes = {(g, c, b): sb("sc%s_%s_%s" % (g, c, b,), [128, 128], U32) for g, c in pairs for b in range(4)}
+        s_scl = {(g, c, b): sb("sx%s_%s_%s" % (g, c, b,), [128, 128], U8) for g, c in pairs for b in range(4)}
+        result = {(c, b, h): sb("o%s_%s_%s" % (c, b, h,), [128, 512], F32) for c in range(2) for b in range(4) for h in range(2)}
+        ident = sb("ident", [128, 128], F32)
+        dist = sb("dist", [128, 7, 128], F32)
+        near = sb("near", [128, 7, 128], F32)
+        far_bias = sb("far_bias", [128, 4], F32)
+        dk = sb("dk", [128, 2, 4], BF16)
+        nd = sb("nd", [128, 8], F32)
+        vs = sb("vs", [128, 2, 4], F32)
+        warm = sb("warm", [128, 8], F32)
+        warm_out = sb("warm_out", [128, 8], F32)
+        zeros = sb("zeros", [128, 512], BF16)
+
+        psum = {}
+
+        def load(name, c, lo, hi):
+            if name == "v":
+                nc.sync.dma_start(out=vb[c][:, lo:hi, :], in_=v_rows[c][:, lo:hi, :])
+            else:
+                nc.sync.dma_start(out=raw[name, c][:, lo:hi, :], in_=x_rows[name][c][:, lo:hi, :])
+
+        def TR(x, c, b):
+            bank = ps_tp.tile([128, 2, 2, 128], F32, name="tp")
+            psum[x, c, b] = bank
+            words = raw[x, c][:, b, :].bitcast(F32)
+            for g in range(2):
+                for u in range(2):
+                    nc.tensor.transpose(bank[:, g, u, :], words[:, 256 * g + u : 256 * (g + 1) : 2], ident[:])
+
+        def CP(x, c, b, eng="S"):
+            src = psum[x, c, b][:].rearrange("p g u r -> p g r u")
+            if eng == "S":
+                nc.scalar.copy(grouped[x, c, b][:], src)
+            else:
+                nc.vector.tensor_copy(out=grouped[x, c, b][:], in_=src)
+
+        def QZ(x, c, b):
+            nc.vector.quantize_mx(
+                out=codes[x, c, b][:].bitcast(FP8X4),
+                scales=scales[x, c, b][:],
+                in_=grouped[x, c, b][:].rearrange("p g r u -> p (g r u)").bitcast(BF16),
+            )
+
+        def WD(g, t, eng="V"):
+            src = vb[g][:, t, :].bitcast(E4M3FN)
+            if eng == "V":
+                nc.vector.tensor_scalar(out=wide[g][:, t, :], in0=src, scalar1=vs[:, g, t : t + 1], scalar2=None, op0=ALU.mult)
+            else:
+                nc.scalar.activation(out=wide[g][:, t, :], in_=src, func=ACT.Copy, scale=vs[:, g, t : t + 1])
+
+        def IL(g, h):
+            nc.vector.tensor_copy(
+                out=vi[g, h][:].rearrange("p (m i) t -> p m t i", i=4),
+                in_=wide[g][:, :, 512 * h : 512 * (h + 1)].rearrange("p t (m i) -> p m t i", i=4),
+            )
+
+        def QV(g, h):
+            nc.vector.quantize_mx(
+                out=v_codes[g, h][:].bitcast(FP8X4), scales=v_scl[g, h][:], in_=vi[g, h][:].rearrange("p n t -> p (n t)")
+            )
+
+        def EX(e, t):
+            table = dist if e == 1 else near
+            col = 4 * (e // 2) + t
+            nc.scalar.activation(
+                out=gain[e][:, :, 4 * t : 4 * (t + 1)],
+                in_=table[:, 3 - t : 7 - t, :].rearrange("p b (m i) -> p (b m) i", i=4),
+                func=ACT.Exp,
+                bias=far_bias[:, t : t + 1] if e == 1 else LOG_SCALE,
+                scale=nd[:, col : col + 1],
+            )
+
+        def M1(g, c, b, pool="sc"):
+            bank = (ps_sc if pool == "sc" else ps_tp).tile([128, 4, 128], F32, name=pool)
+            psum["s", g, c, b] = bank
+            for t in range(4):
+                for f in range(2):
+                    cols = slice(128 * f, 128 * (f + 1))
+                    nc.tensor.matmul_mx(
+                        out=bank[:, t, :],
+                        lhsT=codes["k", g, t][:, cols].bitcast(FP8X4),
+                        lhsT_scale=scales["k", g, t][:, cols],
+                        rhs=codes["q", c, b][:, cols].bitcast(FP8X4),
+                        rhs_scale=scales["q", c, b][:, cols],
+                        start=(f == 0),
+                        stop=(f == 1),
+                    )
+
+        def MK(g, c, b):
+            nc.vector.tensor_tensor(
+                out=s_bf[g, c, b][:].rearrange("p (m i) t -> p m t i", i=4),
+                in0=psum["s", g, c, b][:].rearrange("p t (m i) -> p m t i", i=4),
+                in1=gain[g + c][:, 32 * b : 32 * (b + 1), :].rearrange("p m (t i) -> p m t i", i=4),
+                op=ALU.mult,
+            )
+
+        def QS(g, c, b):
+            nc.vector.quantize_mx(
+                out=s_codes[g, c, b][:].bitcast(FP8X4),
+                scales=s_scl[g, c, b][:],
+                in_=s_bf[g, c, b][:].rearrange("p i t -> p (i t)"),
+            )
+
+        def M2(c, b, h, gs=None, pool="po"):
+            if gs is None:
+                gs = range(c + 1)
+            if ("o", c, b, h) not in psum:
+                psum["o", c, b, h] = (ps_po if pool == "po" else ps_tp).tile([128, 512], F32, name=pool)
+            for g in gs:
+                nc.tensor.matmul_mx(
+                    out=psum["o", c, b, h][:],
+                    lhsT=s_codes[g, c, b][:].bitcast(FP8X4),
+                    lhsT_scale=s_scl[g, c, b][:],
+                    rhs=v_codes[g, h][:].bitcast(FP8X4),
+                    rhs_scale=v_scl[g, h][:],
+                    start=(g == 0),
+                    stop=(g == c),
+                )
+
+        def CO(c, b, h, eng="S"):
+            src = psum["o", c, b, h]
+            res = result[c, b, h]
+            if eng == "S":
+                nc.scalar.copy(res[:], src[:])
+            else:
+                nc.vector.tensor_copy(out=res[:], in_=src[:])
+            nc.sync.dma_start(out=o_rows[c][:, b, 512 * h : 512 * (h + 1)], in_=res[:])
+
+        def DUMMY(n, width=512):
+            bank = ps_sc.tile([128, 512], F32, name="sc")
+            for i in range(n):
+                nc.tensor.matmul(bank[:, :width], lhsT=zeros[:, :128], rhs=zeros[:, :width], start=True, stop=True)
+
+        nc.scalar.dma_start(out=dk[:], in_=decay.rearrange("(g p t) -> p g t", g=2, t=4))
+        nc.scalar.dma_start(out=vs[:], in_=v_scale.rearrange("o (g p t) i -> p (o g) (t i)", g=2, t=4))
+        load("v", 0, 0, 2)
+        load("v", 0, 2, 4)
+        for x, c in (("k", 0), ("q", 0), ("q", 1), ("k", 1)):
+            load(x, c, 0, 2)
+            load(x, c, 2, 4)
+        load("v", 1, 0, 4)
+        nc.vector.memset(warm[:], 0.0)
+        nc.vector.memset(zeros[:], 0.0)
+        nc.scalar.activation(out=warm_out[:], in_=warm[:], func=ACT.Exp)
+        nc.gpsimd.iota(dist[:], pattern=[[1, 7], [4, 128]], base=-3, channel_multiplier=-4, allow_small_or_imprecise_dtypes=True)
+        make_identity(nc, ident[:])
+        nc.vector.scalar_tensor_tensor(out=near[:], in0=dist[:], scalar=-BIG, in1=dist[:], op0=ALU.mult, op1=ALU.max)
+        nc.vector.tensor_scalar(out=nd[:], in0=dk[:].rearrange("p g t -> p (g t)"), scalar1=1.0 / 2.0**90, scalar2=-1.0, op0=ALU.max, op1=ALU.mult)
+        nc.vector.tensor_scalar(out=far_bias[:], in0=nd[:, 0:4], scalar1=512.0, scalar2=LOG_SCALE, op0=ALU.mult, op1=ALU.add)
+
+        DUMMY(6)
+        EX(0, 0)
+        EX(0, 1)
+        EX(0, 2)
+        EX(0, 3)
+        WD(0, 0, 'V')
+        WD(0, 1, 'V')
+        WD(0, 2, 'V')
+        WD(0, 3, 'V')
+        TR('k', 0, 0)
+        CP('k', 0, 0)
+        TR('k', 0, 1)
+        CP('k', 0, 1)
+        DUMMY(1)
+        TR('k', 0, 2)
+        CP('k', 0, 2)
+        TR('k', 0, 3)
+        CP('k', 0, 3)
+        DUMMY(1)
+        IL(0, 0)
+        QZ('k', 0, 0)
+        QZ('k', 0, 1)
+        QZ('k', 0, 2)
+        QZ('k', 0, 3)
+        TR('q', 0, 0)
+        CP('q', 0, 0)
+        TR('q', 0, 1)
+        CP('q', 0, 1)
+        DUMMY(1)
+        TR('q', 0, 2)
+        CP('q', 0, 2)
+        TR('q', 0, 3)
+        CP('q', 0, 3)
+        QZ('q', 0, 0)
+        QZ('q', 0, 1)
+        M1(0, 0, 0)
+        M1(0, 0, 1)
+        IL(0, 1)
+        EX(1, 0)
+        EX(1, 1)
+        TR('q', 1, 0)
+        CP('q', 1, 0)
+        TR('q', 1, 1)
+        CP('q', 1, 1)
+        TR('q', 1, 2)
+        CP('q', 1, 2)
+        QZ('q', 0, 2)
+        MK(0, 0, 0)
+        QZ('q', 0, 3)
+        MK(0, 0, 1)
+        QV(0, 0)
+        QS(0, 0, 0)
+        M1(0, 0, 2)
+        M1(0, 0, 3)
+        EX(1, 2)
+        EX(1, 3)
+        TR('q', 1, 3)
+        CP('q', 1, 3)
+        QZ('q', 1, 0)
+        QV(0, 1)
+        MK(0, 0, 2)
+        QS(0, 0, 1)
+        QZ('q', 1, 1)
+        MK(0, 0, 3)
+        QS(0, 0, 2)
+        QZ('q', 1, 2)
+        TR('k', 1, 0)
+        CP('k', 1, 0)
+        TR('k', 1, 1)
+        CP('k', 1, 1)
+        TR('k', 1, 2)
+        CP('k', 1, 2)
+        QZ('q', 1, 3)
+        QS(0, 0, 3)
+        M1(0, 1, 0)
+        M1(0, 1, 1)
+        WD(1, 0, 'V')
+        WD(1, 1, 'V')
+        WD(1, 2, 'V')
+        TR('k', 1, 3)
+        CP('k', 1, 3)
+        M2(0, 0, 0)
+        M2(0, 1, 0)
+        M2(0, 2, 0)
+        WD(1, 3, 'S')
+        QZ('k', 1, 0)
+        MK(0, 1, 0)
+        QZ('k', 1, 1)
+        CO(0, 0, 0)
+        CO(0, 1, 0)
+        CO(0, 2, 0)
+        QZ('k', 1, 2)
+        QS(0, 1, 0)
+        MK(0, 1, 1)
+        QZ('k', 1, 3)
+        M1(0, 1, 2)
+        M1(1, 1, 0, 'tp')
+        M1(1, 1, 1, 'tp')
+        QS(0, 1, 1)
+        IL(1, 0)
+        IL(1, 1)
+        EX(2, 0)
+        EX(2, 1)
+        EX(2, 2)
+        EX(2, 3)
+        M2(0, 3, 0)
+        M2(0, 0, 1)
+        M2(0, 1, 1)
+        CO(0, 3, 0)
+        CO(0, 0, 1)
+        CO(0, 1, 1)
+        M1(0, 1, 3)
+        M1(1, 1, 2, 'tp')
+        M2(0, 2, 1)
+        M2(0, 3, 1)
+        CO(0, 2, 1)
+        CO(0, 3, 1)
+        QV(1, 0)
+        MK(1, 1, 0)
+        QV(1, 1)
+        QS(1, 1, 0)
+        M1(1, 1, 3, 'tp')
+        MK(1, 1, 1)
+        MK(0, 1, 2)
+        M2(1, 0, 0)
+        CO(1, 0, 0)
+        M2(1, 0, 1)
+        CO(1, 0, 1)
+        QS(1, 1, 1)
+        MK(1, 1, 2)
+        QS(0, 1, 2)
+        M2(1, 1, 0)
+        CO(1, 1, 0)
+        M2(1, 1, 1)
+        CO(1, 1, 1)
+        MK(0, 1, 3)
+        QS(1, 1, 2)
+        M2(1, 2, 0)
+        CO(1, 2, 0)
+        M2(1, 2, 1)
+        CO(1, 2, 1)
+        MK(1, 1, 3)
+        QS(0, 1, 3)
+        QS(1, 1, 3)
+        M2(1, 3, 0, (0,))
+        M2(1, 3, 1, (0,))
+        M2(1, 3, 0, (1,))
+        CO(1, 3, 0)
+        M2(1, 3, 1, (1,))
+        CO(1, 3, 1, 'V')

@@ -16,71 +16,75 @@ ACT = mybir.ActivationFunctionType
 FLOPS = 2 * 1024 * (512 * 512 + 512 * 1024) * 2
 BIG = 2.0**100
 LOG_SCALE = -5.0 * math.log(2.0)
+BANKS = 8
 
 
 def tile_simplifiedretnet_pa_kernel(tc, q, k, v_bytes, v_scale, decay, out):
     nc = tc.nc
     x_rows = {
-        "q": q.rearrange("o (c m b) f -> (o c) m b f", c=2, b=4),
+        "q": q.rearrange("o (c b m) f -> (o c) m b f", c=2, b=4),
         "k": k.rearrange("o (c m b) f -> (o c) m b f", c=2, b=4),
     }
     v_rows = v_bytes.rearrange("o (g p t) n -> (o g) p t n", g=2, t=4)
-    o_rows = out.rearrange("o (c m b) n -> (o c) m b n", c=2, b=4)
+    o_rows = out.rearrange("o (c b m) n -> (o c) m b n", c=2, b=4)
 
     with ExitStack() as ctx:
         keep = ctx.enter_context(tc.tile_pool(name="keep", bufs=1))
-        ps_tp = ctx.enter_context(tc.psum_pool(name="ps_tp", bufs=3))
-        ps_sc = ctx.enter_context(tc.psum_pool(name="ps_sc", bufs=2))
-        ps_po = ctx.enter_context(tc.psum_pool(name="ps_po", bufs=3))
+        banks = ctx.enter_context(tc.psum_pool(name="banks", bufs=BANKS))
         ctx.enter_context(tc.manual_schedule())
 
         def sb(name, shape, dtype):
             return keep.tile(shape, dtype, name=name, align_bytes=64)
 
-        raw = {(x, c): sb("raw_%s_%s" % (x, c,), [128, 4, 1024], BF16) for x in "qk" for c in range(2)}
-        grouped = {(x, c, b): sb("grp_%s_%s_%s" % (x, c, b,), [128, 2, 128, 2], F32) for x in "qk" for c in range(2) for b in range(4)}
-        codes = {(x, c, b): sb("cod_%s_%s_%s" % (x, c, b,), [128, 256], U32) for x in "qk" for c in range(2) for b in range(4)}
-        scales = {(x, c, b): sb("scl_%s_%s_%s" % (x, c, b,), [128, 256], U8) for x in "qk" for c in range(2) for b in range(4)}
+        blocks = [(x, c, b) for x in "qk" for c in range(2) for b in range(4)]
+        halves = [(g, h) for g in range(2) for h in range(2)]
+        pairs = [(0, 0), (0, 1), (1, 1)]
+        tiles = [(g, c, b) for g, c in pairs for b in range(4)]
+        raw = {(x, c): sb("raw_%s_%s" % (x, c), [128, 4, 1024], BF16) for x in "qk" for c in range(2)}
+        grouped = {key: sb("grp_%s_%s_%s" % key, [128, 2, 128, 2], F32) for key in blocks}
+        codes = {key: sb("cod_%s_%s_%s" % key, [128, 256], U32) for key in blocks}
+        scales = {key: sb("scl_%s_%s_%s" % key, [128, 256], U8) for key in blocks}
         vb = [sb("vb%s" % (g,), [128, 4, 1024], U8) for g in range(2)]
         wide = [sb("wide%s" % (g,), [128, 4, 1024], BF16) for g in range(2)]
-        vi = {(g, h): sb("vi%s_%s" % (g, h,), [128, 512, 4], BF16) for g in range(2) for h in range(2)}
-        v_codes = {(g, h): sb("vc%s_%s" % (g, h,), [128, 512], U32) for g in range(2) for h in range(2)}
-        v_scl = {(g, h): sb("vx%s_%s" % (g, h,), [128, 512], U8) for g in range(2) for h in range(2)}
+        vi = {key: sb("vi%s_%s" % key, [128, 512, 4], BF16) for key in halves}
+        v_codes = {key: sb("vc%s_%s" % key, [128, 512], U32) for key in halves}
+        v_scl = {key: sb("vx%s_%s" % key, [128, 512], U8) for key in halves}
         gain = [sb("gain%s" % (e,), [128, 128, 16], F32) for e in range(3)]
-        pairs = [(0, 0), (0, 1), (1, 1)]
-        s_bf = {(g, c, b): sb("s%s_%s_%s" % (g, c, b,), [128, 128, 4], BF16) for g, c in pairs for b in range(4)}
-        s_codes = {(g, c, b): sb("sc%s_%s_%s" % (g, c, b,), [128, 128], U32) for g, c in pairs for b in range(4)}
-        s_scl = {(g, c, b): sb("sx%s_%s_%s" % (g, c, b,), [128, 128], U8) for g, c in pairs for b in range(4)}
-        result = {(c, b, h): sb("o%s_%s_%s" % (c, b, h,), [128, 512], F32) for c in range(2) for b in range(4) for h in range(2)}
+        s_bf = {key: sb("s%s_%s_%s" % key, [128, 128, 4], BF16) for key in tiles}
+        s_codes = {key: sb("sc%s_%s_%s" % key, [128, 128], U32) for key in tiles}
+        s_scl = {key: sb("sx%s_%s_%s" % key, [128, 128], U8) for key in tiles}
+        result = {(c, b, h): sb("o%s_%s_%s" % (c, b, h), [128, 512], F32) for c in range(2) for b in range(4) for h in range(2)}
         ident = sb("ident", [128, 128], F32)
-        dist = sb("dist", [128, 7, 128], F32)
-        near = sb("near", [128, 7, 128], F32)
+        dist = sb("dist", [128, 516], F32)
+        near = sb("near", [128, 516], F32)
         far_bias = sb("far_bias", [128, 4], F32)
         dk = sb("dk", [128, 2, 4], BF16)
         nd = sb("nd", [128, 8], F32)
         vs = sb("vs", [128, 2, 4], F32)
         warm = sb("warm", [128, 8], F32)
         warm_out = sb("warm_out", [128, 8], F32)
-        zeros = sb("zeros", [128, 512], BF16)
 
         psum = {}
 
-        def load(name, c, lo, hi):
-            if name == "v":
-                nc.sync.dma_start(out=vb[c][:, lo:hi, :], in_=v_rows[c][:, lo:hi, :])
-            else:
-                nc.sync.dma_start(out=raw[name, c][:, lo:hi, :], in_=x_rows[name][c][:, lo:hi, :])
+        def load(x, c, lo, hi):
+            nc.sync.dma_start(out=raw[x, c][:, lo:hi, :], in_=x_rows[x][c][:, lo:hi, :])
+
+        def loadv(g, t0, t1, n0, n1):
+            nc.sync.dma_start(out=vb[g][:, t0:t1, n0:n1], in_=v_rows[g][:, t0:t1, n0:n1])
+
+        def new_bank(key):
+            psum[key] = banks.tile([128, 512], F32, name="bank")
+            return psum[key]
 
         def TR(x, c, b):
-            bank = ps_tp.tile([128, 2, 2, 128], F32, name="tp")
-            psum[x, c, b] = bank
+            bank = new_bank(("TR", x, c, b))[:].rearrange("p (g u r) -> p g u r", g=2, u=2)
             words = raw[x, c][:, b, :].bitcast(F32)
             for g in range(2):
                 for u in range(2):
                     nc.tensor.transpose(bank[:, g, u, :], words[:, 256 * g + u : 256 * (g + 1) : 2], ident[:])
 
-        def CP(x, c, b, eng="S"):
-            src = psum[x, c, b][:].rearrange("p g u r -> p g r u")
+        def CP(x, c, b, eng):
+            src = psum["TR", x, c, b][:].rearrange("p (g u r) -> p g r u", g=2, u=2)
             if eng == "S":
                 nc.scalar.copy(grouped[x, c, b][:], src)
             else:
@@ -93,12 +97,13 @@ def tile_simplifiedretnet_pa_kernel(tc, q, k, v_bytes, v_scale, decay, out):
                 in_=grouped[x, c, b][:].rearrange("p g r u -> p (g r u)").bitcast(BF16),
             )
 
-        def WD(g, t, eng="V"):
-            src = vb[g][:, t, :].bitcast(E4M3FN)
+        def WD(g, t, h, eng):
+            cols = slice(0, 1024) if h == 2 else slice(512 * h, 512 * (h + 1))
+            src = vb[g][:, t, cols].bitcast(E4M3FN)
             if eng == "V":
-                nc.vector.tensor_scalar(out=wide[g][:, t, :], in0=src, scalar1=vs[:, g, t : t + 1], scalar2=None, op0=ALU.mult)
+                nc.vector.tensor_scalar(out=wide[g][:, t, cols], in0=src, scalar1=vs[:, g, t : t + 1], scalar2=None, op0=ALU.mult)
             else:
-                nc.scalar.activation(out=wide[g][:, t, :], in_=src, func=ACT.Copy, scale=vs[:, g, t : t + 1])
+                nc.scalar.activation(out=wide[g][:, t, cols], in_=src, func=ACT.Copy, scale=vs[:, g, t : t + 1])
 
         def IL(g, h):
             nc.vector.tensor_copy(
@@ -116,20 +121,19 @@ def tile_simplifiedretnet_pa_kernel(tc, q, k, v_bytes, v_scale, decay, out):
             col = 4 * (e // 2) + t
             nc.scalar.activation(
                 out=gain[e][:, :, 4 * t : 4 * (t + 1)],
-                in_=table[:, 3 - t : 7 - t, :].rearrange("p b (m i) -> p (b m) i", i=4),
+                in_=table[:, 3 - t : 515 - t].rearrange("p (m i) -> p m i", i=4),
                 func=ACT.Exp,
                 bias=far_bias[:, t : t + 1] if e == 1 else LOG_SCALE,
                 scale=nd[:, col : col + 1],
             )
 
-        def M1(g, c, b, pool="sc"):
-            bank = (ps_sc if pool == "sc" else ps_tp).tile([128, 4, 128], F32, name=pool)
-            psum["s", g, c, b] = bank
+        def M1(g, c, b):
+            bank = new_bank(("M1", g, c, b))
             for t in range(4):
                 for f in range(2):
                     cols = slice(128 * f, 128 * (f + 1))
                     nc.tensor.matmul_mx(
-                        out=bank[:, t, :],
+                        out=bank[:, 128 * t : 128 * (t + 1)],
                         lhsT=codes["k", g, t][:, cols].bitcast(FP8X4),
                         lhsT_scale=scales["k", g, t][:, cols],
                         rhs=codes["q", c, b][:, cols].bitcast(FP8X4),
@@ -141,7 +145,7 @@ def tile_simplifiedretnet_pa_kernel(tc, q, k, v_bytes, v_scale, decay, out):
         def MK(g, c, b):
             nc.vector.tensor_tensor(
                 out=s_bf[g, c, b][:].rearrange("p (m i) t -> p m t i", i=4),
-                in0=psum["s", g, c, b][:].rearrange("p t (m i) -> p m t i", i=4),
+                in0=psum["M1", g, c, b][:].rearrange("p (t m i) -> p m t i", t=4, i=4),
                 in1=gain[g + c][:, 32 * b : 32 * (b + 1), :].rearrange("p m (t i) -> p m t i", i=4),
                 op=ALU.mult,
             )
@@ -153,14 +157,11 @@ def tile_simplifiedretnet_pa_kernel(tc, q, k, v_bytes, v_scale, decay, out):
                 in_=s_bf[g, c, b][:].rearrange("p i t -> p (i t)"),
             )
 
-        def M2(c, b, h, gs=None, pool="po"):
-            if gs is None:
-                gs = range(c + 1)
-            if ("o", c, b, h) not in psum:
-                psum["o", c, b, h] = (ps_po if pool == "po" else ps_tp).tile([128, 512], F32, name=pool)
-            for g in gs:
+        def M2(c, b, h):
+            bank = new_bank(("M2", c, b, h))
+            for g in range(c + 1):
                 nc.tensor.matmul_mx(
-                    out=psum["o", c, b, h][:],
+                    out=bank[:],
                     lhsT=s_codes[g, c, b][:].bitcast(FP8X4),
                     lhsT_scale=s_scl[g, c, b][:],
                     rhs=v_codes[g, h][:].bitcast(FP8X4),
@@ -169,184 +170,203 @@ def tile_simplifiedretnet_pa_kernel(tc, q, k, v_bytes, v_scale, decay, out):
                     stop=(g == c),
                 )
 
-        def CO(c, b, h, eng="S"):
-            src = psum["o", c, b, h]
+        def CO(c, b, h, eng):
+            src = psum["M2", c, b, h]
             res = result[c, b, h]
             if eng == "S":
                 nc.scalar.copy(res[:], src[:])
             else:
                 nc.vector.tensor_copy(out=res[:], in_=src[:])
-            nc.sync.dma_start(out=o_rows[c][:, b, 512 * h : 512 * (h + 1)], in_=res[:])
 
-        def DUMMY(n, width=512):
-            bank = ps_sc.tile([128, 512], F32, name="sc")
-            for i in range(n):
-                nc.tensor.matmul(bank[:, :width], lhsT=zeros[:, :128], rhs=zeros[:, :width], start=True, stop=True)
+        def ST(c, b, h):
+            nc.sync.dma_start(out=o_rows[c][:, b, 512 * h : 512 * (h + 1)], in_=result[c, b, h][:])
 
         nc.scalar.dma_start(out=dk[:], in_=decay.rearrange("(g p t) -> p g t", g=2, t=4))
         nc.scalar.dma_start(out=vs[:], in_=v_scale.rearrange("o (g p t) i -> p (o g) (t i)", g=2, t=4))
-        load("v", 0, 0, 2)
-        load("v", 0, 2, 4)
-        for x, c in (("k", 0), ("q", 0), ("q", 1), ("k", 1)):
-            load(x, c, 0, 2)
-            load(x, c, 2, 4)
-        load("v", 1, 0, 4)
+        loadv(0, 0, 4, 0, 512)
+        load("k", 0, 0, 1)
+        load("k", 0, 1, 2)
+        load("k", 0, 2, 3)
+        load("k", 0, 3, 4)
+        load("q", 0, 0, 1)
+        load("q", 0, 1, 2)
+        loadv(0, 0, 4, 512, 1024)
+        load("q", 0, 2, 3)
+        load("q", 0, 3, 4)
+        load("q", 1, 0, 2)
+        loadv(1, 0, 4, 0, 1024)
+        load("k", 1, 0, 2)
+        load("k", 1, 2, 4)
+        load("q", 1, 2, 4)
         nc.vector.memset(warm[:], 0.0)
-        nc.vector.memset(zeros[:], 0.0)
         nc.scalar.activation(out=warm_out[:], in_=warm[:], func=ACT.Exp)
-        nc.gpsimd.iota(dist[:], pattern=[[1, 7], [4, 128]], base=-3, channel_multiplier=-4, allow_small_or_imprecise_dtypes=True)
+        nc.gpsimd.iota(dist[:], pattern=[[1, 516]], base=-3, channel_multiplier=-4, allow_small_or_imprecise_dtypes=True)
         make_identity(nc, ident[:])
         nc.vector.scalar_tensor_tensor(out=near[:], in0=dist[:], scalar=-BIG, in1=dist[:], op0=ALU.mult, op1=ALU.max)
         nc.vector.tensor_scalar(out=nd[:], in0=dk[:].rearrange("p g t -> p (g t)"), scalar1=1.0 / 2.0**90, scalar2=-1.0, op0=ALU.max, op1=ALU.mult)
         nc.vector.tensor_scalar(out=far_bias[:], in0=nd[:, 0:4], scalar1=512.0, scalar2=LOG_SCALE, op0=ALU.mult, op1=ALU.add)
 
-        DUMMY(6)
+        TR("k", 0, 0)
+        TR("k", 0, 1)
+        TR("k", 0, 2)
+        TR("k", 0, 3)
+        TR("q", 0, 0)
+        TR("q", 0, 1)
+        TR("q", 0, 2)
+        TR("q", 0, 3)
         EX(0, 0)
         EX(0, 1)
         EX(0, 2)
+        CP("k", 0, 0, "S")
+        CP("k", 0, 1, "S")
+        CP("k", 0, 2, "S")
+        CP("k", 0, 3, "S")
+        CP("q", 0, 0, "S")
+        CP("q", 0, 1, "S")
         EX(0, 3)
-        WD(0, 0, 'V')
-        WD(0, 1, 'V')
-        WD(0, 2, 'V')
-        WD(0, 3, 'V')
-        TR('k', 0, 0)
-        CP('k', 0, 0)
-        TR('k', 0, 1)
-        CP('k', 0, 1)
-        DUMMY(1)
-        TR('k', 0, 2)
-        CP('k', 0, 2)
-        TR('k', 0, 3)
-        CP('k', 0, 3)
-        DUMMY(1)
-        IL(0, 0)
-        QZ('k', 0, 0)
-        QZ('k', 0, 1)
-        QZ('k', 0, 2)
-        QZ('k', 0, 3)
-        TR('q', 0, 0)
-        CP('q', 0, 0)
-        TR('q', 0, 1)
-        CP('q', 0, 1)
-        DUMMY(1)
-        TR('q', 0, 2)
-        CP('q', 0, 2)
-        TR('q', 0, 3)
-        CP('q', 0, 3)
-        QZ('q', 0, 0)
-        QZ('q', 0, 1)
-        M1(0, 0, 0)
-        M1(0, 0, 1)
-        IL(0, 1)
+        CP("q", 0, 2, "S")
+        CP("q", 0, 3, "S")
         EX(1, 0)
         EX(1, 1)
-        TR('q', 1, 0)
-        CP('q', 1, 0)
-        TR('q', 1, 1)
-        CP('q', 1, 1)
-        TR('q', 1, 2)
-        CP('q', 1, 2)
-        QZ('q', 0, 2)
-        MK(0, 0, 0)
-        QZ('q', 0, 3)
-        MK(0, 0, 1)
-        QV(0, 0)
-        QS(0, 0, 0)
-        M1(0, 0, 2)
-        M1(0, 0, 3)
         EX(1, 2)
         EX(1, 3)
-        TR('q', 1, 3)
-        CP('q', 1, 3)
-        QZ('q', 1, 0)
+        WD(0, 0, 0, "V")
+        WD(0, 1, 0, "V")
+        WD(0, 2, 0, "V")
+        WD(0, 3, 0, "V")
+        IL(0, 0)
+        QZ("k", 0, 0)
+        QZ("k", 0, 1)
+        QV(0, 0)
+        QZ("k", 0, 2)
+        QZ("k", 0, 3)
+        WD(0, 0, 1, "V")
+        QZ("q", 0, 0)
+        WD(0, 1, 1, "V")
+        QZ("q", 0, 1)
+        WD(0, 2, 1, "V")
+        WD(0, 3, 1, "V")
+        QZ("q", 0, 2)
+        IL(0, 1)
+        QZ("q", 0, 3)
+        M1(0, 0, 0)
+        M1(0, 0, 1)
+        TR("q", 1, 0)
+        TR("q", 1, 1)
+        M1(0, 0, 2)
+        M1(0, 0, 3)
+        TR("k", 1, 0)
+        TR("k", 1, 1)
+        CP("q", 1, 0, "S")
+        CP("q", 1, 1, "S")
+        WD(1, 2, 2, "S")
+        WD(1, 3, 2, "S")
+        CP("k", 1, 0, "S")
+        CP("k", 1, 1, "S")
+        MK(0, 0, 0)
         QV(0, 1)
-        MK(0, 0, 2)
+        MK(0, 0, 1)
+        QS(0, 0, 0)
+        QZ("q", 1, 0)
         QS(0, 0, 1)
-        QZ('q', 1, 1)
+        QZ("q", 1, 1)
+        MK(0, 0, 2)
+        WD(1, 0, 2, "V")
         MK(0, 0, 3)
         QS(0, 0, 2)
-        QZ('q', 1, 2)
-        TR('k', 1, 0)
-        CP('k', 1, 0)
-        TR('k', 1, 1)
-        CP('k', 1, 1)
-        TR('k', 1, 2)
-        CP('k', 1, 2)
-        QZ('q', 1, 3)
+        WD(1, 1, 2, "V")
         QS(0, 0, 3)
-        M1(0, 1, 0)
-        M1(0, 1, 1)
-        WD(1, 0, 'V')
-        WD(1, 1, 'V')
-        WD(1, 2, 'V')
-        TR('k', 1, 3)
-        CP('k', 1, 3)
-        M2(0, 0, 0)
-        M2(0, 1, 0)
-        M2(0, 2, 0)
-        WD(1, 3, 'S')
-        QZ('k', 1, 0)
-        MK(0, 1, 0)
-        QZ('k', 1, 1)
-        CO(0, 0, 0)
-        CO(0, 1, 0)
-        CO(0, 2, 0)
-        QZ('k', 1, 2)
-        QS(0, 1, 0)
-        MK(0, 1, 1)
-        QZ('k', 1, 3)
-        M1(0, 1, 2)
-        M1(1, 1, 0, 'tp')
-        M1(1, 1, 1, 'tp')
-        QS(0, 1, 1)
+        QZ("k", 1, 0)
+        QZ("k", 1, 1)
         IL(1, 0)
+        M2(0, 0, 0)
+        M2(0, 0, 1)
+        M1(0, 1, 0)
+        TR("k", 1, 2)
+        TR("k", 1, 3)
+        M2(0, 1, 0)
+        M2(0, 1, 1)
+        M1(0, 1, 1)
+        CO(0, 0, 0, "S")
+        ST(0, 0, 0)
+        CO(0, 0, 1, "S")
+        ST(0, 0, 1)
+        CP("k", 1, 2, "S")
+        CP("k", 1, 3, "S")
+        CO(0, 1, 0, "S")
+        ST(0, 1, 0)
+        CO(0, 1, 1, "S")
+        ST(0, 1, 1)
+        MK(0, 1, 0)
+        QZ("k", 1, 2)
+        QV(1, 0)
+        QS(0, 1, 0)
+        QZ("k", 1, 3)
+        MK(0, 1, 1)
         IL(1, 1)
+        TR("q", 1, 2)
+        TR("q", 1, 3)
+        M1(1, 1, 0)
+        M1(1, 1, 1)
+        M2(0, 2, 0)
+        M2(0, 2, 1)
+        CP("q", 1, 2, "S")
+        CP("q", 1, 3, "S")
         EX(2, 0)
         EX(2, 1)
         EX(2, 2)
         EX(2, 3)
-        M2(0, 3, 0)
-        M2(0, 0, 1)
-        M2(0, 1, 1)
-        CO(0, 3, 0)
-        CO(0, 0, 1)
-        CO(0, 1, 1)
-        M1(0, 1, 3)
-        M1(1, 1, 2, 'tp')
-        M2(0, 2, 1)
-        M2(0, 3, 1)
-        CO(0, 2, 1)
-        CO(0, 3, 1)
-        QV(1, 0)
+        CO(0, 2, 0, "S")
+        ST(0, 2, 0)
+        CO(0, 2, 1, "S")
+        ST(0, 2, 1)
+        QZ("q", 1, 2)
+        QS(0, 1, 1)
+        QZ("q", 1, 3)
         MK(1, 1, 0)
         QV(1, 1)
-        QS(1, 1, 0)
-        M1(1, 1, 3, 'tp')
         MK(1, 1, 1)
-        MK(0, 1, 2)
-        M2(1, 0, 0)
-        CO(1, 0, 0)
-        M2(1, 0, 1)
-        CO(1, 0, 1)
+        QS(1, 1, 0)
         QS(1, 1, 1)
+        M1(0, 1, 2)
+        M1(1, 1, 2)
+        M2(0, 3, 0)
+        M2(0, 3, 1)
+        M2(1, 0, 0)
+        M2(1, 0, 1)
+        M1(0, 1, 3)
+        M1(1, 1, 3)
+        CO(0, 3, 0, "S")
+        ST(0, 3, 0)
+        CO(0, 3, 1, "S")
+        ST(0, 3, 1)
+        CO(1, 0, 0, "S")
+        ST(1, 0, 0)
+        CO(1, 0, 1, "S")
+        ST(1, 0, 1)
+        MK(0, 1, 2)
         MK(1, 1, 2)
         QS(0, 1, 2)
-        M2(1, 1, 0)
-        CO(1, 1, 0)
-        M2(1, 1, 1)
-        CO(1, 1, 1)
-        MK(0, 1, 3)
         QS(1, 1, 2)
-        M2(1, 2, 0)
-        CO(1, 2, 0)
-        M2(1, 2, 1)
-        CO(1, 2, 1)
+        MK(0, 1, 3)
         MK(1, 1, 3)
         QS(0, 1, 3)
         QS(1, 1, 3)
-        M2(1, 3, 0, (0,))
-        M2(1, 3, 1, (0,))
-        M2(1, 3, 0, (1,))
-        CO(1, 3, 0)
-        M2(1, 3, 1, (1,))
-        CO(1, 3, 1, 'V')
+        M2(1, 1, 0)
+        M2(1, 1, 1)
+        M2(1, 2, 0)
+        M2(1, 2, 1)
+        M2(1, 3, 0)
+        M2(1, 3, 1)
+        CO(1, 1, 0, "S")
+        ST(1, 1, 0)
+        CO(1, 1, 1, "S")
+        ST(1, 1, 1)
+        CO(1, 2, 0, "S")
+        ST(1, 2, 0)
+        CO(1, 3, 0, "S")
+        CO(1, 2, 1, "V")
+        ST(1, 2, 1)
+        ST(1, 3, 0)
+        CO(1, 3, 1, "V")
+        ST(1, 3, 1)

@@ -17,6 +17,7 @@ FLOPS = 2 * 1024 * (512 * 512 + 512 * 1024) * 2
 BIG = 2.0**100
 LOG_SCALE = -5.0 * math.log(2.0)
 BANKS = 8
+SLOT = (0, 2, 1, 3)
 
 
 def tile_simplifiedretnet_pa_kernel(tc, q, k, v_bytes, v_scale, decay, out):
@@ -40,12 +41,12 @@ def tile_simplifiedretnet_pa_kernel(tc, q, k, v_bytes, v_scale, decay, out):
         halves = [(g, h) for g in range(2) for h in range(2)]
         pairs = [(0, 0), (0, 1), (1, 1)]
         tiles = [(g, c, b) for g, c in pairs for b in range(4)]
-        raw = {(x, c): sb("raw_%s_%s" % (x, c), [128, 4, 1024], BF16) for x in "qk" for c in range(2)}
+        raw = {}
         grouped = {key: sb("grp_%s_%s_%s" % key, [128, 2, 128, 2], F32) for key in blocks}
         codes = {key: sb("cod_%s_%s_%s" % key, [128, 256], U32) for key in blocks}
         scales = {key: sb("scl_%s_%s_%s" % key, [128, 256], U8) for key in blocks}
-        vb = [sb("vb%s" % (g,), [128, 4, 1024], U8) for g in range(2)]
-        wide = [sb("wide%s" % (g,), [128, 4, 1024], BF16) for g in range(2)]
+        vb = {}
+        wide = [sb("wide%s" % (g,), [128, 2, 1024, 2], BF16) for g in range(2)]
         vi = {key: sb("vi%s_%s" % key, [128, 512, 4], BF16) for key in halves}
         v_codes = {key: sb("vc%s_%s" % key, [128, 512], U32) for key in halves}
         v_scl = {key: sb("vx%s_%s" % key, [128, 512], U8) for key in halves}
@@ -67,10 +68,16 @@ def tile_simplifiedretnet_pa_kernel(tc, q, k, v_bytes, v_scale, decay, out):
         psum = {}
 
         def load(x, c, lo, hi):
-            nc.sync.dma_start(out=raw[x, c][:, lo:hi, :], in_=x_rows[x][c][:, lo:hi, :])
+            rows = sb("raw_%s_%s_%s" % (x, c, lo), [128, hi - lo, 1024], BF16)
+            nc.sync.dma_start(out=rows[:], in_=x_rows[x][c][:, lo:hi, :])
+            for b in range(lo, hi):
+                raw[x, c, b] = rows[:, b - lo, :]
 
         def loadv(g, t0, t1, n0, n1):
-            nc.sync.dma_start(out=vb[g][:, t0:t1, n0:n1], in_=v_rows[g][:, t0:t1, n0:n1])
+            rows = sb("vb_%s_%s" % (g, t0), [128, t1 - t0, 1024], U8)
+            nc.sync.dma_start(out=rows[:], in_=v_rows[g][:, t0:t1, :])
+            for t in range(t0, t1):
+                vb[g, t] = rows[:, t - t0, :]
 
         def new_bank(key):
             psum[key] = banks.tile([128, 512], F32, name="bank")
@@ -78,7 +85,7 @@ def tile_simplifiedretnet_pa_kernel(tc, q, k, v_bytes, v_scale, decay, out):
 
         def TR(x, c, b):
             bank = new_bank(("TR", x, c, b))[:].rearrange("p (g u r) -> p g u r", g=2, u=2)
-            words = raw[x, c][:, b, :].bitcast(F32)
+            words = raw[x, c, b].bitcast(F32)
             for g in range(2):
                 for u in range(2):
                     nc.tensor.transpose(bank[:, g, u, :], words[:, 256 * g + u : 256 * (g + 1) : 2], ident[:])
@@ -99,17 +106,22 @@ def tile_simplifiedretnet_pa_kernel(tc, q, k, v_bytes, v_scale, decay, out):
 
         def WD(g, t, h, eng):
             cols = slice(0, 1024) if h == 2 else slice(512 * h, 512 * (h + 1))
-            src = vb[g][:, t, cols].bitcast(E4M3FN)
-            if eng == "V":
-                nc.vector.tensor_scalar(out=wide[g][:, t, cols], in0=src, scalar1=vs[:, g, t : t + 1], scalar2=None, op0=ALU.mult)
-            else:
-                nc.scalar.activation(out=wide[g][:, t, cols], in_=src, func=ACT.Copy, scale=vs[:, g, t : t + 1])
-
-        def IL(g, h):
-            nc.vector.tensor_copy(
-                out=vi[g, h][:].rearrange("p (m i) t -> p m t i", i=4),
-                in_=wide[g][:, :, 512 * h : 512 * (h + 1)].rearrange("p t (m i) -> p m t i", i=4),
+            nc.vector.tensor_scalar(
+                out=wide[g][:, t % 2, cols, t // 2],
+                in0=vb[g, t][:, cols].bitcast(E4M3FN),
+                scalar1=vs[:, g, t : t + 1],
+                scalar2=None,
+                op0=ALU.mult,
             )
+
+        def IL(g, h, eng):
+            words = wide[g][:].rearrange("p j n e -> p j (n e)").bitcast(F32)
+            src = words[:, :, 512 * h : 512 * (h + 1)].rearrange("p j n -> p n j")
+            dst = vi[g, h][:].bitcast(F32)
+            if eng == "S":
+                nc.scalar.copy(dst, src)
+            else:
+                nc.vector.tensor_copy(out=dst, in_=src)
 
         def QV(g, h):
             nc.vector.quantize_mx(
@@ -120,7 +132,7 @@ def tile_simplifiedretnet_pa_kernel(tc, q, k, v_bytes, v_scale, decay, out):
             table = dist if e == 1 else near
             col = 4 * (e // 2) + t
             nc.scalar.activation(
-                out=gain[e][:, :, 4 * t : 4 * (t + 1)],
+                out=gain[e][:, :, 4 * SLOT[t] : 4 * (SLOT[t] + 1)],
                 in_=table[:, 3 - t : 515 - t].rearrange("p (m i) -> p m i", i=4),
                 func=ACT.Exp,
                 bias=far_bias[:, t : t + 1] if e == 1 else LOG_SCALE,
@@ -133,7 +145,7 @@ def tile_simplifiedretnet_pa_kernel(tc, q, k, v_bytes, v_scale, decay, out):
                 for f in range(2):
                     cols = slice(128 * f, 128 * (f + 1))
                     nc.tensor.matmul_mx(
-                        out=bank[:, 128 * t : 128 * (t + 1)],
+                        out=bank[:, 128 * SLOT[t] : 128 * (SLOT[t] + 1)],
                         lhsT=codes["k", g, t][:, cols].bitcast(FP8X4),
                         lhsT_scale=scales["k", g, t][:, cols],
                         rhs=codes["q", c, b][:, cols].bitcast(FP8X4),
@@ -183,14 +195,14 @@ def tile_simplifiedretnet_pa_kernel(tc, q, k, v_bytes, v_scale, decay, out):
 
         nc.scalar.dma_start(out=dk[:], in_=decay.rearrange("(g p t) -> p g t", g=2, t=4))
         nc.scalar.dma_start(out=vs[:], in_=v_scale.rearrange("o (g p t) i -> p (o g) (t i)", g=2, t=4))
-        loadv(0, 0, 4, 0, 512)
+        loadv(0, 0, 2, 0, 1024)
         load("k", 0, 0, 1)
+        loadv(0, 2, 4, 0, 1024)
         load("k", 0, 1, 2)
         load("k", 0, 2, 3)
         load("k", 0, 3, 4)
         load("q", 0, 0, 1)
         load("q", 0, 1, 2)
-        loadv(0, 0, 4, 512, 1024)
         load("q", 0, 2, 3)
         load("q", 0, 3, 4)
         load("q", 1, 0, 2)
@@ -218,37 +230,36 @@ def tile_simplifiedretnet_pa_kernel(tc, q, k, v_bytes, v_scale, decay, out):
         EX(0, 1)
         EX(0, 2)
         CP("k", 0, 0, "S")
+        EX(0, 3)
         CP("k", 0, 1, "S")
         CP("k", 0, 2, "S")
         CP("k", 0, 3, "S")
         CP("q", 0, 0, "S")
         CP("q", 0, 1, "S")
-        EX(0, 3)
         CP("q", 0, 2, "S")
         CP("q", 0, 3, "S")
         EX(1, 0)
         EX(1, 1)
         EX(1, 2)
         EX(1, 3)
-        WD(0, 0, 0, "V")
-        WD(0, 1, 0, "V")
-        WD(0, 2, 0, "V")
-        WD(0, 3, 0, "V")
-        IL(0, 0)
+        EX(2, 0)
+        WD(0, 0, 2, "V")
+        WD(0, 1, 2, "V")
+        WD(0, 2, 2, "V")
+        WD(0, 3, 2, "V")
         QZ("k", 0, 0)
+        IL(0, 0, "V")
         QZ("k", 0, 1)
-        QV(0, 0)
+        IL(0, 1, "V")
         QZ("k", 0, 2)
         QZ("k", 0, 3)
-        WD(0, 0, 1, "V")
         QZ("q", 0, 0)
-        WD(0, 1, 1, "V")
+        QV(0, 0)
         QZ("q", 0, 1)
-        WD(0, 2, 1, "V")
-        WD(0, 3, 1, "V")
+        QV(0, 1)
         QZ("q", 0, 2)
-        IL(0, 1)
         QZ("q", 0, 3)
+        WD(1, 0, 2, "V")
         M1(0, 0, 0)
         M1(0, 0, 1)
         TR("q", 1, 0)
@@ -259,26 +270,26 @@ def tile_simplifiedretnet_pa_kernel(tc, q, k, v_bytes, v_scale, decay, out):
         TR("k", 1, 1)
         CP("q", 1, 0, "S")
         CP("q", 1, 1, "S")
-        WD(1, 2, 2, "S")
-        WD(1, 3, 2, "S")
+        EX(2, 1)
+        EX(2, 2)
+        EX(2, 3)
         CP("k", 1, 0, "S")
         CP("k", 1, 1, "S")
         MK(0, 0, 0)
-        QV(0, 1)
+        WD(1, 1, 2, "V")
         MK(0, 0, 1)
         QS(0, 0, 0)
         QZ("q", 1, 0)
         QS(0, 0, 1)
         QZ("q", 1, 1)
+        WD(1, 2, 2, "V")
         MK(0, 0, 2)
-        WD(1, 0, 2, "V")
+        WD(1, 3, 2, "V")
         MK(0, 0, 3)
         QS(0, 0, 2)
-        WD(1, 1, 2, "V")
-        QS(0, 0, 3)
         QZ("k", 1, 0)
+        QS(0, 0, 3)
         QZ("k", 1, 1)
-        IL(1, 0)
         M2(0, 0, 0)
         M2(0, 0, 1)
         M1(0, 1, 0)
@@ -293,17 +304,18 @@ def tile_simplifiedretnet_pa_kernel(tc, q, k, v_bytes, v_scale, decay, out):
         ST(0, 0, 1)
         CP("k", 1, 2, "S")
         CP("k", 1, 3, "S")
+        IL(1, 0, "S")
         CO(0, 1, 0, "S")
         ST(0, 1, 0)
         CO(0, 1, 1, "S")
         ST(0, 1, 1)
         MK(0, 1, 0)
         QZ("k", 1, 2)
-        QV(1, 0)
-        QS(0, 1, 0)
         QZ("k", 1, 3)
+        QS(0, 1, 0)
         MK(0, 1, 1)
-        IL(1, 1)
+        QV(1, 0)
+        QS(0, 1, 1)
         TR("q", 1, 2)
         TR("q", 1, 3)
         M1(1, 1, 0)
@@ -312,16 +324,12 @@ def tile_simplifiedretnet_pa_kernel(tc, q, k, v_bytes, v_scale, decay, out):
         M2(0, 2, 1)
         CP("q", 1, 2, "S")
         CP("q", 1, 3, "S")
-        EX(2, 0)
-        EX(2, 1)
-        EX(2, 2)
-        EX(2, 3)
+        IL(1, 1, "S")
         CO(0, 2, 0, "S")
         ST(0, 2, 0)
         CO(0, 2, 1, "S")
         ST(0, 2, 1)
         QZ("q", 1, 2)
-        QS(0, 1, 1)
         QZ("q", 1, 3)
         MK(1, 1, 0)
         QV(1, 1)

@@ -16,7 +16,6 @@ ACT = mybir.ActivationFunctionType
 FLOPS = 2 * 1024 * (512 * 512 + 512 * 1024) * 2
 BIG = 2.0**100
 LOG_SCALE = -5.0 * math.log(2.0)
-BANKS = 8
 SLOT = (0, 2, 1, 3)
 
 
@@ -31,7 +30,8 @@ def tile_simplifiedretnet_pa_kernel(tc, q, k, v_bytes, v_scale, decay, out):
 
     with ExitStack() as ctx:
         keep = ctx.enter_context(tc.tile_pool(name="keep", bufs=1))
-        banks = ctx.enter_context(tc.psum_pool(name="banks", bufs=BANKS))
+        score_banks = ctx.enter_context(tc.psum_pool(name="score_banks", bufs=4))
+        other_banks = ctx.enter_context(tc.psum_pool(name="other_banks", bufs=4))
         ctx.enter_context(tc.manual_schedule())
 
         def sb(name, shape, dtype):
@@ -80,7 +80,7 @@ def tile_simplifiedretnet_pa_kernel(tc, q, k, v_bytes, v_scale, decay, out):
                 vb[g, t] = rows[:, t - t0, :]
 
         def new_bank(key):
-            psum[key] = banks.tile([128, 512], F32, name="bank")
+            psum[key] = (score_banks if key[0] == "M1" else other_banks).tile([128, 512], F32, name="bank")
             return psum[key]
 
         def TR(x, c, b):
@@ -140,19 +140,24 @@ def tile_simplifiedretnet_pa_kernel(tc, q, k, v_bytes, v_scale, decay, out):
             )
 
         def M1(g, c, b):
-            bank = new_bank(("M1", g, c, b))
+            if ("M1", g, c, b) in psum:
+                return
+            pair = (b, b + 1)
+            for a in pair:
+                new_bank(("M1", g, c, a))
             for t in range(4):
                 for f in range(2):
                     cols = slice(128 * f, 128 * (f + 1))
-                    nc.tensor.matmul_mx(
-                        out=bank[:, 128 * SLOT[t] : 128 * (SLOT[t] + 1)],
-                        lhsT=codes["k", g, t][:, cols].bitcast(FP8X4),
-                        lhsT_scale=scales["k", g, t][:, cols],
-                        rhs=codes["q", c, b][:, cols].bitcast(FP8X4),
-                        rhs_scale=scales["q", c, b][:, cols],
-                        start=(f == 0),
-                        stop=(f == 1),
-                    )
+                    for a in pair:
+                        nc.tensor.matmul_mx(
+                            out=psum["M1", g, c, a][:, 128 * SLOT[t] : 128 * (SLOT[t] + 1)],
+                            lhsT=codes["k", g, t][:, cols].bitcast(FP8X4),
+                            lhsT_scale=scales["k", g, t][:, cols],
+                            rhs=codes["q", c, a][:, cols].bitcast(FP8X4),
+                            rhs_scale=scales["q", c, a][:, cols],
+                            start=(f == 0),
+                            stop=(f == 1),
+                        )
 
         def MK(g, c, b):
             nc.vector.tensor_tensor(
@@ -222,10 +227,6 @@ def tile_simplifiedretnet_pa_kernel(tc, q, k, v_bytes, v_scale, decay, out):
         TR("k", 0, 1)
         TR("k", 0, 2)
         TR("k", 0, 3)
-        TR("q", 0, 0)
-        TR("q", 0, 1)
-        TR("q", 0, 2)
-        TR("q", 0, 3)
         EX(0, 0)
         EX(0, 1)
         EX(0, 2)
@@ -234,15 +235,6 @@ def tile_simplifiedretnet_pa_kernel(tc, q, k, v_bytes, v_scale, decay, out):
         CP("k", 0, 1, "S")
         CP("k", 0, 2, "S")
         CP("k", 0, 3, "S")
-        CP("q", 0, 0, "S")
-        CP("q", 0, 1, "S")
-        CP("q", 0, 2, "S")
-        CP("q", 0, 3, "S")
-        EX(1, 0)
-        EX(1, 1)
-        EX(1, 2)
-        EX(1, 3)
-        EX(2, 0)
         WD(0, 0, 2, "V")
         WD(0, 1, 2, "V")
         WD(0, 2, 2, "V")
@@ -253,12 +245,25 @@ def tile_simplifiedretnet_pa_kernel(tc, q, k, v_bytes, v_scale, decay, out):
         IL(0, 1, "V")
         QZ("k", 0, 2)
         QZ("k", 0, 3)
+        TR("q", 0, 0)
+        TR("q", 0, 1)
+        TR("q", 0, 2)
+        TR("q", 0, 3)
+        CP("q", 0, 0, "S")
+        CP("q", 0, 1, "S")
+        CP("q", 0, 2, "S")
+        CP("q", 0, 3, "S")
+        EX(1, 0)
+        EX(1, 1)
+        EX(1, 2)
+        EX(1, 3)
+        EX(2, 0)
         QZ("q", 0, 0)
-        QV(0, 0)
         QZ("q", 0, 1)
-        QV(0, 1)
+        QV(0, 0)
         QZ("q", 0, 2)
         QZ("q", 0, 3)
+        QV(0, 1)
         WD(1, 0, 2, "V")
         M1(0, 0, 0)
         M1(0, 0, 1)
@@ -272,7 +277,6 @@ def tile_simplifiedretnet_pa_kernel(tc, q, k, v_bytes, v_scale, decay, out):
         CP("q", 1, 1, "S")
         EX(2, 1)
         EX(2, 2)
-        EX(2, 3)
         CP("k", 1, 0, "S")
         CP("k", 1, 1, "S")
         MK(0, 0, 0)
@@ -282,21 +286,19 @@ def tile_simplifiedretnet_pa_kernel(tc, q, k, v_bytes, v_scale, decay, out):
         QZ("q", 1, 0)
         QS(0, 0, 1)
         QZ("q", 1, 1)
-        WD(1, 2, 2, "V")
         MK(0, 0, 2)
-        WD(1, 3, 2, "V")
+        WD(1, 2, 2, "V")
         MK(0, 0, 3)
+        WD(1, 3, 2, "V")
         QS(0, 0, 2)
         QZ("k", 1, 0)
         QS(0, 0, 3)
         QZ("k", 1, 1)
         M2(0, 0, 0)
         M2(0, 0, 1)
-        M1(0, 1, 0)
         TR("k", 1, 2)
         TR("k", 1, 3)
-        M2(0, 1, 0)
-        M2(0, 1, 1)
+        M1(0, 1, 0)
         M1(0, 1, 1)
         CO(0, 0, 0, "S")
         ST(0, 0, 0)
@@ -305,71 +307,74 @@ def tile_simplifiedretnet_pa_kernel(tc, q, k, v_bytes, v_scale, decay, out):
         CP("k", 1, 2, "S")
         CP("k", 1, 3, "S")
         IL(1, 0, "S")
-        CO(0, 1, 0, "S")
-        ST(0, 1, 0)
-        CO(0, 1, 1, "S")
-        ST(0, 1, 1)
-        MK(0, 1, 0)
         QZ("k", 1, 2)
         QZ("k", 1, 3)
-        QS(0, 1, 0)
+        MK(0, 1, 0)
         MK(0, 1, 1)
+        QS(0, 1, 0)
         QV(1, 0)
         QS(0, 1, 1)
         TR("q", 1, 2)
         TR("q", 1, 3)
+        M2(0, 1, 0)
+        M2(0, 1, 1)
         M1(1, 1, 0)
         M1(1, 1, 1)
-        M2(0, 2, 0)
-        M2(0, 2, 1)
         CP("q", 1, 2, "S")
         CP("q", 1, 3, "S")
+        EX(2, 3)
         IL(1, 1, "S")
+        CO(0, 1, 0, "S")
+        ST(0, 1, 0)
+        CO(0, 1, 1, "S")
+        ST(0, 1, 1)
+        QZ("q", 1, 2)
+        QZ("q", 1, 3)
+        MK(1, 1, 0)
+        MK(1, 1, 1)
+        QS(1, 1, 0)
+        QV(1, 1)
+        QS(1, 1, 1)
+        M2(0, 2, 0)
+        M2(0, 2, 1)
+        M1(0, 1, 2)
+        M1(0, 1, 3)
+        M2(0, 3, 0)
+        M2(0, 3, 1)
+        M1(1, 1, 2)
+        M1(1, 1, 3)
         CO(0, 2, 0, "S")
         ST(0, 2, 0)
         CO(0, 2, 1, "S")
         ST(0, 2, 1)
-        QZ("q", 1, 2)
-        QZ("q", 1, 3)
-        MK(1, 1, 0)
-        QV(1, 1)
-        MK(1, 1, 1)
-        QS(1, 1, 0)
-        QS(1, 1, 1)
-        M1(0, 1, 2)
-        M1(1, 1, 2)
-        M2(0, 3, 0)
-        M2(0, 3, 1)
-        M2(1, 0, 0)
-        M2(1, 0, 1)
-        M1(0, 1, 3)
-        M1(1, 1, 3)
         CO(0, 3, 0, "S")
         ST(0, 3, 0)
         CO(0, 3, 1, "S")
         ST(0, 3, 1)
+        MK(0, 1, 2)
+        MK(0, 1, 3)
+        QS(0, 1, 2)
+        MK(1, 1, 2)
+        QS(0, 1, 3)
+        MK(1, 1, 3)
+        QS(1, 1, 2)
+        QS(1, 1, 3)
+        M2(1, 0, 0)
+        M2(1, 0, 1)
+        M2(1, 1, 0)
+        M2(1, 1, 1)
         CO(1, 0, 0, "S")
         ST(1, 0, 0)
         CO(1, 0, 1, "S")
         ST(1, 0, 1)
-        MK(0, 1, 2)
-        MK(1, 1, 2)
-        QS(0, 1, 2)
-        QS(1, 1, 2)
-        MK(0, 1, 3)
-        MK(1, 1, 3)
-        QS(0, 1, 3)
-        QS(1, 1, 3)
-        M2(1, 1, 0)
-        M2(1, 1, 1)
-        M2(1, 2, 0)
-        M2(1, 2, 1)
-        M2(1, 3, 0)
-        M2(1, 3, 1)
         CO(1, 1, 0, "S")
         ST(1, 1, 0)
         CO(1, 1, 1, "S")
         ST(1, 1, 1)
+        M2(1, 2, 0)
+        M2(1, 2, 1)
+        M2(1, 3, 0)
+        M2(1, 3, 1)
         CO(1, 2, 0, "S")
         ST(1, 2, 0)
         CO(1, 3, 0, "S")

@@ -2,7 +2,6 @@ import math
 from contextlib import ExitStack
 
 import concourse.mybir as mybir
-from concourse.masks import make_identity
 
 F32 = mybir.dt.float32
 BF16 = mybir.dt.bfloat16
@@ -16,7 +15,7 @@ ACT = mybir.ActivationFunctionType
 FLOPS = 2 * 1024 * (512 * 512 + 512 * 1024) * 2
 BIG = 2.0**100
 LOG_SCALE = -5.0 * math.log(2.0)
-SLOT = (0, 2, 1, 3)
+SLOT = (0, 1, 2, 3)
 
 
 def tile_simplifiedretnet_pa_kernel(tc, q, k, v_bytes, v_scale, decay, out):
@@ -42,18 +41,20 @@ def tile_simplifiedretnet_pa_kernel(tc, q, k, v_bytes, v_scale, decay, out):
         pairs = [(0, 0), (0, 1), (1, 1)]
         tiles = [(g, c, b) for g, c in pairs for b in range(4)]
         raw = {}
-        grouped = {key: sb("grp_%s_%s_%s" % key, [128, 2, 128, 2], F32) for key in blocks}
-        codes = {key: sb("cod_%s_%s_%s" % key, [128, 256], U32) for key in blocks}
-        scales = {key: sb("scl_%s_%s_%s" % key, [128, 256], U8) for key in blocks}
+        twos = [(x, c, a) for x in "qk" for c in range(2) for a in range(2)]
+        grouped = {key: sb("grp_%s_%s_%s" % key, [128, 2, 2, 128, 2], F32) for key in twos}
+        codes = {key: sb("cod_%s_%s_%s" % key, [128, 512], U32) for key in twos}
+        scales = {key: sb("scl_%s_%s_%s" % key, [128, 512], U8) for key in twos}
         vb = {}
-        wide = [sb("wide%s" % (g,), [128, 2, 1024, 2], BF16) for g in range(2)]
+        wide = [sb("wide%s" % (g,), [128, 4, 1024], BF16) for g in range(2)]
         vi = {key: sb("vi%s_%s" % key, [128, 512, 4], BF16) for key in halves}
         v_codes = {key: sb("vc%s_%s" % key, [128, 512], U32) for key in halves}
         v_scl = {key: sb("vx%s_%s" % key, [128, 512], U8) for key in halves}
         gain = [sb("gain%s" % (e,), [128, 128, 16], F32) for e in range(3)]
-        s_bf = {key: sb("s%s_%s_%s" % key, [128, 128, 4], BF16) for key in tiles}
-        s_codes = {key: sb("sc%s_%s_%s" % key, [128, 128], U32) for key in tiles}
-        s_scl = {key: sb("sx%s_%s_%s" % key, [128, 128], U8) for key in tiles}
+        s_twos = [(g, c, a) for g, c in pairs for a in range(2)]
+        s_bf = {key: sb("s%s_%s_%s" % key, [128, 2, 128, 4], BF16) for key in s_twos}
+        s_codes = {key: sb("sc%s_%s_%s" % key, [128, 256], U32) for key in s_twos}
+        s_scl = {key: sb("sx%s_%s_%s" % key, [128, 256], U8) for key in s_twos}
         result = {(c, b, h): sb("o%s_%s_%s" % (c, b, h), [128, 512], F32) for c in range(2) for b in range(4) for h in range(2)}
         ident = sb("ident", [128, 128], F32)
         dist = sb("dist", [128, 516], F32)
@@ -93,35 +94,35 @@ def tile_simplifiedretnet_pa_kernel(tc, q, k, v_bytes, v_scale, decay, out):
         def CP(x, c, b, eng):
             src = psum["TR", x, c, b][:].rearrange("p (g u r) -> p g r u", g=2, u=2)
             if eng == "S":
-                nc.scalar.copy(grouped[x, c, b][:], src)
+                nc.scalar.copy(grouped[x, c, b // 2][:, :, b % 2], src)
             else:
-                nc.vector.tensor_copy(out=grouped[x, c, b][:], in_=src)
+                nc.vector.tensor_copy(out=grouped[x, c, b // 2][:, :, b % 2], in_=src)
 
         def QZ(x, c, b):
             nc.vector.quantize_mx(
-                out=codes[x, c, b][:].bitcast(FP8X4),
-                scales=scales[x, c, b][:],
-                in_=grouped[x, c, b][:].rearrange("p g r u -> p (g r u)").bitcast(BF16),
+                out=codes[x, c, b // 2][:].bitcast(FP8X4),
+                scales=scales[x, c, b // 2][:],
+                in_=grouped[x, c, b // 2][:].rearrange("p f j r u -> p (f j r u)").bitcast(BF16),
             )
 
         def WD(g, t, h, eng):
             cols = slice(0, 1024) if h == 2 else slice(512 * h, 512 * (h + 1))
-            nc.vector.tensor_scalar(
-                out=wide[g][:, t % 2, cols, t // 2],
-                in0=vb[g, t][:, cols].bitcast(E4M3FN),
-                scalar1=vs[:, g, t : t + 1],
-                scalar2=None,
-                op0=ALU.mult,
-            )
+            src = vb[g, t][:, cols].bitcast(E4M3FN)
+            if eng == "V":
+                nc.vector.tensor_scalar(out=wide[g][:, t, cols], in0=src, scalar1=vs[:, g, t : t + 1], scalar2=None, op0=ALU.mult)
+            else:
+                nc.scalar.activation(out=wide[g][:, t, cols], in_=src, func=ACT.Copy, scale=vs[:, g, t : t + 1])
 
         def IL(g, h, eng):
-            words = wide[g][:].rearrange("p j n e -> p j (n e)").bitcast(F32)
-            src = words[:, :, 512 * h : 512 * (h + 1)].rearrange("p j n -> p n j")
-            dst = vi[g, h][:].bitcast(F32)
-            if eng == "S":
-                nc.scalar.copy(dst, src)
+            src = wide[g][:, :, 512 * h : 512 * (h + 1)]
+            if eng == "V":
+                nc.vector.tensor_copy(
+                    out=vi[g, h][:].rearrange("p (m i) t -> p m t i", i=4), in_=src.rearrange("p t (m i) -> p m t i", i=4)
+                )
             else:
-                nc.vector.tensor_copy(out=dst, in_=src)
+                nc.gpsimd.tensor_scalar(
+                    out=vi[g, h][:], in0=src.rearrange("p t n -> p n t"), scalar1=1.0, scalar2=0.0, op0=ALU.mult, op1=ALU.add
+                )
 
         def QV(g, h):
             nc.vector.quantize_mx(
@@ -140,38 +141,38 @@ def tile_simplifiedretnet_pa_kernel(tc, q, k, v_bytes, v_scale, decay, out):
             )
 
         def M1(g, c, b):
-            if ("M1", g, c, b) in psum:
-                return
             pair = (b, b + 1)
             for a in pair:
                 new_bank(("M1", g, c, a))
             for t in range(4):
                 for f in range(2):
-                    cols = slice(128 * f, 128 * (f + 1))
+                    keys = slice(256 * f + 128 * (t % 2), 256 * f + 128 * (t % 2 + 1))
                     for a in pair:
+                        cols = slice(256 * f + 128 * (a % 2), 256 * f + 128 * (a % 2 + 1))
                         nc.tensor.matmul_mx(
                             out=psum["M1", g, c, a][:, 128 * SLOT[t] : 128 * (SLOT[t] + 1)],
-                            lhsT=codes["k", g, t][:, cols].bitcast(FP8X4),
-                            lhsT_scale=scales["k", g, t][:, cols],
-                            rhs=codes["q", c, a][:, cols].bitcast(FP8X4),
-                            rhs_scale=scales["q", c, a][:, cols],
+                            lhsT=codes["k", g, t // 2][:, keys].bitcast(FP8X4),
+                            lhsT_scale=scales["k", g, t // 2][:, keys],
+                            rhs=codes["q", c, a // 2][:, cols].bitcast(FP8X4),
+                            rhs_scale=scales["q", c, a // 2][:, cols],
                             start=(f == 0),
                             stop=(f == 1),
                         )
 
         def MK(g, c, b):
             nc.vector.tensor_tensor(
-                out=s_bf[g, c, b][:].rearrange("p (m i) t -> p m t i", i=4),
+                out=s_bf[g, c, b // 2][:, b % 2].rearrange("p (m i) t -> p m t i", i=4),
                 in0=psum["M1", g, c, b][:].rearrange("p (t m i) -> p m t i", t=4, i=4),
                 in1=gain[g + c][:, 32 * b : 32 * (b + 1), :].rearrange("p m (t i) -> p m t i", i=4),
                 op=ALU.mult,
             )
 
-        def QS(g, c, b):
+        def QS(g, c, b, n=2):
+            lo = b % 2 + 1 - n
             nc.vector.quantize_mx(
-                out=s_codes[g, c, b][:].bitcast(FP8X4),
-                scales=s_scl[g, c, b][:],
-                in_=s_bf[g, c, b][:].rearrange("p i t -> p (i t)"),
+                out=s_codes[g, c, b // 2][:, 128 * lo : 128 * (lo + n)].bitcast(FP8X4),
+                scales=s_scl[g, c, b // 2][:, 128 * lo : 128 * (lo + n)],
+                in_=s_bf[g, c, b // 2][:, lo : lo + n].rearrange("p j i t -> p (j i t)"),
             )
 
         def M2(c, b, h):
@@ -179,8 +180,8 @@ def tile_simplifiedretnet_pa_kernel(tc, q, k, v_bytes, v_scale, decay, out):
             for g in range(c + 1):
                 nc.tensor.matmul_mx(
                     out=bank[:],
-                    lhsT=s_codes[g, c, b][:].bitcast(FP8X4),
-                    lhsT_scale=s_scl[g, c, b][:],
+                    lhsT=s_codes[g, c, b // 2][:, 128 * (b % 2) : 128 * (b % 2 + 1)].bitcast(FP8X4),
+                    lhsT_scale=s_scl[g, c, b // 2][:, 128 * (b % 2) : 128 * (b % 2 + 1)],
                     rhs=v_codes[g, h][:].bitcast(FP8X4),
                     rhs_scale=v_scl[g, h][:],
                     start=(g == 0),
@@ -218,7 +219,7 @@ def tile_simplifiedretnet_pa_kernel(tc, q, k, v_bytes, v_scale, decay, out):
         nc.vector.memset(warm[:], 0.0)
         nc.scalar.activation(out=warm_out[:], in_=warm[:], func=ACT.Exp)
         nc.gpsimd.iota(dist[:], pattern=[[1, 516]], base=-3, channel_multiplier=-4, allow_small_or_imprecise_dtypes=True)
-        make_identity(nc, ident[:])
+        nc.vector.tensor_scalar(out=ident[:], in0=dist[:, 3:515:4], scalar1=0.0, scalar2=None, op0=ALU.is_equal)
         nc.vector.scalar_tensor_tensor(out=near[:], in0=dist[:], scalar=-BIG, in1=dist[:], op0=ALU.mult, op1=ALU.max)
         nc.vector.tensor_scalar(out=nd[:], in0=dk[:].rearrange("p g t -> p (g t)"), scalar1=1.0 / 2.0**90, scalar2=-1.0, op0=ALU.max, op1=ALU.mult)
         nc.vector.tensor_scalar(out=far_bias[:], in0=nd[:, 0:4], scalar1=512.0, scalar2=LOG_SCALE, op0=ALU.mult, op1=ALU.add)
@@ -239,11 +240,9 @@ def tile_simplifiedretnet_pa_kernel(tc, q, k, v_bytes, v_scale, decay, out):
         WD(0, 1, 2, "V")
         WD(0, 2, 2, "V")
         WD(0, 3, 2, "V")
-        QZ("k", 0, 0)
         IL(0, 0, "V")
         QZ("k", 0, 1)
-        IL(0, 1, "V")
-        QZ("k", 0, 2)
+        QV(0, 0)
         QZ("k", 0, 3)
         TR("q", 0, 0)
         TR("q", 0, 1)
@@ -255,94 +254,77 @@ def tile_simplifiedretnet_pa_kernel(tc, q, k, v_bytes, v_scale, decay, out):
         CP("q", 0, 3, "S")
         EX(1, 0)
         EX(1, 1)
+        WD(1, 2, 2, "S")
         EX(1, 2)
-        EX(1, 3)
-        EX(2, 0)
-        QZ("q", 0, 0)
         QZ("q", 0, 1)
-        QV(0, 0)
-        QZ("q", 0, 2)
+        IL(0, 1, "V")
         QZ("q", 0, 3)
         QV(0, 1)
         WD(1, 0, 2, "V")
         M1(0, 0, 0)
-        M1(0, 0, 1)
         TR("q", 1, 0)
         TR("q", 1, 1)
         M1(0, 0, 2)
-        M1(0, 0, 3)
         TR("k", 1, 0)
         TR("k", 1, 1)
         CP("q", 1, 0, "S")
         CP("q", 1, 1, "S")
-        EX(2, 1)
-        EX(2, 2)
+        WD(1, 3, 2, "S")
         CP("k", 1, 0, "S")
         CP("k", 1, 1, "S")
+        EX(1, 3)
         MK(0, 0, 0)
-        WD(1, 1, 2, "V")
         MK(0, 0, 1)
-        QS(0, 0, 0)
-        QZ("q", 1, 0)
+        WD(1, 1, 2, "V")
         QS(0, 0, 1)
         QZ("q", 1, 1)
         MK(0, 0, 2)
-        WD(1, 2, 2, "V")
         MK(0, 0, 3)
-        WD(1, 3, 2, "V")
-        QS(0, 0, 2)
-        QZ("k", 1, 0)
-        QS(0, 0, 3)
         QZ("k", 1, 1)
-        M2(0, 0, 0)
-        M2(0, 0, 1)
+        QS(0, 0, 3)
+        IL(1, 0, "V")
         TR("k", 1, 2)
         TR("k", 1, 3)
+        M2(0, 0, 0)
+        M2(0, 0, 1)
         M1(0, 1, 0)
-        M1(0, 1, 1)
+        CP("k", 1, 2, "S")
+        CP("k", 1, 3, "S")
+        EX(2, 0)
+        EX(2, 1)
         CO(0, 0, 0, "S")
         ST(0, 0, 0)
         CO(0, 0, 1, "S")
         ST(0, 0, 1)
-        CP("k", 1, 2, "S")
-        CP("k", 1, 3, "S")
-        IL(1, 0, "S")
-        QZ("k", 1, 2)
         QZ("k", 1, 3)
         MK(0, 1, 0)
         MK(0, 1, 1)
-        QS(0, 1, 0)
         QV(1, 0)
         QS(0, 1, 1)
         TR("q", 1, 2)
         TR("q", 1, 3)
+        M1(1, 1, 0)
         M2(0, 1, 0)
         M2(0, 1, 1)
-        M1(1, 1, 0)
-        M1(1, 1, 1)
         CP("q", 1, 2, "S")
         CP("q", 1, 3, "S")
+        EX(2, 2)
         EX(2, 3)
-        IL(1, 1, "S")
         CO(0, 1, 0, "S")
         ST(0, 1, 0)
         CO(0, 1, 1, "S")
         ST(0, 1, 1)
-        QZ("q", 1, 2)
         QZ("q", 1, 3)
         MK(1, 1, 0)
         MK(1, 1, 1)
-        QS(1, 1, 0)
-        QV(1, 1)
+        IL(1, 1, "V")
         QS(1, 1, 1)
         M2(0, 2, 0)
         M2(0, 2, 1)
         M1(0, 1, 2)
-        M1(0, 1, 3)
         M2(0, 3, 0)
         M2(0, 3, 1)
         M1(1, 1, 2)
-        M1(1, 1, 3)
         CO(0, 2, 0, "S")
         ST(0, 2, 0)
         CO(0, 2, 1, "S")
@@ -352,23 +334,24 @@ def tile_simplifiedretnet_pa_kernel(tc, q, k, v_bytes, v_scale, decay, out):
         CO(0, 3, 1, "S")
         ST(0, 3, 1)
         MK(0, 1, 2)
-        MK(0, 1, 3)
-        QS(0, 1, 2)
+        QV(1, 1)
         MK(1, 1, 2)
-        QS(0, 1, 3)
+        QS(0, 1, 2, 1)
+        MK(0, 1, 3)
+        QS(1, 1, 2, 1)
         MK(1, 1, 3)
-        QS(1, 1, 2)
-        QS(1, 1, 3)
+        QS(0, 1, 3, 1)
+        QS(1, 1, 3, 1)
         M2(1, 0, 0)
-        M2(1, 0, 1)
         M2(1, 1, 0)
+        M2(1, 0, 1)
         M2(1, 1, 1)
         CO(1, 0, 0, "S")
         ST(1, 0, 0)
-        CO(1, 0, 1, "S")
-        ST(1, 0, 1)
         CO(1, 1, 0, "S")
         ST(1, 1, 0)
+        CO(1, 0, 1, "S")
+        ST(1, 0, 1)
         CO(1, 1, 1, "S")
         ST(1, 1, 1)
         M2(1, 2, 0)
@@ -377,9 +360,9 @@ def tile_simplifiedretnet_pa_kernel(tc, q, k, v_bytes, v_scale, decay, out):
         M2(1, 3, 1)
         CO(1, 2, 0, "S")
         ST(1, 2, 0)
-        CO(1, 3, 0, "S")
-        CO(1, 2, 1, "V")
+        CO(1, 2, 1, "S")
         ST(1, 2, 1)
+        CO(1, 3, 0, "S")
         ST(1, 3, 0)
         CO(1, 3, 1, "V")
         ST(1, 3, 1)

@@ -15,7 +15,6 @@ ACT = mybir.ActivationFunctionType
 FLOPS = 2 * 1024 * (512 * 512 + 512 * 1024) * 2
 BIG = 2.0**100
 LOG_SCALE = -5.0 * math.log(2.0)
-SLOT = (0, 1, 2, 3)
 
 
 def tile_simplifiedretnet_pa_kernel(tc, q, k, v_bytes, v_scale, decay, out):
@@ -50,9 +49,10 @@ def tile_simplifiedretnet_pa_kernel(tc, q, k, v_bytes, v_scale, decay, out):
         vi = {key: sb("vi%s_%s" % key, [128, 512, 4], BF16) for key in halves}
         v_codes = {key: sb("vc%s_%s" % key, [128, 512], U32) for key in halves}
         v_scl = {key: sb("vx%s_%s" % key, [128, 512], U8) for key in halves}
-        gain = [sb("gain%s" % (e,), [128, 128, 16], F32) for e in range(3)]
+        gain = [sb("gain%s" % (e,), [128, 2, 128, 8], F32) for e in range(3)]
         s_twos = [(g, c, a) for g, c in pairs for a in range(2)]
         s_bf = {key: sb("s%s_%s_%s" % key, [128, 2, 128, 4], BF16) for key in s_twos}
+        s_two = {key: sb("sp%s_%s_%s" % key, [128, 2, 256, 2], BF16) for key in s_twos}
         s_codes = {key: sb("sc%s_%s_%s" % key, [128, 256], U32) for key in s_twos}
         s_scl = {key: sb("sx%s_%s_%s" % key, [128, 256], U8) for key in s_twos}
         result = {(c, b, h): sb("o%s_%s_%s" % (c, b, h), [128, 512], F32) for c in range(2) for b in range(4) for h in range(2)}
@@ -80,8 +80,8 @@ def tile_simplifiedretnet_pa_kernel(tc, q, k, v_bytes, v_scale, decay, out):
             for t in range(t0, t1):
                 vb[g, t] = rows[:, t - t0, :]
 
-        def new_bank(key):
-            psum[key] = (score_banks if key[0] == "M1" else other_banks).tile([128, 512], F32, name="bank")
+        def new_bank(key, score=False):
+            psum[key] = (score_banks if score else other_banks).tile([128, 512], F32, name="bank")
             return psum[key]
 
         def TR(x, c, b):
@@ -133,7 +133,7 @@ def tile_simplifiedretnet_pa_kernel(tc, q, k, v_bytes, v_scale, decay, out):
             table = dist if e == 1 else near
             col = 4 * (e // 2) + t
             nc.scalar.activation(
-                out=gain[e][:, :, 4 * SLOT[t] : 4 * (SLOT[t] + 1)],
+                out=gain[e][:, t // 2, :, 4 * (t % 2) : 4 * (t % 2 + 1)],
                 in_=table[:, 3 - t : 515 - t].rearrange("p (m i) -> p m i", i=4),
                 func=ACT.Exp,
                 bias=far_bias[:, t : t + 1] if e == 1 else LOG_SCALE,
@@ -141,31 +141,38 @@ def tile_simplifiedretnet_pa_kernel(tc, q, k, v_bytes, v_scale, decay, out):
             )
 
         def M1(g, c, b):
-            pair = (b, b + 1)
-            for a in pair:
-                new_bank(("M1", g, c, a))
-            for t in range(4):
+            a, j = divmod(b, 2)
+            bank = new_bank(("M1", g, c, b), True)
+            for e in range(2):
                 for f in range(2):
-                    keys = slice(256 * f + 128 * (t % 2), 256 * f + 128 * (t % 2 + 1))
-                    for a in pair:
-                        cols = slice(256 * f + 128 * (a % 2), 256 * f + 128 * (a % 2 + 1))
-                        nc.tensor.matmul_mx(
-                            out=psum["M1", g, c, a][:, 128 * SLOT[t] : 128 * (SLOT[t] + 1)],
-                            lhsT=codes["k", g, t // 2][:, keys].bitcast(FP8X4),
-                            lhsT_scale=scales["k", g, t // 2][:, keys],
-                            rhs=codes["q", c, a // 2][:, cols].bitcast(FP8X4),
-                            rhs_scale=scales["q", c, a // 2][:, cols],
-                            start=(f == 0),
-                            stop=(f == 1),
-                        )
+                    keys = slice(256 * f + 128 * e, 256 * f + 128 * (e + 1))
+                    cols = slice(256 * f, 256 * (f + 1))
+                    nc.tensor.matmul_mx(
+                        out=bank[:, 256 * e : 256 * (e + 1)],
+                        lhsT=codes["k", g, j][:, keys].bitcast(FP8X4),
+                        lhsT_scale=scales["k", g, j][:, keys],
+                        rhs=codes["q", c, a][:, cols].bitcast(FP8X4),
+                        rhs_scale=scales["q", c, a][:, cols],
+                        start=(f == 0),
+                        stop=(f == 1),
+                    )
 
-        def MK(g, c, b):
+        def MK(g, c, b, lo=0, hi=2):
+            a, j = divmod(b, 2)
             nc.vector.tensor_tensor(
-                out=s_bf[g, c, b // 2][:, b % 2].rearrange("p (m i) t -> p m t i", i=4),
-                in0=psum["M1", g, c, b][:].rearrange("p (t m i) -> p m t i", t=4, i=4),
-                in1=gain[g + c][:, 32 * b : 32 * (b + 1), :].rearrange("p m (t i) -> p m t i", i=4),
+                out=s_two[g, c, a][:, j, 128 * lo : 128 * hi].rearrange("p (m i) e -> p m e i", i=4),
+                in0=psum["M1", g, c, b][:].rearrange("p (e m i) -> p m e i", e=2, i=4)[:, 32 * lo : 32 * hi],
+                in1=gain[g + c][:, j, 64 * a + 32 * lo : 64 * a + 32 * hi, :].rearrange("p m (e i) -> p m e i", i=4),
                 op=ALU.mult,
             )
+
+        def WC(g, c, b, eng, lo=0, hi=2):
+            words = s_two[g, c, b // 2][:].rearrange("p j q e -> p j (q e)").bitcast(F32)[:, :, 128 * lo : 128 * hi]
+            dst = s_bf[g, c, b // 2][:, lo:hi].rearrange("p j i t -> p (j i) t").bitcast(F32)
+            if eng == "S":
+                nc.scalar.copy(dst, words.rearrange("p j q -> p q j"))
+            else:
+                nc.vector.tensor_copy(out=dst, in_=words.rearrange("p j q -> p q j"))
 
         def QS(g, c, b, n=2):
             lo = b % 2 + 1 - n
@@ -175,9 +182,9 @@ def tile_simplifiedretnet_pa_kernel(tc, q, k, v_bytes, v_scale, decay, out):
                 in_=s_bf[g, c, b // 2][:, lo : lo + n].rearrange("p j i t -> p (j i t)"),
             )
 
-        def M2(c, b, h):
-            bank = new_bank(("M2", c, b, h))
-            for g in range(c + 1):
+        def M2(c, b, h, first=0, last=1, score=False):
+            bank = new_bank(("M2", c, b, h), score) if first == 0 else psum["M2", c, b, h]
+            for g in range(first, min(c, last) + 1):
                 nc.tensor.matmul_mx(
                     out=bank[:],
                     lhsT=s_codes[g, c, b // 2][:, 128 * (b % 2) : 128 * (b % 2 + 1)].bitcast(FP8X4),
@@ -242,7 +249,7 @@ def tile_simplifiedretnet_pa_kernel(tc, q, k, v_bytes, v_scale, decay, out):
         WD(0, 3, 2, "V")
         IL(0, 0, "V")
         QZ("k", 0, 1)
-        QV(0, 0)
+        IL(0, 1, "V")
         QZ("k", 0, 3)
         TR("q", 0, 0)
         TR("q", 0, 1)
@@ -257,14 +264,15 @@ def tile_simplifiedretnet_pa_kernel(tc, q, k, v_bytes, v_scale, decay, out):
         WD(1, 2, 2, "S")
         EX(1, 2)
         QZ("q", 0, 1)
-        IL(0, 1, "V")
+        QV(0, 0)
         QZ("q", 0, 3)
         QV(0, 1)
-        WD(1, 0, 2, "V")
         M1(0, 0, 0)
+        M1(0, 0, 1)
         TR("q", 1, 0)
         TR("q", 1, 1)
         M1(0, 0, 2)
+        M1(0, 0, 3)
         TR("k", 1, 0)
         TR("k", 1, 1)
         CP("q", 1, 0, "S")
@@ -274,38 +282,44 @@ def tile_simplifiedretnet_pa_kernel(tc, q, k, v_bytes, v_scale, decay, out):
         CP("k", 1, 1, "S")
         EX(1, 3)
         MK(0, 0, 0)
+        WD(1, 0, 2, "V")
         MK(0, 0, 1)
         WD(1, 1, 2, "V")
-        QS(0, 0, 1)
+        WC(0, 0, 1, "V")
         QZ("q", 1, 1)
+        QS(0, 0, 1)
         MK(0, 0, 2)
         MK(0, 0, 3)
+        IL(1, 0, "V")
+        WC(0, 0, 3, "V")
         QZ("k", 1, 1)
         QS(0, 0, 3)
-        IL(1, 0, "V")
-        TR("k", 1, 2)
-        TR("k", 1, 3)
         M2(0, 0, 0)
         M2(0, 0, 1)
+        TR("k", 1, 2)
+        TR("k", 1, 3)
         M1(0, 1, 0)
+        M1(0, 1, 1)
         CP("k", 1, 2, "S")
         CP("k", 1, 3, "S")
-        EX(2, 0)
-        EX(2, 1)
         CO(0, 0, 0, "S")
         ST(0, 0, 0)
         CO(0, 0, 1, "S")
         ST(0, 0, 1)
+        EX(2, 0)
+        EX(2, 1)
         QZ("k", 1, 3)
+        QV(1, 0)
         MK(0, 1, 0)
         MK(0, 1, 1)
-        QV(1, 0)
-        QS(0, 1, 1)
+        IL(1, 1, "V")
+        WC(0, 1, 1, "V")
         TR("q", 1, 2)
         TR("q", 1, 3)
-        M1(1, 1, 0)
         M2(0, 1, 0)
         M2(0, 1, 1)
+        M1(1, 1, 0)
+        M1(1, 1, 1)
         CP("q", 1, 2, "S")
         CP("q", 1, 3, "S")
         EX(2, 2)
@@ -315,16 +329,19 @@ def tile_simplifiedretnet_pa_kernel(tc, q, k, v_bytes, v_scale, decay, out):
         CO(0, 1, 1, "S")
         ST(0, 1, 1)
         QZ("q", 1, 3)
+        QS(0, 1, 1)
         MK(1, 1, 0)
         MK(1, 1, 1)
-        IL(1, 1, "V")
-        QS(1, 1, 1)
+        QV(1, 1)
+        WC(1, 1, 1, "V")
         M2(0, 2, 0)
         M2(0, 2, 1)
         M1(0, 1, 2)
+        M1(0, 1, 3)
         M2(0, 3, 0)
         M2(0, 3, 1)
         M1(1, 1, 2)
+        M1(1, 1, 3)
         CO(0, 2, 0, "S")
         ST(0, 2, 0)
         CO(0, 2, 1, "S")
@@ -333,31 +350,41 @@ def tile_simplifiedretnet_pa_kernel(tc, q, k, v_bytes, v_scale, decay, out):
         ST(0, 3, 0)
         CO(0, 3, 1, "S")
         ST(0, 3, 1)
-        MK(0, 1, 2)
-        QV(1, 1)
-        MK(1, 1, 2)
+        MK(0, 1, 2, 0, 1)
+        QS(1, 1, 1)
+        MK(0, 1, 3, 0, 1)
+        MK(1, 1, 2, 0, 1)
+        WC(0, 1, 3, "V", 0, 1)
+        MK(1, 1, 3, 0, 1)
         QS(0, 1, 2, 1)
-        MK(0, 1, 3)
+        MK(0, 1, 2, 1, 2)
+        WC(1, 1, 3, "V", 0, 1)
+        MK(0, 1, 3, 1, 2)
         QS(1, 1, 2, 1)
-        MK(1, 1, 3)
+        MK(1, 1, 2, 1, 2)
+        WC(0, 1, 3, "V", 1, 2)
+        MK(1, 1, 3, 1, 2)
         QS(0, 1, 3, 1)
+        WC(1, 1, 3, "V", 1, 2)
         QS(1, 1, 3, 1)
         M2(1, 0, 0)
-        M2(1, 1, 0)
         M2(1, 0, 1)
+        M2(1, 1, 0)
         M2(1, 1, 1)
         CO(1, 0, 0, "S")
         ST(1, 0, 0)
-        CO(1, 1, 0, "S")
-        ST(1, 1, 0)
         CO(1, 0, 1, "S")
         ST(1, 0, 1)
+        CO(1, 1, 0, "S")
+        ST(1, 1, 0)
         CO(1, 1, 1, "S")
         ST(1, 1, 1)
         M2(1, 2, 0)
         M2(1, 2, 1)
-        M2(1, 3, 0)
-        M2(1, 3, 1)
+        M2(1, 3, 0, 0, 0, True)
+        M2(1, 3, 1, 0, 0, True)
+        M2(1, 3, 0, 1)
+        M2(1, 3, 1, 1)
         CO(1, 2, 0, "S")
         ST(1, 2, 0)
         CO(1, 2, 1, "S")

@@ -15,6 +15,7 @@ ACT = mybir.ActivationFunctionType
 FLOPS = 2 * 1024 * (512 * 512 + 512 * 1024) * 2
 BIG = 2.0**100
 LOG_SCALE = -5.0 * math.log(2.0)
+WIDE = (1,)
 
 
 def tile_simplifiedretnet_pa_kernel(tc, q, k, v_bytes, v_scale, decay, out):
@@ -45,11 +46,11 @@ def tile_simplifiedretnet_pa_kernel(tc, q, k, v_bytes, v_scale, decay, out):
         codes = {key: sb("cod_%s_%s_%s" % key, [128, 512], U32) for key in twos}
         scales = {key: sb("scl_%s_%s_%s" % key, [128, 512], U8) for key in twos}
         vb = {}
-        wide = [sb("wide%s" % (g,), [128, 4, 1024], BF16) for g in range(2)]
+        wide = [sb("wide%s" % (g,), [128, 2, 1024, 2], BF16) for g in range(2)]
         vi = {key: sb("vi%s_%s" % key, [128, 512, 4], BF16) for key in halves}
         v_codes = {key: sb("vc%s_%s" % key, [128, 512], U32) for key in halves}
         v_scl = {key: sb("vx%s_%s" % key, [128, 512], U8) for key in halves}
-        gain = [sb("gain%s" % (e,), [128, 2, 128, 8], F32) for e in range(3)]
+        gain = [sb("gain%s" % (e,), [128, 2048], F32) for e in range(3)]
         s_twos = [(g, c, a) for g, c in pairs for a in range(2)]
         s_bf = {key: sb("s%s_%s_%s" % key, [128, 2, 128, 4], BF16) for key in s_twos}
         s_two = {key: sb("sp%s_%s_%s" % key, [128, 2, 256, 2], BF16) for key in s_twos}
@@ -106,34 +107,38 @@ def tile_simplifiedretnet_pa_kernel(tc, q, k, v_bytes, v_scale, decay, out):
             )
 
         def WD(g, t, h, eng):
-            cols = slice(0, 1024) if h == 2 else slice(512 * h, 512 * (h + 1))
-            src = vb[g, t][:, cols].bitcast(E4M3FN)
-            if eng == "V":
-                nc.vector.tensor_scalar(out=wide[g][:, t, cols], in0=src, scalar1=vs[:, g, t : t + 1], scalar2=None, op0=ALU.mult)
-            else:
-                nc.scalar.activation(out=wide[g][:, t, cols], in_=src, func=ACT.Copy, scale=vs[:, g, t : t + 1])
+            nc.vector.tensor_scalar(
+                out=wide[g][:, t % 2, :, t // 2],
+                in0=vb[g, t].bitcast(E4M3FN),
+                scalar1=vs[:, g, t : t + 1],
+                scalar2=None,
+                op0=ALU.mult,
+            )
 
         def IL(g, h, eng):
-            src = wide[g][:, :, 512 * h : 512 * (h + 1)]
-            if eng == "V":
-                nc.vector.tensor_copy(
-                    out=vi[g, h][:].rearrange("p (m i) t -> p m t i", i=4), in_=src.rearrange("p t (m i) -> p m t i", i=4)
-                )
+            words = wide[g][:].rearrange("p j n e -> p j (n e)").bitcast(F32)
+            src = words[:, :, 512 * h : 512 * (h + 1)].rearrange("p j n -> p n j")
+            dst = vi[g, h][:].bitcast(F32)
+            if eng == "S":
+                nc.scalar.copy(dst, src)
             else:
-                nc.gpsimd.tensor_scalar(
-                    out=vi[g, h][:], in0=src.rearrange("p t n -> p n t"), scalar1=1.0, scalar2=0.0, op0=ALU.mult, op1=ALU.add
-                )
+                nc.vector.tensor_copy(out=dst, in_=src)
 
         def QV(g, h):
             nc.vector.quantize_mx(
                 out=v_codes[g, h][:].bitcast(FP8X4), scales=v_scl[g, h][:], in_=vi[g, h][:].rearrange("p n t -> p (n t)")
             )
 
+        def gain_view(e):
+            if e in WIDE:
+                return gain[e][:].rearrange("p (j m e i) -> p j m e i", j=2, e=2, i=4)
+            return gain[e][:].rearrange("p (m j e i) -> p j m e i", j=2, e=2, i=4)
+
         def EX(e, t):
             table = dist if e == 1 else near
             col = 4 * (e // 2) + t
             nc.scalar.activation(
-                out=gain[e][:, t // 2, :, 4 * (t % 2) : 4 * (t % 2 + 1)],
+                out=gain_view(e)[:, t % 2, :, t // 2, :],
                 in_=table[:, 3 - t : 515 - t].rearrange("p (m i) -> p m i", i=4),
                 func=ACT.Exp,
                 bias=far_bias[:, t : t + 1] if e == 1 else LOG_SCALE,
@@ -143,14 +148,30 @@ def tile_simplifiedretnet_pa_kernel(tc, q, k, v_bytes, v_scale, decay, out):
         def M1(g, c, b):
             a, j = divmod(b, 2)
             bank = new_bank(("M1", g, c, b), True)
+            if g + c not in WIDE:
+                for t in range(4):
+                    slot = 2 * (t % 2) + t // 2
+                    for f in range(2):
+                        keys = slice(256 * f + 128 * (t % 2), 256 * f + 128 * (t % 2 + 1))
+                        cols = slice(256 * f + 128 * j, 256 * f + 128 * (j + 1))
+                        nc.tensor.matmul_mx(
+                            out=bank[:, 128 * slot : 128 * (slot + 1)],
+                            lhsT=codes["k", g, t // 2][:, keys].bitcast(FP8X4),
+                            lhsT_scale=scales["k", g, t // 2][:, keys],
+                            rhs=codes["q", c, a][:, cols].bitcast(FP8X4),
+                            rhs_scale=scales["q", c, a][:, cols],
+                            start=(f == 0),
+                            stop=(f == 1),
+                        )
+                return
             for e in range(2):
                 for f in range(2):
-                    keys = slice(256 * f + 128 * e, 256 * f + 128 * (e + 1))
+                    keys = slice(256 * f + 128 * j, 256 * f + 128 * (j + 1))
                     cols = slice(256 * f, 256 * (f + 1))
                     nc.tensor.matmul_mx(
                         out=bank[:, 256 * e : 256 * (e + 1)],
-                        lhsT=codes["k", g, j][:, keys].bitcast(FP8X4),
-                        lhsT_scale=scales["k", g, j][:, keys],
+                        lhsT=codes["k", g, e][:, keys].bitcast(FP8X4),
+                        lhsT_scale=scales["k", g, e][:, keys],
                         rhs=codes["q", c, a][:, cols].bitcast(FP8X4),
                         rhs_scale=scales["q", c, a][:, cols],
                         start=(f == 0),
@@ -159,10 +180,18 @@ def tile_simplifiedretnet_pa_kernel(tc, q, k, v_bytes, v_scale, decay, out):
 
         def MK(g, c, b, lo=0, hi=2):
             a, j = divmod(b, 2)
+            if g + c not in WIDE:
+                nc.vector.tensor_tensor(
+                    out=s_bf[g, c, a][:, j].rearrange("p (m i) t -> p m t i", i=4),
+                    in0=psum["M1", g, c, b][:].rearrange("p (t m i) -> p m t i", t=4, i=4),
+                    in1=gain[g + c][:, 512 * b : 512 * (b + 1)].rearrange("p (m t i) -> p m t i", t=4, i=4),
+                    op=ALU.mult,
+                )
+                return
             nc.vector.tensor_tensor(
                 out=s_two[g, c, a][:, j, 128 * lo : 128 * hi].rearrange("p (m i) e -> p m e i", i=4),
                 in0=psum["M1", g, c, b][:].rearrange("p (e m i) -> p m e i", e=2, i=4)[:, 32 * lo : 32 * hi],
-                in1=gain[g + c][:, j, 64 * a + 32 * lo : 64 * a + 32 * hi, :].rearrange("p m (e i) -> p m e i", i=4),
+                in1=gain_view(g + c)[:, j, 64 * a + 32 * lo : 64 * a + 32 * hi],
                 op=ALU.mult,
             )
 
@@ -236,8 +265,8 @@ def tile_simplifiedretnet_pa_kernel(tc, q, k, v_bytes, v_scale, decay, out):
         TR("k", 0, 2)
         TR("k", 0, 3)
         EX(0, 0)
-        EX(0, 1)
         EX(0, 2)
+        EX(0, 1)
         CP("k", 0, 0, "S")
         EX(0, 3)
         CP("k", 0, 1, "S")
@@ -247,8 +276,8 @@ def tile_simplifiedretnet_pa_kernel(tc, q, k, v_bytes, v_scale, decay, out):
         WD(0, 1, 2, "V")
         WD(0, 2, 2, "V")
         WD(0, 3, 2, "V")
-        IL(0, 0, "V")
         QZ("k", 0, 1)
+        IL(0, 0, "V")
         IL(0, 1, "V")
         QZ("k", 0, 3)
         TR("q", 0, 0)
@@ -260,44 +289,44 @@ def tile_simplifiedretnet_pa_kernel(tc, q, k, v_bytes, v_scale, decay, out):
         CP("q", 0, 2, "S")
         CP("q", 0, 3, "S")
         EX(1, 0)
-        EX(1, 1)
-        WD(1, 2, 2, "S")
-        EX(1, 2)
         QZ("q", 0, 1)
         QV(0, 0)
         QZ("q", 0, 3)
         QV(0, 1)
-        M1(0, 0, 0)
-        M1(0, 0, 1)
+        WD(1, 0, 2, "V")
         TR("q", 1, 0)
         TR("q", 1, 1)
-        M1(0, 0, 2)
-        M1(0, 0, 3)
+        M1(0, 0, 0)
+        M1(0, 0, 1)
         TR("k", 1, 0)
         TR("k", 1, 1)
+        M1(0, 0, 2)
+        M1(0, 0, 3)
         CP("q", 1, 0, "S")
         CP("q", 1, 1, "S")
-        WD(1, 3, 2, "S")
+        EX(1, 2)
+        EX(1, 1)
+        EX(1, 3)
         CP("k", 1, 0, "S")
         CP("k", 1, 1, "S")
-        EX(1, 3)
-        MK(0, 0, 0)
-        WD(1, 0, 2, "V")
-        MK(0, 0, 1)
-        WD(1, 1, 2, "V")
-        WC(0, 0, 1, "V")
+        EX(2, 0)
+        EX(2, 2)
+        EX(2, 1)
+        EX(2, 3)
         QZ("q", 1, 1)
+        MK(0, 0, 0)
+        WD(1, 1, 2, "V")
+        MK(0, 0, 1)
+        WD(1, 2, 2, "V")
         QS(0, 0, 1)
-        MK(0, 0, 2)
-        MK(0, 0, 3)
-        IL(1, 0, "V")
-        WC(0, 0, 3, "V")
         QZ("k", 1, 1)
-        QS(0, 0, 3)
-        M2(0, 0, 0)
-        M2(0, 0, 1)
+        MK(0, 0, 2)
+        WD(1, 3, 2, "V")
+        MK(0, 0, 3)
         TR("k", 1, 2)
         TR("k", 1, 3)
+        M2(0, 0, 0)
+        M2(0, 0, 1)
         M1(0, 1, 0)
         M1(0, 1, 1)
         CP("k", 1, 2, "S")
@@ -306,13 +335,12 @@ def tile_simplifiedretnet_pa_kernel(tc, q, k, v_bytes, v_scale, decay, out):
         ST(0, 0, 0)
         CO(0, 0, 1, "S")
         ST(0, 0, 1)
-        EX(2, 0)
-        EX(2, 1)
+        IL(1, 0, "S")
         QZ("k", 1, 3)
-        QV(1, 0)
+        QS(0, 0, 3)
         MK(0, 1, 0)
         MK(0, 1, 1)
-        IL(1, 1, "V")
+        QV(1, 0)
         WC(0, 1, 1, "V")
         TR("q", 1, 2)
         TR("q", 1, 3)
@@ -322,8 +350,7 @@ def tile_simplifiedretnet_pa_kernel(tc, q, k, v_bytes, v_scale, decay, out):
         M1(1, 1, 1)
         CP("q", 1, 2, "S")
         CP("q", 1, 3, "S")
-        EX(2, 2)
-        EX(2, 3)
+        IL(1, 1, "S")
         CO(0, 1, 0, "S")
         ST(0, 1, 0)
         CO(0, 1, 1, "S")
@@ -333,7 +360,7 @@ def tile_simplifiedretnet_pa_kernel(tc, q, k, v_bytes, v_scale, decay, out):
         MK(1, 1, 0)
         MK(1, 1, 1)
         QV(1, 1)
-        WC(1, 1, 1, "V")
+        QS(1, 1, 1)
         M2(0, 2, 0)
         M2(0, 2, 1)
         M1(0, 1, 2)
@@ -341,7 +368,6 @@ def tile_simplifiedretnet_pa_kernel(tc, q, k, v_bytes, v_scale, decay, out):
         M2(0, 3, 0)
         M2(0, 3, 1)
         M1(1, 1, 2)
-        M1(1, 1, 3)
         CO(0, 2, 0, "S")
         ST(0, 2, 0)
         CO(0, 2, 1, "S")
@@ -350,25 +376,15 @@ def tile_simplifiedretnet_pa_kernel(tc, q, k, v_bytes, v_scale, decay, out):
         ST(0, 3, 0)
         CO(0, 3, 1, "S")
         ST(0, 3, 1)
-        MK(0, 1, 2, 0, 1)
-        QS(1, 1, 1)
-        MK(0, 1, 3, 0, 1)
-        MK(1, 1, 2, 0, 1)
-        WC(0, 1, 3, "V", 0, 1)
-        MK(1, 1, 3, 0, 1)
-        QS(0, 1, 2, 1)
-        MK(0, 1, 2, 1, 2)
-        WC(1, 1, 3, "V", 0, 1)
-        MK(0, 1, 3, 1, 2)
+        MK(0, 1, 2)
+        MK(0, 1, 3)
+        MK(1, 1, 2)
+        WC(0, 1, 3, "V")
         QS(1, 1, 2, 1)
-        MK(1, 1, 2, 1, 2)
-        WC(0, 1, 3, "V", 1, 2)
-        MK(1, 1, 3, 1, 2)
-        QS(0, 1, 3, 1)
-        WC(1, 1, 3, "V", 1, 2)
-        QS(1, 1, 3, 1)
+        QS(0, 1, 3)
         M2(1, 0, 0)
         M2(1, 0, 1)
+        M1(1, 1, 3)
         M2(1, 1, 0)
         M2(1, 1, 1)
         CO(1, 0, 0, "S")
@@ -379,17 +395,17 @@ def tile_simplifiedretnet_pa_kernel(tc, q, k, v_bytes, v_scale, decay, out):
         ST(1, 1, 0)
         CO(1, 1, 1, "S")
         ST(1, 1, 1)
+        MK(1, 1, 3)
+        QS(1, 1, 3, 1)
         M2(1, 2, 0)
         M2(1, 2, 1)
-        M2(1, 3, 0, 0, 0, True)
-        M2(1, 3, 1, 0, 0, True)
-        M2(1, 3, 0, 1)
-        M2(1, 3, 1, 1)
+        M2(1, 3, 0)
+        M2(1, 3, 1)
         CO(1, 2, 0, "S")
         ST(1, 2, 0)
-        CO(1, 2, 1, "S")
-        ST(1, 2, 1)
         CO(1, 3, 0, "S")
+        CO(1, 2, 1, "V")
+        ST(1, 2, 1)
         ST(1, 3, 0)
         CO(1, 3, 1, "V")
         ST(1, 3, 1)

@@ -56,7 +56,7 @@ def tile_simplifiedretnet_pa_kernel(tc, q, k, v_bytes, v_scale, decay, out):
         s_two = {key: sb("sp%s_%s_%s" % key, [128, 2, 256, 2], BF16) for key in s_twos}
         s_codes = {key: sb("sc%s_%s_%s" % key, [128, 256], U32) for key in s_twos}
         s_scl = {key: sb("sx%s_%s_%s" % key, [128, 256], U8) for key in s_twos}
-        result = {(c, b, h): sb("o%s_%s_%s" % (c, b, h), [128, 512], F32) for c in range(2) for b in range(4) for h in range(2)}
+        result = {(c, b): sb("o%s_%s" % (c, b), [128, 1024], F32) for c in range(2) for b in range(4)}
         ident = sb("ident", [128, 128], F32)
         dist = sb("dist", [128, 516], F32)
         near = sb("near", [128, 516], F32)
@@ -226,14 +226,14 @@ def tile_simplifiedretnet_pa_kernel(tc, q, k, v_bytes, v_scale, decay, out):
 
         def CO(c, b, h, eng):
             src = psum["M2", c, b, h]
-            res = result[c, b, h]
+            res = result[c, b][:, 512 * h : 512 * (h + 1)]
             if eng == "S":
-                nc.scalar.copy(res[:], src[:])
+                nc.scalar.copy(res, src[:])
             else:
-                nc.vector.tensor_copy(out=res[:], in_=src[:])
+                nc.vector.tensor_copy(out=res, in_=src[:])
 
-        def ST(c, b, h):
-            nc.sync.dma_start(out=o_rows[c][:, b, 512 * h : 512 * (h + 1)], in_=result[c, b, h][:])
+        def ST(c, b, lo, hi):
+            nc.sync.dma_start(out=o_rows[c][:, b, 512 * lo : 512 * hi], in_=result[c, b][:, 512 * lo : 512 * hi])
 
         nc.scalar.dma_start(out=dk[:], in_=decay.rearrange("(g p t) -> p g t", g=2, t=4))
         nc.scalar.dma_start(out=vs[:], in_=v_scale.rearrange("o (g p t) i -> p (o g) (t i)", g=2, t=4))
@@ -267,8 +267,9 @@ def tile_simplifiedretnet_pa_kernel(tc, q, k, v_bytes, v_scale, decay, out):
         EX(0, 0)
         EX(0, 2)
         EX(0, 1)
-        CP("k", 0, 0, "S")
         EX(0, 3)
+        CP("k", 0, 0, "S")
+        EX(1, 0)
         CP("k", 0, 1, "S")
         CP("k", 0, 2, "S")
         CP("k", 0, 3, "S")
@@ -288,7 +289,7 @@ def tile_simplifiedretnet_pa_kernel(tc, q, k, v_bytes, v_scale, decay, out):
         CP("q", 0, 1, "S")
         CP("q", 0, 2, "S")
         CP("q", 0, 3, "S")
-        EX(1, 0)
+        EX(1, 2)
         QZ("q", 0, 1)
         QV(0, 0)
         QZ("q", 0, 3)
@@ -304,13 +305,12 @@ def tile_simplifiedretnet_pa_kernel(tc, q, k, v_bytes, v_scale, decay, out):
         M1(0, 0, 3)
         CP("q", 1, 0, "S")
         CP("q", 1, 1, "S")
-        EX(1, 2)
         EX(1, 1)
         EX(1, 3)
-        CP("k", 1, 0, "S")
-        CP("k", 1, 1, "S")
         EX(2, 0)
         EX(2, 2)
+        CP("k", 1, 0, "S")
+        CP("k", 1, 1, "S")
         EX(2, 1)
         EX(2, 3)
         QZ("q", 1, 1)
@@ -332,9 +332,8 @@ def tile_simplifiedretnet_pa_kernel(tc, q, k, v_bytes, v_scale, decay, out):
         CP("k", 1, 2, "S")
         CP("k", 1, 3, "S")
         CO(0, 0, 0, "S")
-        ST(0, 0, 0)
         CO(0, 0, 1, "S")
-        ST(0, 0, 1)
+        ST(0, 0, 0, 2)
         IL(1, 0, "S")
         QZ("k", 1, 3)
         QS(0, 0, 3)
@@ -350,11 +349,10 @@ def tile_simplifiedretnet_pa_kernel(tc, q, k, v_bytes, v_scale, decay, out):
         M1(1, 1, 1)
         CP("q", 1, 2, "S")
         CP("q", 1, 3, "S")
-        IL(1, 1, "S")
         CO(0, 1, 0, "S")
-        ST(0, 1, 0)
         CO(0, 1, 1, "S")
-        ST(0, 1, 1)
+        ST(0, 1, 0, 2)
+        IL(1, 1, "S")
         QZ("q", 1, 3)
         QS(0, 1, 1)
         MK(1, 1, 0)
@@ -369,13 +367,11 @@ def tile_simplifiedretnet_pa_kernel(tc, q, k, v_bytes, v_scale, decay, out):
         M2(0, 3, 1)
         M1(1, 1, 2)
         CO(0, 2, 0, "S")
-        ST(0, 2, 0)
         CO(0, 2, 1, "S")
-        ST(0, 2, 1)
+        ST(0, 2, 0, 2)
         CO(0, 3, 0, "S")
-        ST(0, 3, 0)
         CO(0, 3, 1, "S")
-        ST(0, 3, 1)
+        ST(0, 3, 0, 2)
         MK(0, 1, 2)
         MK(0, 1, 3)
         MK(1, 1, 2)
@@ -388,24 +384,26 @@ def tile_simplifiedretnet_pa_kernel(tc, q, k, v_bytes, v_scale, decay, out):
         M2(1, 1, 0)
         M2(1, 1, 1)
         CO(1, 0, 0, "S")
-        ST(1, 0, 0)
+        ST(1, 0, 0, 1)
         CO(1, 0, 1, "S")
-        ST(1, 0, 1)
+        ST(1, 0, 1, 2)
         CO(1, 1, 0, "S")
-        ST(1, 1, 0)
+        ST(1, 1, 0, 1)
         CO(1, 1, 1, "S")
-        ST(1, 1, 1)
+        ST(1, 1, 1, 2)
         MK(1, 1, 3)
         QS(1, 1, 3, 1)
         M2(1, 2, 0)
         M2(1, 2, 1)
-        M2(1, 3, 0)
-        M2(1, 3, 1)
+        M2(1, 3, 0, 0, 0, True)
+        M2(1, 3, 1, 0, 0, True)
+        M2(1, 3, 0, 1)
+        M2(1, 3, 1, 1)
         CO(1, 2, 0, "S")
-        ST(1, 2, 0)
+        ST(1, 2, 0, 1)
+        CO(1, 2, 1, "S")
+        ST(1, 2, 1, 2)
         CO(1, 3, 0, "S")
-        CO(1, 2, 1, "V")
-        ST(1, 2, 1)
-        ST(1, 3, 0)
+        ST(1, 3, 0, 1)
         CO(1, 3, 1, "V")
-        ST(1, 3, 1)
+        ST(1, 3, 1, 2)

@@ -13,19 +13,23 @@ ALU = mybir.AluOpType
 ACT = mybir.ActivationFunctionType
 
 FLOPS = 2 * 1024 * (512 * 512 + 512 * 1024) * 2
-BIG = 2.0**100
+P = 128
+CHUNK = 512
+RUN = 4
+MASKED = 2.0**100
+LEAST_RATE = 2.0**-90
 LOG_SCALE = -5.0 * math.log(2.0)
-WIDE = (1,)
+NEAR0, FAR, NEAR1 = (0, 0), (0, 1), (1, 1)
 
 
 def tile_simplifiedretnet_pa_kernel(tc, q, k, v_bytes, v_scale, decay, out):
     nc = tc.nc
-    x_rows = {
+    rows_of = {
         "q": q.rearrange("o (c b m) f -> (o c) m b f", c=2, b=4),
         "k": k.rearrange("o (c m b) f -> (o c) m b f", c=2, b=4),
     }
-    v_rows = v_bytes.rearrange("o (g p t) n -> (o g) p t n", g=2, t=4)
-    o_rows = out.rearrange("o (c b m) n -> (o c) m b n", c=2, b=4)
+    v_planes = v_bytes.rearrange("o (g p r) n -> (o g) p r n", g=2, r=4)
+    out_rows = out.rearrange("o (c b m) n -> (o c) m b n", c=2, b=4)
 
     with ExitStack() as ctx:
         keep = ctx.enter_context(tc.tile_pool(name="keep", bufs=1))
@@ -36,374 +40,320 @@ def tile_simplifiedretnet_pa_kernel(tc, q, k, v_bytes, v_scale, decay, out):
         def sb(name, shape, dtype):
             return keep.tile(shape, dtype, name=name, align_bytes=64)
 
-        blocks = [(x, c, b) for x in "qk" for c in range(2) for b in range(4)]
-        halves = [(g, h) for g in range(2) for h in range(2)]
-        pairs = [(0, 0), (0, 1), (1, 1)]
-        tiles = [(g, c, b) for g, c in pairs for b in range(4)]
-        raw = {}
-        twos = [(x, c, a) for x in "qk" for c in range(2) for a in range(2)]
-        grouped = {key: sb("grp_%s_%s_%s" % key, [128, 2, 2, 128, 2], F32) for key in twos}
-        codes = {key: sb("cod_%s_%s_%s" % key, [128, 512], U32) for key in twos}
-        scales = {key: sb("scl_%s_%s_%s" % key, [128, 512], U8) for key in twos}
-        vb = {}
-        wide = [sb("wide%s" % (g,), [128, 2, 1024, 2], BF16) for g in range(2)]
-        vi = {key: sb("vi%s_%s" % key, [128, 512, 4], BF16) for key in halves}
-        v_codes = {key: sb("vc%s_%s" % key, [128, 512], U32) for key in halves}
-        v_scl = {key: sb("vx%s_%s" % key, [128, 512], U8) for key in halves}
-        gain = [sb("gain%s" % (e,), [128, 2048], F32) for e in range(3)]
-        s_twos = [(g, c, a) for g, c in pairs for a in range(2)]
-        s_bf = {key: sb("s%s_%s_%s" % key, [128, 2, 128, 4], BF16) for key in s_twos}
-        s_two = {key: sb("sp%s_%s_%s" % key, [128, 2, 256, 2], BF16) for key in s_twos}
-        s_codes = {key: sb("sc%s_%s_%s" % key, [128, 256], U32) for key in s_twos}
-        s_scl = {key: sb("sx%s_%s_%s" % key, [128, 256], U8) for key in s_twos}
-        result = {(c, b): sb("o%s_%s" % (c, b), [128, 1024], F32) for c in range(2) for b in range(4)}
-        ident = sb("ident", [128, 128], F32)
-        dist = sb("dist", [128, 516], F32)
-        near = sb("near", [128, 516], F32)
-        far_bias = sb("far_bias", [128, 4], F32)
-        dk = sb("dk", [128, 2, 4], BF16)
-        nd = sb("nd", [128, 8], F32)
-        vs = sb("vs", [128, 2, 4], F32)
-        warm = sb("warm", [128, 8], F32)
-        warm_out = sb("warm_out", [128, 8], F32)
+        row_pairs = [(x, c, a) for x in "qk" for c in range(2) for a in range(2)]
+        v_halves = [(g, h) for g in range(2) for h in range(2)]
+        score_pairs = [(g, c, a) for g, c in (NEAR0, FAR, NEAR1) for a in range(2)]
+        turned = {key: sb("turned_%s_%s_%s" % key, [P, 2, 2, P, 2], F32) for key in row_pairs}
+        x_codes = {key: sb("x_codes_%s_%s_%s" % key, [P, 512], U32) for key in row_pairs}
+        x_scales = {key: sb("x_scales_%s_%s_%s" % key, [P, 512], U8) for key in row_pairs}
+        v_wide = [sb("v_wide_%s" % (g,), [P, 2, 1024, 2], BF16) for g in range(2)]
+        v_words = {key: sb("v_words_%s_%s" % key, [P, CHUNK, 4], BF16) for key in v_halves}
+        v_codes = {key: sb("v_codes_%s_%s" % key, [P, CHUNK], U32) for key in v_halves}
+        v_scales = {key: sb("v_scales_%s_%s" % key, [P, CHUNK], U8) for key in v_halves}
+        gain = [sb("gain_%s" % (table,), [P, 4 * CHUNK], F32) for table in range(3)]
+        s_words = {key: sb("s_words_%s_%s_%s" % key, [P, 2, P, 4], BF16) for key in score_pairs}
+        far_halves = [sb("far_halves_%s" % (a,), [P, 2, 2 * P, 2], BF16) for a in range(2)]
+        s_codes = {key: sb("s_codes_%s_%s_%s" % key, [P, 2 * P], U32) for key in score_pairs}
+        s_scales = {key: sb("s_scales_%s_%s_%s" % key, [P, 2 * P], U8) for key in score_pairs}
+        result = {(c, b): sb("result_%s_%s" % (c, b), [P, 1024], F32) for c in range(2) for b in range(4)}
+        ident = sb("ident", [P, P], F32)
+        dist = sb("dist", [P, CHUNK + 4], F32)
+        causal_dist = sb("causal_dist", [P, CHUNK + 4], F32)
+        far_bias = sb("far_bias", [P, 4], F32)
+        rate = sb("rate", [P, 2, 4], BF16)
+        neg_rate = sb("neg_rate", [P, 8], F32)
+        key_scale = sb("key_scale", [P, 2, 4], F32)
 
+        raw = {}
+        fp8 = {}
         psum = {}
 
-        def load(x, c, lo, hi):
-            rows = sb("raw_%s_%s_%s" % (x, c, lo), [128, hi - lo, 1024], BF16)
-            nc.sync.dma_start(out=rows[:], in_=x_rows[x][c][:, lo:hi, :])
+        def load_rows(x, c, lo, hi):
+            rows = sb("raw_%s_%s_%s" % (x, c, lo), [P, hi - lo, 1024], BF16)
+            nc.sync.dma_start(out=rows[:], in_=rows_of[x][c][:, lo:hi, :])
             for b in range(lo, hi):
                 raw[x, c, b] = rows[:, b - lo, :]
 
-        def loadv(g, t0, t1, n0, n1):
-            rows = sb("vb_%s_%s" % (g, t0), [128, t1 - t0, 1024], U8)
-            nc.sync.dma_start(out=rows[:], in_=v_rows[g][:, t0:t1, :])
-            for t in range(t0, t1):
-                vb[g, t] = rows[:, t - t0, :]
+        def load_v(g, lo, hi):
+            planes = sb("fp8_%s_%s" % (g, lo), [P, hi - lo, 1024], U8)
+            nc.sync.dma_start(out=planes[:], in_=v_planes[g][:, lo:hi, :])
+            for r in range(lo, hi):
+                fp8[g, r] = planes[:, r - lo, :]
 
-        def new_bank(key, score=False):
-            psum[key] = (score_banks if score else other_banks).tile([128, 512], F32, name="bank")
+        def new_bank(key, pool):
+            psum[key] = pool.tile([P, CHUNK], F32, name="bank")
             return psum[key]
 
-        def TR(x, c, b):
-            bank = new_bank(("TR", x, c, b))[:].rearrange("p (g u r) -> p g u r", g=2, u=2)
+        def turn(x, c, b):
+            bank = new_bank(("turn", x, c, b), other_banks)[:].rearrange("p (f u m) -> p f u m", f=2, u=2)
             words = raw[x, c, b].bitcast(F32)
-            for g in range(2):
+            for f in range(2):
                 for u in range(2):
-                    nc.tensor.transpose(bank[:, g, u, :], words[:, 256 * g + u : 256 * (g + 1) : 2], ident[:])
+                    nc.tensor.transpose(bank[:, f, u, :], words[:, 256 * f + u : 256 * (f + 1) : 2], ident[:])
 
-        def CP(x, c, b, eng):
-            src = psum["TR", x, c, b][:].rearrange("p (g u r) -> p g r u", g=2, u=2)
-            if eng == "S":
-                nc.scalar.copy(grouped[x, c, b // 2][:, :, b % 2], src)
-            else:
-                nc.vector.tensor_copy(out=grouped[x, c, b // 2][:, :, b % 2], in_=src)
+        def copy_turned(x, c, b):
+            src = psum["turn", x, c, b][:].rearrange("p (f u m) -> p f m u", f=2, u=2)
+            nc.scalar.copy(turned[x, c, b // 2][:, :, b % 2], src)
 
-        def QZ(x, c, b):
+        def quantise_rows(x, c, a):
             nc.vector.quantize_mx(
-                out=codes[x, c, b // 2][:].bitcast(FP8X4),
-                scales=scales[x, c, b // 2][:],
-                in_=grouped[x, c, b // 2][:].rearrange("p f j r u -> p (f j r u)").bitcast(BF16),
+                out=x_codes[x, c, a][:].bitcast(FP8X4),
+                scales=x_scales[x, c, a][:],
+                in_=turned[x, c, a][:].rearrange("p f b m u -> p (f b m u)").bitcast(BF16),
             )
 
-        def WD(g, t, h, eng):
+        def widen_v(g, r):
             nc.vector.tensor_scalar(
-                out=wide[g][:, t % 2, :, t // 2],
-                in0=vb[g, t].bitcast(E4M3FN),
-                scalar1=vs[:, g, t : t + 1],
+                out=v_wide[g][:, r % 2, :, r // 2],
+                in0=fp8[g, r].bitcast(E4M3FN),
+                scalar1=key_scale[:, g, r : r + 1],
                 scalar2=None,
                 op0=ALU.mult,
             )
 
-        def IL(g, h, eng):
-            words = wide[g][:].rearrange("p j n e -> p j (n e)").bitcast(F32)
-            src = words[:, :, 512 * h : 512 * (h + 1)].rearrange("p j n -> p n j")
-            dst = vi[g, h][:].bitcast(F32)
-            if eng == "S":
-                nc.scalar.copy(dst, src)
+        def join_halves(dst, halves, on_scalar):
+            src = halves.rearrange("p j n -> p n j")
+            if on_scalar:
+                nc.scalar.copy(dst.bitcast(F32), src)
             else:
-                nc.vector.tensor_copy(out=dst, in_=src)
+                nc.vector.tensor_copy(out=dst.bitcast(F32), in_=src)
 
-        def QV(g, h):
+        def join_v(g, h):
+            halves = v_wide[g][:].rearrange("p j n e -> p j (n e)").bitcast(F32)
+            join_halves(v_words[g, h][:], halves[:, :, CHUNK * h : CHUNK * (h + 1)], g == 1)
+
+        def quantise_v(g, h):
             nc.vector.quantize_mx(
-                out=v_codes[g, h][:].bitcast(FP8X4), scales=v_scl[g, h][:], in_=vi[g, h][:].rearrange("p n t -> p (n t)")
+                out=v_codes[g, h][:].bitcast(FP8X4),
+                scales=v_scales[g, h][:],
+                in_=v_words[g, h][:].rearrange("p n t -> p (n t)"),
             )
 
-        def gain_view(e):
-            if e in WIDE:
-                return gain[e][:].rearrange("p (j m e i) -> p j m e i", j=2, e=2, i=4)
-            return gain[e][:].rearrange("p (m j e i) -> p j m e i", j=2, e=2, i=4)
+        def gain_view(tile):
+            order = "p (j m e i) -> p j m e i" if tile == FAR else "p (m j e i) -> p j m e i"
+            return gain[sum(tile)][:].rearrange(order, j=2, e=2, i=RUN)
 
-        def EX(e, t):
-            table = dist if e == 1 else near
-            col = 4 * (e // 2) + t
+        def make_gain(tile, r):
+            table = dist if tile == FAR else causal_dist
+            col = 4 * tile[0] + r
             nc.scalar.activation(
-                out=gain_view(e)[:, t % 2, :, t // 2, :],
-                in_=table[:, 3 - t : 515 - t].rearrange("p (m i) -> p m i", i=4),
+                out=gain_view(tile)[:, r % 2, :, r // 2, :],
+                in_=table[:, 3 - r : 3 - r + CHUNK].rearrange("p (m i) -> p m i", i=RUN),
                 func=ACT.Exp,
-                bias=far_bias[:, t : t + 1] if e == 1 else LOG_SCALE,
-                scale=nd[:, col : col + 1],
+                bias=far_bias[:, r : r + 1] if tile == FAR else LOG_SCALE,
+                scale=neg_rate[:, col : col + 1],
             )
 
-        def M1(g, c, b):
-            a, j = divmod(b, 2)
-            bank = new_bank(("M1", g, c, b), True)
-            if g + c not in WIDE:
-                for t in range(4):
-                    slot = 2 * (t % 2) + t // 2
-                    for f in range(2):
-                        keys = slice(256 * f + 128 * (t % 2), 256 * f + 128 * (t % 2 + 1))
-                        cols = slice(256 * f + 128 * j, 256 * f + 128 * (j + 1))
-                        nc.tensor.matmul_mx(
-                            out=bank[:, 128 * slot : 128 * (slot + 1)],
-                            lhsT=codes["k", g, t // 2][:, keys].bitcast(FP8X4),
-                            lhsT_scale=scales["k", g, t // 2][:, keys],
-                            rhs=codes["q", c, a][:, cols].bitcast(FP8X4),
-                            rhs_scale=scales["q", c, a][:, cols],
-                            start=(f == 0),
-                            stop=(f == 1),
-                        )
-                return
-            for e in range(2):
-                for f in range(2):
-                    keys = slice(256 * f + 128 * j, 256 * f + 128 * (j + 1))
-                    cols = slice(256 * f, 256 * (f + 1))
-                    nc.tensor.matmul_mx(
-                        out=bank[:, 256 * e : 256 * (e + 1)],
-                        lhsT=codes["k", g, e][:, keys].bitcast(FP8X4),
-                        lhsT_scale=scales["k", g, e][:, keys],
-                        rhs=codes["q", c, a][:, cols].bitcast(FP8X4),
-                        rhs_scale=scales["q", c, a][:, cols],
-                        start=(f == 0),
-                        stop=(f == 1),
-                    )
-
-        def MK(g, c, b, lo=0, hi=2):
-            a, j = divmod(b, 2)
-            if g + c not in WIDE:
-                nc.vector.tensor_tensor(
-                    out=s_bf[g, c, a][:, j].rearrange("p (m i) t -> p m t i", i=4),
-                    in0=psum["M1", g, c, b][:].rearrange("p (t m i) -> p m t i", t=4, i=4),
-                    in1=gain[g + c][:, 512 * b : 512 * (b + 1)].rearrange("p (m t i) -> p m t i", t=4, i=4),
-                    op=ALU.mult,
+        def score_passes(out_cols, g, r, c, a, first, width):
+            for f in range(2):
+                keys = slice(2 * P * f + P * (r % 2), 2 * P * f + P * (r % 2 + 1))
+                cols = slice(2 * P * f + first, 2 * P * f + first + width)
+                nc.tensor.matmul_mx(
+                    out=out_cols,
+                    lhsT=x_codes["k", g, r // 2][:, keys].bitcast(FP8X4),
+                    lhsT_scale=x_scales["k", g, r // 2][:, keys],
+                    rhs=x_codes["q", c, a][:, cols].bitcast(FP8X4),
+                    rhs_scale=x_scales["q", c, a][:, cols],
+                    start=(f == 0),
+                    stop=(f == 1),
                 )
-                return
+
+        def near_scores(c, b):
+            bank = new_bank(("near", c, b), score_banks)
+            for r in range(4):
+                place = 2 * (r % 2) + r // 2
+                score_passes(bank[:, P * place : P * (place + 1)], c, r, c, b // 2, P * (b % 2), P)
+
+        def far_scores(a, j):
+            bank = new_bank(("far", a, j), score_banks)
+            for e in range(2):
+                score_passes(bank[:, 2 * P * e : 2 * P * (e + 1)], 0, 2 * e + j, 1, a, 0, 2 * P)
+
+        def weigh_near(c, b):
             nc.vector.tensor_tensor(
-                out=s_two[g, c, a][:, j, 128 * lo : 128 * hi].rearrange("p (m i) e -> p m e i", i=4),
-                in0=psum["M1", g, c, b][:].rearrange("p (e m i) -> p m e i", e=2, i=4)[:, 32 * lo : 32 * hi],
-                in1=gain_view(g + c)[:, j, 64 * a + 32 * lo : 64 * a + 32 * hi],
+                out=s_words[c, c, b // 2][:, b % 2].rearrange("p (m i) t -> p m t i", i=RUN),
+                in0=psum["near", c, b][:].rearrange("p (t m i) -> p m t i", t=4, i=RUN),
+                in1=gain[2 * c][:, CHUNK * b : CHUNK * (b + 1)].rearrange("p (m t i) -> p m t i", t=4, i=RUN),
                 op=ALU.mult,
             )
 
-        def WC(g, c, b, eng, lo=0, hi=2):
-            words = s_two[g, c, b // 2][:].rearrange("p j q e -> p j (q e)").bitcast(F32)[:, :, 128 * lo : 128 * hi]
-            dst = s_bf[g, c, b // 2][:, lo:hi].rearrange("p j i t -> p (j i) t").bitcast(F32)
-            if eng == "S":
-                nc.scalar.copy(dst, words.rearrange("p j q -> p q j"))
-            else:
-                nc.vector.tensor_copy(out=dst, in_=words.rearrange("p j q -> p q j"))
-
-        def QS(g, c, b, n=2):
-            lo = b % 2 + 1 - n
-            nc.vector.quantize_mx(
-                out=s_codes[g, c, b // 2][:, 128 * lo : 128 * (lo + n)].bitcast(FP8X4),
-                scales=s_scl[g, c, b // 2][:, 128 * lo : 128 * (lo + n)],
-                in_=s_bf[g, c, b // 2][:, lo : lo + n].rearrange("p j i t -> p (j i t)"),
+        def weigh_far(a, j):
+            runs = 2 * P // RUN
+            nc.vector.tensor_tensor(
+                out=far_halves[a][:, j].rearrange("p (m i) e -> p m e i", i=RUN),
+                in0=psum["far", a, j][:].rearrange("p (e m i) -> p m e i", e=2, i=RUN),
+                in1=gain_view(FAR)[:, j, runs * a : runs * (a + 1)],
+                op=ALU.mult,
             )
 
-        def M2(c, b, h, first=0, last=1, score=False):
-            bank = new_bank(("M2", c, b, h), score) if first == 0 else psum["M2", c, b, h]
-            for g in range(first, min(c, last) + 1):
-                nc.tensor.matmul_mx(
-                    out=bank[:],
-                    lhsT=s_codes[g, c, b // 2][:, 128 * (b % 2) : 128 * (b % 2 + 1)].bitcast(FP8X4),
-                    lhsT_scale=s_scl[g, c, b // 2][:, 128 * (b % 2) : 128 * (b % 2 + 1)],
-                    rhs=v_codes[g, h][:].bitcast(FP8X4),
-                    rhs_scale=v_scl[g, h][:],
-                    start=(g == 0),
-                    stop=(g == c),
-                )
+        def join_far(a):
+            halves = far_halves[a][:].rearrange("p j n e -> p j (n e)").bitcast(F32)
+            join_halves(s_words[0, 1, a][:].rearrange("p b i t -> p (b i) t"), halves, False)
 
-        def CO(c, b, h, eng):
-            src = psum["M2", c, b, h]
-            res = result[c, b][:, 512 * h : 512 * (h + 1)]
-            if eng == "S":
-                nc.scalar.copy(res, src[:])
-            else:
-                nc.vector.tensor_copy(out=res, in_=src[:])
+        def quantise_scores(tile, a, lo=0, hi=2):
+            key = tile + (a,)
+            nc.vector.quantize_mx(
+                out=s_codes[key][:, P * lo : P * hi].bitcast(FP8X4),
+                scales=s_scales[key][:, P * lo : P * hi],
+                in_=s_words[key][:, lo:hi].rearrange("p b i t -> p (b i t)"),
+            )
 
-        def ST(c, b, lo, hi):
-            nc.sync.dma_start(out=o_rows[c][:, b, 512 * lo : 512 * hi], in_=result[c, b][:, 512 * lo : 512 * hi])
+        def mix_pass(c, b, h, g):
+            cols = slice(P * (b % 2), P * (b % 2 + 1))
+            nc.tensor.matmul_mx(
+                out=psum["mix", c, b, h][:],
+                lhsT=s_codes[g, c, b // 2][:, cols].bitcast(FP8X4),
+                lhsT_scale=s_scales[g, c, b // 2][:, cols],
+                rhs=v_codes[g, h][:].bitcast(FP8X4),
+                rhs_scale=v_scales[g, h][:],
+                start=(g == 0),
+                stop=(g == c),
+            )
 
-        nc.scalar.dma_start(out=dk[:], in_=decay.rearrange("(g p t) -> p g t", g=2, t=4))
-        nc.scalar.dma_start(out=vs[:], in_=v_scale.rearrange("o (g p t) i -> p (o g) (t i)", g=2, t=4))
-        loadv(0, 0, 2, 0, 1024)
-        load("k", 0, 0, 1)
-        loadv(0, 2, 4, 0, 1024)
-        load("k", 0, 1, 2)
-        load("k", 0, 2, 3)
-        load("k", 0, 3, 4)
-        load("q", 0, 0, 1)
-        load("q", 0, 1, 2)
-        load("q", 0, 2, 3)
-        load("q", 0, 3, 4)
-        load("q", 1, 0, 2)
-        loadv(1, 0, 4, 0, 1024)
-        load("k", 1, 0, 2)
-        load("k", 1, 2, 4)
-        load("q", 1, 2, 4)
-        nc.vector.memset(warm[:], 0.0)
-        nc.scalar.activation(out=warm_out[:], in_=warm[:], func=ACT.Exp)
-        nc.gpsimd.iota(dist[:], pattern=[[1, 516]], base=-3, channel_multiplier=-4, allow_small_or_imprecise_dtypes=True)
-        nc.vector.tensor_scalar(out=ident[:], in0=dist[:, 3:515:4], scalar1=0.0, scalar2=None, op0=ALU.is_equal)
-        nc.vector.scalar_tensor_tensor(out=near[:], in0=dist[:], scalar=-BIG, in1=dist[:], op0=ALU.mult, op1=ALU.max)
-        nc.vector.tensor_scalar(out=nd[:], in0=dk[:].rearrange("p g t -> p (g t)"), scalar1=1.0 / 2.0**90, scalar2=-1.0, op0=ALU.max, op1=ALU.mult)
-        nc.vector.tensor_scalar(out=far_bias[:], in0=nd[:, 0:4], scalar1=512.0, scalar2=LOG_SCALE, op0=ALU.mult, op1=ALU.add)
+        def mix(c, b, h):
+            new_bank(("mix", c, b, h), other_banks)
+            for g in range(c + 1):
+                mix_pass(c, b, h, g)
 
-        TR("k", 0, 0)
-        TR("k", 0, 1)
-        TR("k", 0, 2)
-        TR("k", 0, 3)
-        EX(0, 0)
-        EX(0, 2)
-        EX(0, 1)
-        EX(0, 3)
-        CP("k", 0, 0, "S")
-        EX(1, 0)
-        CP("k", 0, 1, "S")
-        CP("k", 0, 2, "S")
-        CP("k", 0, 3, "S")
-        WD(0, 0, 2, "V")
-        WD(0, 1, 2, "V")
-        WD(0, 2, 2, "V")
-        WD(0, 3, 2, "V")
-        QZ("k", 0, 1)
-        IL(0, 0, "V")
-        IL(0, 1, "V")
-        QZ("k", 0, 3)
-        TR("q", 0, 0)
-        TR("q", 0, 1)
-        TR("q", 0, 2)
-        TR("q", 0, 3)
-        CP("q", 0, 0, "S")
-        CP("q", 0, 1, "S")
-        CP("q", 0, 2, "S")
-        CP("q", 0, 3, "S")
-        EX(1, 2)
-        QZ("q", 0, 1)
-        QV(0, 0)
-        QZ("q", 0, 3)
-        QV(0, 1)
-        WD(1, 0, 2, "V")
-        TR("q", 1, 0)
-        TR("q", 1, 1)
-        M1(0, 0, 0)
-        M1(0, 0, 1)
-        TR("k", 1, 0)
-        TR("k", 1, 1)
-        M1(0, 0, 2)
-        M1(0, 0, 3)
-        CP("q", 1, 0, "S")
-        CP("q", 1, 1, "S")
-        EX(1, 1)
-        EX(1, 3)
-        EX(2, 0)
-        EX(2, 2)
-        CP("k", 1, 0, "S")
-        CP("k", 1, 1, "S")
-        EX(2, 1)
-        EX(2, 3)
-        QZ("q", 1, 1)
-        MK(0, 0, 0)
-        WD(1, 1, 2, "V")
-        MK(0, 0, 1)
-        WD(1, 2, 2, "V")
-        QS(0, 0, 1)
-        QZ("k", 1, 1)
-        MK(0, 0, 2)
-        WD(1, 3, 2, "V")
-        MK(0, 0, 3)
-        TR("k", 1, 2)
-        TR("k", 1, 3)
-        M2(0, 0, 0)
-        M2(0, 0, 1)
-        M1(0, 1, 0)
-        M1(0, 1, 1)
-        CP("k", 1, 2, "S")
-        CP("k", 1, 3, "S")
-        CO(0, 0, 0, "S")
-        CO(0, 0, 1, "S")
-        ST(0, 0, 0, 2)
-        IL(1, 0, "S")
-        QZ("k", 1, 3)
-        QS(0, 0, 3)
-        MK(0, 1, 0)
-        MK(0, 1, 1)
-        QV(1, 0)
-        WC(0, 1, 1, "V")
-        TR("q", 1, 2)
-        TR("q", 1, 3)
-        M2(0, 1, 0)
-        M2(0, 1, 1)
-        M1(1, 1, 0)
-        M1(1, 1, 1)
-        CP("q", 1, 2, "S")
-        CP("q", 1, 3, "S")
-        CO(0, 1, 0, "S")
-        CO(0, 1, 1, "S")
-        ST(0, 1, 0, 2)
-        IL(1, 1, "S")
-        QZ("q", 1, 3)
-        QS(0, 1, 1)
-        MK(1, 1, 0)
-        MK(1, 1, 1)
-        QV(1, 1)
-        QS(1, 1, 1)
-        M2(0, 2, 0)
-        M2(0, 2, 1)
-        M1(0, 1, 2)
-        M1(0, 1, 3)
-        M2(0, 3, 0)
-        M2(0, 3, 1)
-        M1(1, 1, 2)
-        CO(0, 2, 0, "S")
-        CO(0, 2, 1, "S")
-        ST(0, 2, 0, 2)
-        CO(0, 3, 0, "S")
-        CO(0, 3, 1, "S")
-        ST(0, 3, 0, 2)
-        MK(0, 1, 2)
-        MK(0, 1, 3)
-        MK(1, 1, 2)
-        WC(0, 1, 3, "V")
-        QS(1, 1, 2, 1)
-        QS(0, 1, 3)
-        M2(1, 0, 0)
-        M2(1, 0, 1)
-        M1(1, 1, 3)
-        M2(1, 1, 0)
-        M2(1, 1, 1)
-        CO(1, 0, 0, "S")
-        ST(1, 0, 0, 1)
-        CO(1, 0, 1, "S")
-        ST(1, 0, 1, 2)
-        CO(1, 1, 0, "S")
-        ST(1, 1, 0, 1)
-        CO(1, 1, 1, "S")
-        ST(1, 1, 1, 2)
-        MK(1, 1, 3)
-        QS(1, 1, 3, 1)
-        M2(1, 2, 0)
-        M2(1, 2, 1)
-        M2(1, 3, 0, 0, 0, True)
-        M2(1, 3, 1, 0, 0, True)
-        M2(1, 3, 0, 1)
-        M2(1, 3, 1, 1)
-        CO(1, 2, 0, "S")
-        ST(1, 2, 0, 1)
-        CO(1, 2, 1, "S")
-        ST(1, 2, 1, 2)
-        CO(1, 3, 0, "S")
-        ST(1, 3, 0, 1)
-        CO(1, 3, 1, "V")
-        ST(1, 3, 1, 2)
+        def store(c, b, lo, hi):
+            cols = slice(CHUNK * lo, CHUNK * hi)
+            nc.sync.dma_start(out=out_rows[c][:, b, cols], in_=result[c, b][:, cols])
+
+        def copy_result(c, b, h):
+            nc.scalar.copy(result[c, b][:, CHUNK * h : CHUNK * (h + 1)], psum["mix", c, b, h][:])
+
+        def emit_rows(b):
+            for h in range(2):
+                copy_result(0, b, h)
+            store(0, b, 0, 2)
+
+        def emit_half(b, h):
+            copy_result(1, b, h)
+            store(1, b, h, h + 1)
+
+        nc.scalar.dma_start(out=rate[:], in_=decay.rearrange("(g p r) -> p g r", g=2, r=4))
+        nc.scalar.dma_start(out=key_scale[:], in_=v_scale.rearrange("o (g p r) i -> p (o g) (r i)", g=2, r=4))
+        load_v(0, 0, 2)
+        load_rows("k", 0, 0, 1)
+        load_v(0, 2, 4)
+        for x, c, blocks in (("k", 0, range(1, 4)), ("q", 0, range(4)), ("q", 1, range(2))):
+            for b in blocks:
+                load_rows(x, c, b, b + 1)
+        load_v(1, 0, 4)
+        for x, lo in (("k", 0), ("k", 2), ("q", 2)):
+            load_rows(x, 1, lo, lo + 2)
+
+        nc.gpsimd.iota(dist[:], pattern=[[1, CHUNK + 4]], base=-3, channel_multiplier=-4, allow_small_or_imprecise_dtypes=True)
+        nc.vector.tensor_scalar(out=ident[:], in0=dist[:, 3 : 3 + CHUNK : 4], scalar1=0.0, scalar2=None, op0=ALU.is_equal)
+        nc.vector.scalar_tensor_tensor(out=causal_dist[:], in0=dist[:], scalar=-MASKED, in1=dist[:], op0=ALU.mult, op1=ALU.max)
+        nc.vector.tensor_scalar(
+            out=neg_rate[:], in0=rate[:].rearrange("p g r -> p (g r)"), scalar1=LEAST_RATE, scalar2=-1.0, op0=ALU.max, op1=ALU.mult
+        )
+        nc.vector.tensor_scalar(out=far_bias[:], in0=neg_rate[:, 0:4], scalar1=float(CHUNK), scalar2=LOG_SCALE, op0=ALU.mult, op1=ALU.add)
+
+        gains = [(tile, r) for tile in (NEAR0, FAR, NEAR1) for r in (0, 2, 1, 3)]
+
+        def make_gains(lo, hi):
+            for tile, r in gains[lo:hi]:
+                make_gain(tile, r)
+
+        make_gains(0, 4)
+        for r in range(4):
+            widen_v(0, r)
+        turn("k", 0, 0)
+        copy_turned("k", 0, 0)
+        make_gains(4, 5)
+        for b in range(1, 4):
+            turn("k", 0, b)
+            copy_turned("k", 0, b)
+        quantise_rows("k", 0, 0)
+        for h in range(2):
+            join_v(0, h)
+        quantise_rows("k", 0, 1)
+        for b in range(4):
+            turn("q", 0, b)
+            copy_turned("q", 0, b)
+        for a in range(2):
+            quantise_rows("q", 0, a)
+            quantise_v(0, a)
+        turn("q", 1, 0)
+        copy_turned("q", 1, 0)
+
+        for a, (lo, hi), behind in ((0, (5, 10), (("q", 1), ("k", 0))), (1, (10, 12), (("k", 1), ("k", 2)))):
+            for b in (2 * a, 2 * a + 1):
+                near_scores(0, b)
+            make_gains(lo, hi)
+            for x, b in behind:
+                turn(x, 1, b)
+                copy_turned(x, 1, b)
+            for b in (2 * a, 2 * a + 1):
+                widen_v(1, b)
+                weigh_near(0, b)
+            quantise_rows(behind[0][0], 1, 0)
+            quantise_scores(NEAR0, a)
+
+        for h in range(2):
+            mix(0, 0, h)
+        far_scores(0, 0)
+        emit_rows(0)
+        turn("k", 1, 3)
+        copy_turned("k", 1, 3)
+        quantise_rows("k", 1, 1)
+        turn("q", 1, 2)
+        copy_turned("q", 1, 2)
+        join_v(1, 0)
+        for h in range(2):
+            mix(0, 1, h)
+        far_scores(0, 1)
+        emit_rows(1)
+        turn("q", 1, 3)
+        copy_turned("q", 1, 3)
+        for j in range(2):
+            weigh_far(0, j)
+        quantise_v(1, 0)
+        join_far(0)
+        quantise_rows("q", 1, 1)
+        quantise_scores(FAR, 0)
+        for h in range(2):
+            mix(0, 2, h)
+        emit_rows(2)
+        for b in range(2):
+            near_scores(1, b)
+        join_v(1, 1)
+        for h in range(2):
+            mix(0, 3, h)
+        emit_rows(3)
+
+        for j in range(2):
+            far_scores(1, j)
+        for b in range(2):
+            weigh_near(1, b)
+        near_scores(1, 2)
+        weigh_far(1, 0)
+        quantise_scores(NEAR1, 0)
+        quantise_v(1, 1)
+        weigh_far(1, 1)
+        for b, h in ((0, 0), (1, 0), (0, 1)):
+            mix(1, b, h)
+            emit_half(b, h)
+        near_scores(1, 3)
+        mix(1, 1, 1)
+        emit_half(1, 1)
+        weigh_near(1, 2)
+        join_far(1)
+        quantise_scores(NEAR1, 1, 0, 1)
+        quantise_scores(FAR, 1)
+        weigh_near(1, 3)
+        quantise_scores(NEAR1, 1, 1, 2)
+        for h in range(2):
+            mix(1, 2, h)
+            emit_half(2, h)
+
+        for h in range(2):
+            new_bank(("mix", 1, 3, h), score_banks)
+            mix_pass(1, 3, h, 0)
+        for h in range(2):
+            mix_pass(1, 3, h, 1)
+        emit_half(3, 0)
+        nc.vector.tensor_copy(out=result[1, 3][:, CHUNK:], in_=psum["mix", 1, 3, 1][:])
+        store(1, 3, 1, 2)

@@ -63,6 +63,8 @@ def tile_simplifiedretnet_pa_kernel(tc, q, k, v_bytes, v_scale, decay, out):
         rate = sb("rate", [P, 2, 4], BF16)
         neg_rate = sb("neg_rate", [P, 8], F32)
         key_scale = sb("key_scale", [P, 2, 4], F32)
+        warm_in = sb("warm_in", [P, 8], F32)
+        warm_out = sb("warm_out", [P, 8], F32)
 
         raw = {}
         fp8 = {}
@@ -242,6 +244,9 @@ def tile_simplifiedretnet_pa_kernel(tc, q, k, v_bytes, v_scale, decay, out):
         load_v(1, 0, 4)
         for x, lo in (("k", 0), ("k", 2), ("q", 2)):
             load_rows(x, 1, lo, lo + 2)
+
+        nc.vector.memset(warm_in[:], 0.0)
+        nc.scalar.activation(out=warm_out[:], in_=warm_in[:], func=ACT.Exp)
 
         nc.gpsimd.iota(dist[:], pattern=[[1, CHUNK + 4]], base=-3, channel_multiplier=-4, allow_small_or_imprecise_dtypes=True)
         nc.vector.tensor_scalar(out=ident[:], in0=dist[:, 3 : 3 + CHUNK : 4], scalar1=0.0, scalar2=None, op0=ALU.is_equal)

@@ -249,12 +249,12 @@ def tile_simplifiedretnet_pa_kernel(tc, q, k, v_bytes, v_scale, decay, out):
         nc.scalar.activation(out=warm_out[:], in_=warm_in[:], func=ACT.Exp)
 
         nc.gpsimd.iota(dist[:], pattern=[[1, CHUNK + 4]], base=-3, channel_multiplier=-4, allow_small_or_imprecise_dtypes=True)
-        nc.vector.tensor_scalar(out=ident[:], in0=dist[:, 3 : 3 + CHUNK : 4], scalar1=0.0, scalar2=None, op0=ALU.is_equal)
         nc.vector.scalar_tensor_tensor(out=causal_dist[:], in0=dist[:], scalar=-MASKED, in1=dist[:], op0=ALU.mult, op1=ALU.max)
         nc.vector.tensor_scalar(
             out=neg_rate[:], in0=rate[:].rearrange("p g r -> p (g r)"), scalar1=LEAST_RATE, scalar2=-1.0, op0=ALU.max, op1=ALU.mult
         )
         nc.vector.tensor_scalar(out=far_bias[:], in0=neg_rate[:, 0:4], scalar1=float(CHUNK), scalar2=LOG_SCALE, op0=ALU.mult, op1=ALU.add)
+        nc.vector.tensor_scalar(out=ident[:], in0=dist[:, 3 : 3 + CHUNK : 4], scalar1=0.0, scalar2=None, op0=ALU.is_equal)
 
         gains = [(tile, r) for tile in (NEAR0, FAR, NEAR1) for r in (0, 2, 1, 3)]
 
@@ -284,7 +284,7 @@ def tile_simplifiedretnet_pa_kernel(tc, q, k, v_bytes, v_scale, decay, out):
         turn("q", 1, 0)
         copy_turned("q", 1, 0)
 
-        for a, (lo, hi), behind in ((0, (5, 10), (("q", 1), ("k", 0))), (1, (10, 12), (("k", 1), ("k", 2)))):
+        for a, (lo, hi), behind in ((0, (5, 10), (("q", 1), ("k", 0))), (1, (10, 12), (("k", 1), ("k", 2), ("k", 3)))):
             for b in (2 * a, 2 * a + 1):
                 near_scores(0, b)
             make_gains(lo, hi)
@@ -297,33 +297,28 @@ def tile_simplifiedretnet_pa_kernel(tc, q, k, v_bytes, v_scale, decay, out):
             quantise_rows(behind[0][0], 1, 0)
             quantise_scores(NEAR0, a)
 
+        quantise_rows("k", 1, 1)
+
         for h in range(2):
             mix(0, 0, h)
-        far_scores(0, 0)
         emit_rows(0)
-        turn("k", 1, 3)
-        copy_turned("k", 1, 3)
-        quantise_rows("k", 1, 1)
-        turn("q", 1, 2)
-        copy_turned("q", 1, 2)
         join_v(1, 0)
-        for h in range(2):
-            mix(0, 1, h)
-        far_scores(0, 1)
-        emit_rows(1)
-        turn("q", 1, 3)
-        copy_turned("q", 1, 3)
+        for j in range(2):
+            far_scores(0, j)
+        for b in range(2, 4):
+            turn("q", 1, b)
+            copy_turned("q", 1, b)
         for j in range(2):
             weigh_far(0, j)
         quantise_v(1, 0)
         join_far(0)
         quantise_rows("q", 1, 1)
         quantise_scores(FAR, 0)
-        for h in range(2):
-            mix(0, 2, h)
-        emit_rows(2)
-        for b in range(2):
-            near_scores(1, b)
+        for b in range(1, 3):
+            for h in range(2):
+                mix(0, b, h)
+            emit_rows(b)
+            near_scores(1, b - 1)
         join_v(1, 1)
         for h in range(2):
             mix(0, 3, h)

@@ -43,7 +43,7 @@ def tile_simplifiedretnet_pa_kernel(tc, q, k, v_bytes, v_scale, decay, out):
         row_pairs = [(x, c, a) for x in "qk" for c in range(2) for a in range(2)]
         v_halves = [(g, h) for g in range(2) for h in range(2)]
         score_pairs = [(g, c, a) for g, c in (NEAR0, FAR, NEAR1) for a in range(2)]
-        turned = {key: sb("turned_%s_%s_%s" % key, [P, 2, 2, P, 2], F32) for key in row_pairs}
+        turned = {key: sb("turned_%s_%s_%s" % key, [P, 4, P, 2], F32) for key in row_pairs}
         x_codes = {key: sb("x_codes_%s_%s_%s" % key, [P, 512], U32) for key in row_pairs}
         x_scales = {key: sb("x_scales_%s_%s_%s" % key, [P, 512], U8) for key in row_pairs}
         v_wide = [sb("v_wide_%s" % (g,), [P, 2, 1024, 2], BF16) for g in range(2)]
@@ -67,6 +67,7 @@ def tile_simplifiedretnet_pa_kernel(tc, q, k, v_bytes, v_scale, decay, out):
         warm_out = sb("warm_out", [P, 8], F32)
 
         raw = {}
+        halves = {}
         fp8 = {}
         psum = {}
 
@@ -75,6 +76,7 @@ def tile_simplifiedretnet_pa_kernel(tc, q, k, v_bytes, v_scale, decay, out):
             nc.sync.dma_start(out=rows[:], in_=rows_of[x][c][:, lo:hi, :])
             for b in range(lo, hi):
                 raw[x, c, b] = rows[:, b - lo, :]
+                halves[x, c, b] = raw[x, c, b].bitcast(F32).rearrange("p (f m u) -> p f u m", f=2, u=2)
 
         def load_v(g, lo, hi):
             planes = sb("fp8_%s_%s" % (g, lo), [P, hi - lo, 1024], U8)
@@ -86,25 +88,54 @@ def tile_simplifiedretnet_pa_kernel(tc, q, k, v_bytes, v_scale, decay, out):
             psum[key] = pool.tile([P, CHUNK], F32, name="bank")
             return psum[key]
 
+        def sort_words(x, c, b, engine):
+            runs = sb("sorted_%s_%s_%s" % (x, c, b), [P, 2, 2, P], F32)
+            if engine == "v":
+                nc.vector.tensor_copy(out=runs[:], in_=halves[x, c, b])
+            elif engine == "s":
+                nc.scalar.copy(runs[:], halves[x, c, b])
+            else:
+                nc.gpsimd.tensor_copy(out=runs[:], in_=halves[x, c, b])
+            halves[x, c, b] = runs
+
         def turn(x, c, b):
             bank = new_bank(("turn", x, c, b), other_banks)[:].rearrange("p (f u m) -> p f u m", f=2, u=2)
-            words = raw[x, c, b].bitcast(F32)
             for f in range(2):
                 for u in range(2):
-                    nc.tensor.transpose(bank[:, f, u, :], words[:, 256 * f + u : 256 * (f + 1) : 2], ident[:])
+                    nc.tensor.transpose(bank[:, f, u, :], halves[x, c, b][:, f, u, :], ident[:])
 
-        def copy_turned(x, c, b):
+        def slot(x, c, b, f):
+            return 2 * f + b % 2
+
+        def copy(out, in_, on_vector):
+            if on_vector:
+                nc.vector.tensor_copy(out=out, in_=in_)
+            else:
+                nc.scalar.copy(out, in_)
+
+        def copy_turned(x, c, b, on_vector=False):
             src = psum["turn", x, c, b][:].rearrange("p (f u m) -> p f m u", f=2, u=2)
-            nc.scalar.copy(turned[x, c, b // 2][:, :, b % 2], src)
+            first, second = slot(x, c, b, 0), slot(x, c, b, 1)
+            copy(turned[x, c, b // 2][:, first : second + 1 : second - first], src, on_vector)
 
-        def quantise_rows(x, c, a):
+        def quantise_rows(x, c, a, lo=0, hi=2):
+            cols = slice(2 * P * lo, 2 * P * hi)
             nc.vector.quantize_mx(
-                out=x_codes[x, c, a][:].bitcast(FP8X4),
-                scales=x_scales[x, c, a][:],
-                in_=turned[x, c, a][:].rearrange("p f b m u -> p (f b m u)").bitcast(BF16),
+                out=x_codes[x, c, a][:, cols].bitcast(FP8X4),
+                scales=x_scales[x, c, a][:, cols],
+                in_=turned[x, c, a][:, 2 * lo : 2 * hi].rearrange("p s m u -> p (s m u)").bitcast(BF16),
             )
 
-        def widen_v(g, r):
+        def quantise_block(x, c, b):
+            for f in range(2):
+                n = slot(x, c, b, f)
+                nc.vector.quantize_mx(
+                    out=x_codes[x, c, b // 2][:, P * n : P * (n + 1)].bitcast(FP8X4),
+                    scales=x_scales[x, c, b // 2][:, P * n : P * (n + 1)],
+                    in_=turned[x, c, b // 2][:, n].rearrange("p m u -> p (m u)").bitcast(BF16),
+                )
+
+        def widen_v(g, r, on_vector):
             nc.vector.tensor_scalar(
                 out=v_wide[g][:, r % 2, :, r // 2],
                 in0=fp8[g, r].bitcast(E4M3FN),
@@ -113,16 +144,12 @@ def tile_simplifiedretnet_pa_kernel(tc, q, k, v_bytes, v_scale, decay, out):
                 op0=ALU.mult,
             )
 
-        def join_halves(dst, halves, on_scalar):
-            src = halves.rearrange("p j n -> p n j")
-            if on_scalar:
-                nc.scalar.copy(dst.bitcast(F32), src)
-            else:
-                nc.vector.tensor_copy(out=dst.bitcast(F32), in_=src)
+        def join_halves(dst, pairs, on_vector):
+            copy(dst.bitcast(F32), pairs.rearrange("p j n -> p n j"), on_vector)
 
-        def join_v(g, h):
-            halves = v_wide[g][:].rearrange("p j n e -> p j (n e)").bitcast(F32)
-            join_halves(v_words[g, h][:], halves[:, :, CHUNK * h : CHUNK * (h + 1)], g == 1)
+        def join_v(g, h, on_vector):
+            pairs = v_wide[g][:].rearrange("p j n e -> p j (n e)").bitcast(F32)
+            join_halves(v_words[g, h][:], pairs[:, :, CHUNK * h : CHUNK * (h + 1)], on_vector)
 
         def quantise_v(g, h):
             nc.vector.quantize_mx(
@@ -146,10 +173,11 @@ def tile_simplifiedretnet_pa_kernel(tc, q, k, v_bytes, v_scale, decay, out):
                 scale=neg_rate[:, col : col + 1],
             )
 
-        def score_passes(out_cols, g, r, c, a, first, width):
+        def score_passes(out_cols, g, r, c, b, width):
+            a = b // 2
             for f in range(2):
-                keys = slice(2 * P * f + P * (r % 2), 2 * P * f + P * (r % 2 + 1))
-                cols = slice(2 * P * f + first, 2 * P * f + first + width)
+                keys = slice(P * slot("k", g, r, f), P * slot("k", g, r, f) + P)
+                cols = slice(P * slot("q", c, b, f), P * slot("q", c, b, f) + width)
                 nc.tensor.matmul_mx(
                     out=out_cols,
                     lhsT=x_codes["k", g, r // 2][:, keys].bitcast(FP8X4),
@@ -164,12 +192,12 @@ def tile_simplifiedretnet_pa_kernel(tc, q, k, v_bytes, v_scale, decay, out):
             bank = new_bank(("near", c, b), score_banks)
             for r in range(4):
                 place = 2 * (r % 2) + r // 2
-                score_passes(bank[:, P * place : P * (place + 1)], c, r, c, b // 2, P * (b % 2), P)
+                score_passes(bank[:, P * place : P * (place + 1)], c, r, c, b, P)
 
         def far_scores(a, j):
             bank = new_bank(("far", a, j), score_banks)
             for e in range(2):
-                score_passes(bank[:, 2 * P * e : 2 * P * (e + 1)], 0, 2 * e + j, 1, a, 0, 2 * P)
+                score_passes(bank[:, 2 * P * e : 2 * P * (e + 1)], 0, 2 * e + j, 1, 2 * a, 2 * P)
 
         def weigh_near(c, b):
             nc.vector.tensor_tensor(
@@ -188,9 +216,9 @@ def tile_simplifiedretnet_pa_kernel(tc, q, k, v_bytes, v_scale, decay, out):
                 op=ALU.mult,
             )
 
-        def join_far(a):
-            halves = far_halves[a][:].rearrange("p j n e -> p j (n e)").bitcast(F32)
-            join_halves(s_words[0, 1, a][:].rearrange("p b i t -> p (b i) t"), halves, False)
+        def join_far(a, on_vector):
+            pairs = far_halves[a][:].rearrange("p j n e -> p j (n e)").bitcast(F32)
+            join_halves(s_words[0, 1, a][:].rearrange("p b i t -> p (b i) t"), pairs, on_vector)
 
         def quantise_scores(tile, a, lo=0, hi=2):
             key = tile + (a,)
@@ -200,50 +228,70 @@ def tile_simplifiedretnet_pa_kernel(tc, q, k, v_bytes, v_scale, decay, out):
                 in_=s_words[key][:, lo:hi].rearrange("p b i t -> p (b i t)"),
             )
 
-        def mix_pass(c, b, h, g):
-            cols = slice(P * (b % 2), P * (b % 2 + 1))
+        def mix_pass(c, b, lo, width, g):
+            rows = slice(P * (b % 2), P * (b % 2 + 1))
+            h, cols = lo // CHUNK, slice(lo % CHUNK, lo % CHUNK + width)
             nc.tensor.matmul_mx(
-                out=psum["mix", c, b, h][:],
-                lhsT=s_codes[g, c, b // 2][:, cols].bitcast(FP8X4),
-                lhsT_scale=s_scales[g, c, b // 2][:, cols],
-                rhs=v_codes[g, h][:].bitcast(FP8X4),
-                rhs_scale=v_scales[g, h][:],
+                out=psum["mix", c, b, lo][:, :width],
+                lhsT=s_codes[g, c, b // 2][:, rows].bitcast(FP8X4),
+                lhsT_scale=s_scales[g, c, b // 2][:, rows],
+                rhs=v_codes[g, h][:, cols].bitcast(FP8X4),
+                rhs_scale=v_scales[g, h][:, cols],
                 start=(g == 0),
                 stop=(g == c),
             )
 
-        def mix(c, b, h):
-            new_bank(("mix", c, b, h), other_banks)
+        def mix(c, b, h, pool=other_banks):
+            new_bank(("mix", c, b, CHUNK * h), pool)
             for g in range(c + 1):
-                mix_pass(c, b, h, g)
+                mix_pass(c, b, CHUNK * h, CHUNK, g)
 
-        def store(c, b, lo, hi):
-            cols = slice(CHUNK * lo, CHUNK * hi)
-            nc.sync.dma_start(out=out_rows[c][:, b, cols], in_=result[c, b][:, cols])
+        def store(c, b, lo, width):
+            nc.sync.dma_start(out=out_rows[c][:, b, lo : lo + width], in_=result[c, b][:, lo : lo + width])
 
-        def copy_result(c, b, h):
-            nc.scalar.copy(result[c, b][:, CHUNK * h : CHUNK * (h + 1)], psum["mix", c, b, h][:])
+        def copy_result(c, b, lo, width=CHUNK, on_vector=False):
+            copy(result[c, b][:, lo : lo + width], psum["mix", c, b, lo][:, :width], on_vector)
 
         def emit_rows(b):
             for h in range(2):
-                copy_result(0, b, h)
-            store(0, b, 0, 2)
+                copy_result(0, b, CHUNK * h)
+            store(0, b, 0, 2 * CHUNK)
 
-        def emit_half(b, h):
-            copy_result(1, b, h)
-            store(1, b, h, h + 1)
+        def emit_half(c, b, h, on_vector=False):
+            copy_result(c, b, CHUNK * h, CHUNK, on_vector)
+            store(c, b, CHUNK * h, CHUNK)
+
+        def warm_tensor(x, c, b, width):
+            nc.tensor.matmul(psum["warm"][:, :width], raw[x, c, b][:, :P], raw[x, c, b][:, :width], start=True, stop=True)
+
+        def turn_copy(x, c, b, on_vector=False):
+            turn(x, c, b)
+            copy_turned(x, c, b, on_vector)
 
         nc.scalar.dma_start(out=rate[:], in_=decay.rearrange("(g p r) -> p g r", g=2, r=4))
         nc.scalar.dma_start(out=key_scale[:], in_=v_scale.rearrange("o (g p r) i -> p (o g) (r i)", g=2, r=4))
-        load_v(0, 0, 2)
+        load_v(0, 0, 1)
+        load_v(0, 1, 2)
+        load_rows("q", 0, 0, 1)
         load_rows("k", 0, 0, 1)
-        load_v(0, 2, 4)
-        for x, c, blocks in (("k", 0, range(1, 4)), ("q", 0, range(4)), ("q", 1, range(2))):
-            for b in blocks:
-                load_rows(x, c, b, b + 1)
-        load_v(1, 0, 4)
-        for x, lo in (("k", 0), ("k", 2), ("q", 2)):
-            load_rows(x, 1, lo, lo + 2)
+        load_v(0, 2, 3)
+        load_rows("k", 0, 1, 2)
+        load_v(0, 3, 4)
+        load_rows("k", 0, 2, 3)
+        load_rows("k", 0, 3, 4)
+        load_rows("q", 0, 1, 2)
+        load_rows("q", 0, 2, 3)
+        load_rows("q", 0, 3, 4)
+        load_rows("q", 1, 0, 1)
+        load_v(1, 0, 2)
+        load_rows("q", 1, 1, 2)
+        load_rows("k", 1, 0, 1)
+        load_v(1, 2, 4)
+        load_rows("k", 1, 1, 2)
+        load_rows("k", 1, 2, 3)
+        load_rows("k", 1, 3, 4)
+        load_rows("q", 1, 2, 3)
+        load_rows("q", 1, 3, 4)
 
         nc.vector.memset(warm_in[:], 0.0)
         nc.scalar.activation(out=warm_out[:], in_=warm_in[:], func=ACT.Exp)
@@ -253,7 +301,6 @@ def tile_simplifiedretnet_pa_kernel(tc, q, k, v_bytes, v_scale, decay, out):
         nc.vector.tensor_scalar(
             out=neg_rate[:], in0=rate[:].rearrange("p g r -> p (g r)"), scalar1=LEAST_RATE, scalar2=-1.0, op0=ALU.max, op1=ALU.mult
         )
-        nc.vector.tensor_scalar(out=far_bias[:], in0=neg_rate[:, 0:4], scalar1=float(CHUNK), scalar2=LOG_SCALE, op0=ALU.mult, op1=ALU.add)
         nc.vector.tensor_scalar(out=ident[:], in0=dist[:, 3 : 3 + CHUNK : 4], scalar1=0.0, scalar2=None, op0=ALU.is_equal)
 
         gains = [(tile, r) for tile in (NEAR0, FAR, NEAR1) for r in (0, 2, 1, 3)]
@@ -262,98 +309,138 @@ def tile_simplifiedretnet_pa_kernel(tc, q, k, v_bytes, v_scale, decay, out):
             for tile, r in gains[lo:hi]:
                 make_gain(tile, r)
 
-        make_gains(0, 4)
-        for r in range(4):
-            widen_v(0, r)
-        turn("k", 0, 0)
-        copy_turned("k", 0, 0)
+        make_gains(0, 1)
+        make_gains(1, 2)
+        make_gains(2, 3)
+        make_gains(3, 4)
+        widen_v(0, 0, True)
+        nc.vector.tensor_scalar(out=far_bias[:], in0=neg_rate[:, 0:4], scalar1=float(CHUNK), scalar2=LOG_SCALE, op0=ALU.mult, op1=ALU.add)
+        widen_v(0, 1, True)
+        widen_v(0, 2, True)
+        widen_v(0, 3, True)
+        turn("q", 0, 0)
+        copy_turned("q", 0, 0, False)
         make_gains(4, 5)
-        for b in range(1, 4):
-            turn("k", 0, b)
-            copy_turned("k", 0, b)
+        turn("k", 0, 0)
+        copy_turned("k", 0, 0, False)
+        make_gains(5, 6)
+        turn("k", 0, 1)
+        copy_turned("k", 0, 1, False)
+        quantise_block("q", 0, 0)
+        join_v(0, 0, True)
+        join_v(0, 1, True)
+        quantise_v(0, 0)
         quantise_rows("k", 0, 0)
-        for h in range(2):
-            join_v(0, h)
+        turn("k", 0, 2)
+        copy_turned("k", 0, 2, False)
+        turn("k", 0, 3)
+        copy_turned("k", 0, 3, False)
         quantise_rows("k", 0, 1)
-        for b in range(4):
-            turn("q", 0, b)
-            copy_turned("q", 0, b)
-        for a in range(2):
-            quantise_rows("q", 0, a)
-            quantise_v(0, a)
+        turn("q", 0, 1)
+        copy_turned("q", 0, 1, False)
+        quantise_block("q", 0, 1)
+        quantise_v(0, 1)
+        turn("q", 0, 2)
+        copy_turned("q", 0, 2, False)
+        widen_v(1, 0, True)
+        turn("q", 0, 3)
+        copy_turned("q", 0, 3, False)
         turn("q", 1, 0)
-        copy_turned("q", 1, 0)
-
-        for a, (lo, hi), behind in ((0, (5, 10), (("q", 1), ("k", 0))), (1, (10, 12), (("k", 1), ("k", 2), ("k", 3)))):
-            for b in (2 * a, 2 * a + 1):
-                near_scores(0, b)
-            make_gains(lo, hi)
-            for x, b in behind:
-                turn(x, 1, b)
-                copy_turned(x, 1, b)
-            for b in (2 * a, 2 * a + 1):
-                widen_v(1, b)
-                weigh_near(0, b)
-            quantise_rows(behind[0][0], 1, 0)
-            quantise_scores(NEAR0, a)
-
-        quantise_rows("k", 1, 1)
-
-        for h in range(2):
-            mix(0, 0, h)
+        make_gains(6, 7)
+        copy_turned("q", 1, 0, False)
+        near_scores(0, 0)
+        near_scores(0, 1)
+        quantise_rows("q", 0, 1)
+        weigh_near(0, 0)
+        widen_v(1, 1, True)
+        weigh_near(0, 1)
+        make_gains(7, 8)
+        make_gains(8, 9)
+        make_gains(9, 10)
+        make_gains(10, 11)
+        turn("q", 1, 1)
+        copy_turned("q", 1, 1, False)
+        turn("k", 1, 0)
+        copy_turned("k", 1, 0, False)
+        turn("k", 1, 1)
+        copy_turned("k", 1, 1, False)
+        widen_v(1, 2, True)
+        quantise_scores(NEAR0, 0)
+        near_scores(0, 2)
+        near_scores(0, 3)
+        weigh_near(0, 2)
+        quantise_rows("q", 1, 0)
+        widen_v(1, 3, True)
+        weigh_near(0, 3)
+        quantise_rows("k", 1, 0)
+        make_gains(11, 12)
+        turn("k", 1, 2)
+        copy_turned("k", 1, 2, False)
+        turn("k", 1, 3)
+        copy_turned("k", 1, 3, False)
+        turn("q", 1, 2)
+        copy_turned("q", 1, 2, False)
+        turn("q", 1, 3)
+        copy_turned("q", 1, 3, False)
+        mix(0, 0, 0)
+        mix(0, 0, 1)
+        far_scores(0, 0)
+        far_scores(0, 1)
         emit_rows(0)
-        join_v(1, 0)
-        for j in range(2):
-            far_scores(0, j)
-        for b in range(2, 4):
-            turn("q", 1, b)
-            copy_turned("q", 1, b)
-        for j in range(2):
-            weigh_far(0, j)
-        quantise_v(1, 0)
-        join_far(0)
+        quantise_scores(NEAR0, 1)
+        quantise_rows("k", 1, 1)
+        weigh_far(0, 0)
+        weigh_far(0, 1)
+        mix(0, 1, 0)
+        mix(0, 1, 1)
+        join_v(1, 0, False)
+        emit_rows(1)
+        join_v(1, 1, False)
+        mix(0, 2, 0)
+        mix(0, 2, 1)
+        near_scores(1, 0)
         quantise_rows("q", 1, 1)
+        join_far(0, True)
+        quantise_v(1, 0)
         quantise_scores(FAR, 0)
-        for b in range(1, 3):
-            for h in range(2):
-                mix(0, b, h)
-            emit_rows(b)
-            near_scores(1, b - 1)
-        join_v(1, 1)
-        for h in range(2):
-            mix(0, 3, h)
+        emit_rows(2)
+        near_scores(1, 1)
+        weigh_near(1, 0)
+        weigh_near(1, 1)
+        mix(0, 3, 0)
+        mix(0, 3, 1)
+        far_scores(1, 0)
+        far_scores(1, 1)
         emit_rows(3)
-
-        for j in range(2):
-            far_scores(1, j)
-        for b in range(2):
-            weigh_near(1, b)
-        near_scores(1, 2)
         weigh_far(1, 0)
         quantise_scores(NEAR1, 0)
         quantise_v(1, 1)
         weigh_far(1, 1)
-        for b, h in ((0, 0), (1, 0), (0, 1)):
-            mix(1, b, h)
-            emit_half(b, h)
+        near_scores(1, 2)
+        mix(1, 0, 0)
+        emit_half(1, 0, 0, False)
+        mix(1, 1, 0)
+        emit_half(1, 1, 0, False)
+        mix(1, 0, 1)
+        emit_half(1, 0, 1, False)
         near_scores(1, 3)
         mix(1, 1, 1)
-        emit_half(1, 1)
+        emit_half(1, 1, 1, False)
         weigh_near(1, 2)
-        join_far(1)
+        join_far(1, True)
         quantise_scores(NEAR1, 1, 0, 1)
         quantise_scores(FAR, 1)
         weigh_near(1, 3)
         quantise_scores(NEAR1, 1, 1, 2)
-        for h in range(2):
-            mix(1, 2, h)
-            emit_half(2, h)
-
-        for h in range(2):
-            new_bank(("mix", 1, 3, h), score_banks)
-            mix_pass(1, 3, h, 0)
-        for h in range(2):
-            mix_pass(1, 3, h, 1)
-        emit_half(3, 0)
-        nc.vector.tensor_copy(out=result[1, 3][:, CHUNK:], in_=psum["mix", 1, 3, 1][:])
-        store(1, 3, 1, 2)
+        mix(1, 2, 0)
+        emit_half(1, 2, 0, False)
+        mix(1, 2, 1)
+        emit_half(1, 2, 1, False)
+        new_bank(("mix", 1, 3, CHUNK * 0), score_banks)
+        mix_pass(1, 3, CHUNK * 0, CHUNK, 0)
+        new_bank(("mix", 1, 3, CHUNK * 1), score_banks)
+        mix_pass(1, 3, CHUNK * 1, CHUNK, 0)
+        mix_pass(1, 3, CHUNK * 0, CHUNK, 1)
+        mix_pass(1, 3, CHUNK * 1, CHUNK, 1)
+        emit_half(1, 3, 0, False)
+        emit_half(1, 3, 1, True)

@@ -159,7 +159,7 @@ def tile_simplifiedretnet_pa_kernel(tc, q, k, v_bytes, v_scale, decay, out):
             )
 
         def gain_view(tile):
-            order = "p (j m e i) -> p j m e i" if tile == FAR else "p (m j e i) -> p j m e i"
+            order = "p (j m e i) -> p j m e i" if tile == FAR else "p (j e m i) -> p j m e i"
             return gain[sum(tile)][:].rearrange(order, j=2, e=2, i=RUN)
 
         def make_gain(tile, r):
@@ -201,9 +201,9 @@ def tile_simplifiedretnet_pa_kernel(tc, q, k, v_bytes, v_scale, decay, out):
 
         def weigh_near(c, b):
             nc.vector.tensor_tensor(
-                out=s_words[c, c, b // 2][:, b % 2].rearrange("p (m i) t -> p m t i", i=RUN),
-                in0=psum["near", c, b][:].rearrange("p (t m i) -> p m t i", t=4, i=RUN),
-                in1=gain[2 * c][:, CHUNK * b : CHUNK * (b + 1)].rearrange("p (m t i) -> p m t i", t=4, i=RUN),
+                out=s_words[c, c, b // 2][:, b % 2].rearrange("p (m i) t -> p m t i", i=2),
+                in0=psum["near", c, b][:].rearrange("p (t m i) -> p m t i", t=4, i=2),
+                in1=gain[2 * c][:].rearrange("p (t b m i) -> p b m t i", t=4, b=4, i=2)[:, b],
                 op=ALU.mult,
             )
 

@@ -60,9 +60,9 @@ def tile_simplifiedretnet_pa_kernel(tc, q, k, v_bytes, v_scale, decay, out):
         dist = sb("dist", [P, CHUNK + 4], F32)
         causal_dist = sb("causal_dist", [P, CHUNK + 4], F32)
         far_bias = sb("far_bias", [P, 4], F32)
-        rate = sb("rate", [P, 2, 4], BF16)
-        neg_rate = sb("neg_rate", [P, 8], F32)
-        key_scale = sb("key_scale", [P, 2, 4], F32)
+        rate = [sb("rate_%s" % (g,), [P, 4], BF16) for g in range(2)]
+        neg_rate = [sb("neg_rate_%s" % (g,), [P, 4], F32) for g in range(2)]
+        key_scale = [sb("key_scale_%s" % (g,), [P, 4], F32) for g in range(2)]
         warm_in = sb("warm_in", [P, 8], F32)
         warm_out = sb("warm_out", [P, 8], F32)
 
@@ -83,6 +83,13 @@ def tile_simplifiedretnet_pa_kernel(tc, q, k, v_bytes, v_scale, decay, out):
             nc.sync.dma_start(out=planes[:], in_=v_planes[g][:, lo:hi, :])
             for r in range(lo, hi):
                 fp8[g, r] = planes[:, r - lo, :]
+
+        def load_key_values(g, rate_queue):
+            rate_queue.dma_start(out=rate[g][:], in_=decay.rearrange("(g p r) -> g p r", g=2, r=4)[g])
+            nc.sync.dma_start(out=key_scale[g][:], in_=v_scale.rearrange("o (g p r) i -> (o g) p (r i)", g=2, r=4)[g])
+
+        def negate_rate(g):
+            nc.scalar.activation(out=neg_rate[g][:], in_=rate[g][:], func=ACT.Copy, scale=-1.0, bias=-LEAST_RATE)
 
         def new_bank(key, pool):
             psum[key] = pool.tile([P, CHUNK], F32, name="bank")
@@ -139,7 +146,7 @@ def tile_simplifiedretnet_pa_kernel(tc, q, k, v_bytes, v_scale, decay, out):
             nc.vector.tensor_scalar(
                 out=v_wide[g][:, r % 2, :, r // 2],
                 in0=fp8[g, r].bitcast(E4M3FN),
-                scalar1=key_scale[:, g, r : r + 1],
+                scalar1=key_scale[g][:, r : r + 1],
                 scalar2=None,
                 op0=ALU.mult,
             )
@@ -164,13 +171,12 @@ def tile_simplifiedretnet_pa_kernel(tc, q, k, v_bytes, v_scale, decay, out):
 
         def make_gain(tile, r):
             table = dist if tile == FAR else causal_dist
-            col = 4 * tile[0] + r
             nc.scalar.activation(
                 out=gain_view(tile)[:, r % 2, :, r // 2, :],
                 in_=table[:, 3 - r : 3 - r + CHUNK].rearrange("p (m i) -> p m i", i=RUN),
                 func=ACT.Exp,
                 bias=far_bias[:, r : r + 1] if tile == FAR else LOG_SCALE,
-                scale=neg_rate[:, col : col + 1],
+                scale=neg_rate[tile[0]][:, r : r + 1],
             )
 
         def score_passes(out_cols, g, r, c, b, width):
@@ -268,8 +274,7 @@ def tile_simplifiedretnet_pa_kernel(tc, q, k, v_bytes, v_scale, decay, out):
             turn(x, c, b)
             copy_turned(x, c, b, on_vector)
 
-        nc.scalar.dma_start(out=rate[:], in_=decay.rearrange("(g p r) -> p g r", g=2, r=4))
-        nc.scalar.dma_start(out=key_scale[:], in_=v_scale.rearrange("o (g p r) i -> p (o g) (r i)", g=2, r=4))
+        load_key_values(0, nc.scalar)
         load_v(0, 0, 1)
         load_v(0, 1, 2)
         load_rows("q", 0, 0, 1)
@@ -284,6 +289,7 @@ def tile_simplifiedretnet_pa_kernel(tc, q, k, v_bytes, v_scale, decay, out):
         load_rows("q", 0, 3, 4)
         load_rows("q", 1, 0, 1)
         load_v(1, 0, 2)
+        load_key_values(1, nc.sync)
         load_rows("q", 1, 1, 2)
         load_rows("k", 1, 0, 1)
         load_v(1, 2, 4)
@@ -298,9 +304,8 @@ def tile_simplifiedretnet_pa_kernel(tc, q, k, v_bytes, v_scale, decay, out):
 
         nc.gpsimd.iota(dist[:], pattern=[[1, CHUNK + 4]], base=-3, channel_multiplier=-4, allow_small_or_imprecise_dtypes=True)
         nc.vector.scalar_tensor_tensor(out=causal_dist[:], in0=dist[:], scalar=-MASKED, in1=dist[:], op0=ALU.mult, op1=ALU.max)
-        nc.vector.tensor_scalar(
-            out=neg_rate[:], in0=rate[:].rearrange("p g r -> p (g r)"), scalar1=LEAST_RATE, scalar2=-1.0, op0=ALU.max, op1=ALU.mult
-        )
+        negate_rate(0)
+        nc.scalar.activation(out=far_bias[:], in_=rate[0][:], func=ACT.Copy, scale=-float(CHUNK), bias=LOG_SCALE)
         nc.vector.tensor_scalar(out=ident[:], in0=dist[:, 3 : 3 + CHUNK : 4], scalar1=0.0, scalar2=None, op0=ALU.is_equal)
 
         gains = [(tile, r) for tile in (NEAR0, FAR, NEAR1) for r in (0, 2, 1, 3)]
@@ -314,7 +319,6 @@ def tile_simplifiedretnet_pa_kernel(tc, q, k, v_bytes, v_scale, decay, out):
         make_gains(2, 3)
         make_gains(3, 4)
         widen_v(0, 0, True)
-        nc.vector.tensor_scalar(out=far_bias[:], in0=neg_rate[:, 0:4], scalar1=float(CHUNK), scalar2=LOG_SCALE, op0=ALU.mult, op1=ALU.add)
         widen_v(0, 1, True)
         widen_v(0, 2, True)
         widen_v(0, 3, True)
@@ -346,6 +350,7 @@ def tile_simplifiedretnet_pa_kernel(tc, q, k, v_bytes, v_scale, decay, out):
         turn("q", 0, 3)
         copy_turned("q", 0, 3, False)
         turn("q", 1, 0)
+        negate_rate(1)
         make_gains(6, 7)
         copy_turned("q", 1, 0, False)
         near_scores(0, 0)

@@ -84,9 +84,11 @@ def tile_simplifiedretnet_pa_kernel(tc, q, k, v_bytes, v_scale, decay, out):
             for r in range(lo, hi):
                 fp8[g, r] = planes[:, r - lo, :]
 
-        def load_key_values(g, rate_queue):
-            rate_queue.dma_start(out=rate[g][:], in_=decay.rearrange("(g p r) -> g p r", g=2, r=4)[g])
-            nc.sync.dma_start(out=key_scale[g][:], in_=v_scale.rearrange("o (g p r) i -> (o g) p (r i)", g=2, r=4)[g])
+        def load_rate(g, queue):
+            queue.dma_start(out=rate[g][:], in_=decay.rearrange("(g p r) -> g p r", g=2, r=4)[g])
+
+        def load_scale(g, queue):
+            queue.dma_start(out=key_scale[g][:], in_=v_scale.rearrange("o (g p r) i -> (o g) p (r i)", g=2, r=4)[g])
 
         def negate_rate(g):
             nc.scalar.activation(out=neg_rate[g][:], in_=rate[g][:], func=ACT.Copy, scale=-1.0, bias=-LEAST_RATE)
@@ -274,7 +276,8 @@ def tile_simplifiedretnet_pa_kernel(tc, q, k, v_bytes, v_scale, decay, out):
             turn(x, c, b)
             copy_turned(x, c, b, on_vector)
 
-        load_key_values(0, nc.scalar)
+        load_rate(0, nc.scalar)
+        load_scale(0, nc.sync)
         load_v(0, 0, 1)
         load_v(0, 1, 2)
         load_rows("q", 0, 0, 1)
@@ -289,7 +292,8 @@ def tile_simplifiedretnet_pa_kernel(tc, q, k, v_bytes, v_scale, decay, out):
         load_rows("q", 0, 3, 4)
         load_rows("q", 1, 0, 1)
         load_v(1, 0, 2)
-        load_key_values(1, nc.sync)
+        load_rate(1, nc.sync)
+        load_scale(1, nc.sync)
         load_rows("q", 1, 1, 2)
         load_rows("k", 1, 0, 1)
         load_v(1, 2, 4)
@@ -441,11 +445,23 @@ def tile_simplifiedretnet_pa_kernel(tc, q, k, v_bytes, v_scale, decay, out):
         emit_half(1, 2, 0, False)
         mix(1, 2, 1)
         emit_half(1, 2, 1, False)
-        new_bank(("mix", 1, 3, CHUNK * 0), score_banks)
-        mix_pass(1, 3, CHUNK * 0, CHUNK, 0)
-        new_bank(("mix", 1, 3, CHUNK * 1), score_banks)
-        mix_pass(1, 3, CHUNK * 1, CHUNK, 0)
-        mix_pass(1, 3, CHUNK * 0, CHUNK, 1)
-        mix_pass(1, 3, CHUNK * 1, CHUNK, 1)
-        emit_half(1, 3, 0, False)
-        emit_half(1, 3, 1, True)
+        new_bank(("mix", 1, 3, 256 * 0), score_banks)
+        mix_pass(1, 3, 256 * 0, 256, 0)
+        new_bank(("mix", 1, 3, 256 * 1), score_banks)
+        mix_pass(1, 3, 256 * 1, 256, 0)
+        new_bank(("mix", 1, 3, 256 * 2), score_banks)
+        mix_pass(1, 3, 256 * 2, 256, 0)
+        new_bank(("mix", 1, 3, 256 * 3), score_banks)
+        mix_pass(1, 3, 256 * 3, 256, 0)
+        mix_pass(1, 3, 256 * 0, 256, 1)
+        mix_pass(1, 3, 256 * 1, 256, 1)
+        mix_pass(1, 3, 256 * 2, 256, 1)
+        mix_pass(1, 3, 256 * 3, 256, 1)
+        copy_result(1, 3, 256 * 0, 256, False)
+        store(1, 3, 256 * 0, 256)
+        copy_result(1, 3, 256 * 1, 256, True)
+        store(1, 3, 256 * 1, 256)
+        copy_result(1, 3, 256 * 2, 256, False)
+        store(1, 3, 256 * 2, 256)
+        copy_result(1, 3, 256 * 3, 256, True)
+        store(1, 3, 256 * 3, 256)

@@ -15,6 +15,7 @@ ACT = mybir.ActivationFunctionType
 FLOPS = 2 * 1024 * (512 * 512 + 512 * 1024) * 2
 P = 128
 CHUNK = 512
+QUARTER = 256
 RUN = 4
 MASKED = 2.0**100
 LEAST_RATE = 2.0**-90
@@ -52,7 +53,7 @@ def tile_simplifiedretnet_pa_kernel(tc, q, k, v_bytes, v_scale, decay, out):
         v_scales = {key: sb("v_scales_%s_%s" % key, [P, CHUNK], U8) for key in v_halves}
         gain = [sb("gain_%s" % (table,), [P, 4 * CHUNK], F32) for table in range(3)]
         s_words = {key: sb("s_words_%s_%s_%s" % key, [P, 2, P, 4], BF16) for key in score_pairs}
-        far_halves = [sb("far_halves_%s" % (a,), [P, 2, 2 * P, 2], BF16) for a in range(2)]
+        wide_halves = sb("wide_halves", [P, 2, 2 * P, 2], BF16)
         s_codes = {key: sb("s_codes_%s_%s_%s" % key, [P, 2 * P], U32) for key in score_pairs}
         s_scales = {key: sb("s_scales_%s_%s_%s" % key, [P, 2 * P], U8) for key in score_pairs}
         result = {(c, b): sb("result_%s_%s" % (c, b), [P, 1024], F32) for c in range(2) for b in range(4)}
@@ -66,17 +67,14 @@ def tile_simplifiedretnet_pa_kernel(tc, q, k, v_bytes, v_scale, decay, out):
         warm_in = sb("warm_in", [P, 8], F32)
         warm_out = sb("warm_out", [P, 8], F32)
 
-        raw = {}
-        halves = {}
+        words = {}
         fp8 = {}
         psum = {}
 
-        def load_rows(x, c, lo, hi):
-            rows = sb("raw_%s_%s_%s" % (x, c, lo), [P, hi - lo, 1024], BF16)
-            nc.sync.dma_start(out=rows[:], in_=rows_of[x][c][:, lo:hi, :])
-            for b in range(lo, hi):
-                raw[x, c, b] = rows[:, b - lo, :]
-                halves[x, c, b] = raw[x, c, b].bitcast(F32).rearrange("p (f m u) -> p f u m", f=2, u=2)
+        def load_rows(x, c, b):
+            rows = sb("raw_%s_%s_%s" % (x, c, b), [P, 1024], BF16)
+            nc.sync.dma_start(out=rows[:], in_=rows_of[x][c][:, b, :])
+            words[x, c, b] = rows[:].bitcast(F32).rearrange("p (f m u) -> p f u m", f=2, u=2)
 
         def load_v(g, lo, hi):
             planes = sb("fp8_%s_%s" % (g, lo), [P, hi - lo, 1024], U8)
@@ -87,8 +85,8 @@ def tile_simplifiedretnet_pa_kernel(tc, q, k, v_bytes, v_scale, decay, out):
         def load_rate(g, queue):
             queue.dma_start(out=rate[g][:], in_=decay.rearrange("(g p r) -> g p r", g=2, r=4)[g])
 
-        def load_scale(g, queue):
-            queue.dma_start(out=key_scale[g][:], in_=v_scale.rearrange("o (g p r) i -> (o g) p (r i)", g=2, r=4)[g])
+        def load_scale(g):
+            nc.sync.dma_start(out=key_scale[g][:], in_=v_scale.rearrange("o (g p r) i -> (o g) p (r i)", g=2, r=4)[g])
 
         def negate_rate(g):
             nc.scalar.activation(out=neg_rate[g][:], in_=rate[g][:], func=ACT.Copy, scale=-1.0, bias=-LEAST_RATE)
@@ -97,23 +95,13 @@ def tile_simplifiedretnet_pa_kernel(tc, q, k, v_bytes, v_scale, decay, out):
             psum[key] = pool.tile([P, CHUNK], F32, name="bank")
             return psum[key]
 
-        def sort_words(x, c, b, engine):
-            runs = sb("sorted_%s_%s_%s" % (x, c, b), [P, 2, 2, P], F32)
-            if engine == "v":
-                nc.vector.tensor_copy(out=runs[:], in_=halves[x, c, b])
-            elif engine == "s":
-                nc.scalar.copy(runs[:], halves[x, c, b])
-            else:
-                nc.gpsimd.tensor_copy(out=runs[:], in_=halves[x, c, b])
-            halves[x, c, b] = runs
-
         def turn(x, c, b):
             bank = new_bank(("turn", x, c, b), other_banks)[:].rearrange("p (f u m) -> p f u m", f=2, u=2)
             for f in range(2):
                 for u in range(2):
-                    nc.tensor.transpose(bank[:, f, u, :], halves[x, c, b][:, f, u, :], ident[:])
+                    nc.tensor.transpose(bank[:, f, u, :], words[x, c, b][:, f, u, :], ident[:])
 
-        def slot(x, c, b, f):
+        def slot(b, f):
             return 2 * f + b % 2
 
         def copy(out, in_, on_vector):
@@ -122,29 +110,27 @@ def tile_simplifiedretnet_pa_kernel(tc, q, k, v_bytes, v_scale, decay, out):
             else:
                 nc.scalar.copy(out, in_)
 
-        def copy_turned(x, c, b, on_vector=False):
+        def copy_turned(x, c, b):
             src = psum["turn", x, c, b][:].rearrange("p (f u m) -> p f m u", f=2, u=2)
-            first, second = slot(x, c, b, 0), slot(x, c, b, 1)
-            copy(turned[x, c, b // 2][:, first : second + 1 : second - first], src, on_vector)
+            nc.scalar.copy(turned[x, c, b // 2][:, b % 2 :: 2], src)
 
-        def quantise_rows(x, c, a, lo=0, hi=2):
-            cols = slice(2 * P * lo, 2 * P * hi)
+        def quantise_rows(x, c, a):
             nc.vector.quantize_mx(
-                out=x_codes[x, c, a][:, cols].bitcast(FP8X4),
-                scales=x_scales[x, c, a][:, cols],
-                in_=turned[x, c, a][:, 2 * lo : 2 * hi].rearrange("p s m u -> p (s m u)").bitcast(BF16),
+                out=x_codes[x, c, a][:].bitcast(FP8X4),
+                scales=x_scales[x, c, a][:],
+                in_=turned[x, c, a][:].rearrange("p s m u -> p (s m u)").bitcast(BF16),
             )
 
         def quantise_block(x, c, b):
             for f in range(2):
-                n = slot(x, c, b, f)
+                n = slot(b, f)
                 nc.vector.quantize_mx(
                     out=x_codes[x, c, b // 2][:, P * n : P * (n + 1)].bitcast(FP8X4),
                     scales=x_scales[x, c, b // 2][:, P * n : P * (n + 1)],
                     in_=turned[x, c, b // 2][:, n].rearrange("p m u -> p (m u)").bitcast(BF16),
                 )
 
-        def widen_v(g, r, on_vector):
+        def widen_v(g, r):
             nc.vector.tensor_scalar(
                 out=v_wide[g][:, r % 2, :, r // 2],
                 in0=fp8[g, r].bitcast(E4M3FN),
@@ -167,15 +153,14 @@ def tile_simplifiedretnet_pa_kernel(tc, q, k, v_bytes, v_scale, decay, out):
                 in_=v_words[g, h][:].rearrange("p n t -> p (n t)"),
             )
 
-        def gain_view(tile):
-            order = "p (j m e i) -> p j m e i" if tile == FAR else "p (j e m i) -> p j m e i"
-            return gain[sum(tile)][:].rearrange(order, j=2, e=2, i=RUN)
+        def place(r):
+            return 2 * (r % 2) + r // 2
 
         def make_gain(tile, r):
             table = dist if tile == FAR else causal_dist
             nc.scalar.activation(
-                out=gain_view(tile)[:, r % 2, :, r // 2, :],
-                in_=table[:, 3 - r : 3 - r + CHUNK].rearrange("p (m i) -> p m i", i=RUN),
+                out=gain[sum(tile)][:, CHUNK * place(r) : CHUNK * (place(r) + 1)],
+                in_=table[:, 3 - r : 3 - r + CHUNK],
                 func=ACT.Exp,
                 bias=far_bias[:, r : r + 1] if tile == FAR else LOG_SCALE,
                 scale=neg_rate[tile[0]][:, r : r + 1],
@@ -184,8 +169,8 @@ def tile_simplifiedretnet_pa_kernel(tc, q, k, v_bytes, v_scale, decay, out):
         def score_passes(out_cols, g, r, c, b, width):
             a = b // 2
             for f in range(2):
-                keys = slice(P * slot("k", g, r, f), P * slot("k", g, r, f) + P)
-                cols = slice(P * slot("q", c, b, f), P * slot("q", c, b, f) + width)
+                keys = slice(P * slot(r, f), P * slot(r, f) + P)
+                cols = slice(P * slot(b, f), P * slot(b, f) + width)
                 nc.tensor.matmul_mx(
                     out=out_cols,
                     lhsT=x_codes["k", g, r // 2][:, keys].bitcast(FP8X4),
@@ -196,37 +181,35 @@ def tile_simplifiedretnet_pa_kernel(tc, q, k, v_bytes, v_scale, decay, out):
                     stop=(f == 1),
                 )
 
-        def near_scores(c, b):
-            bank = new_bank(("near", c, b), score_banks)
+        def block_scores(tile, b):
+            bank = new_bank(("scores", tile, b), score_banks)
             for r in range(4):
-                place = 2 * (r % 2) + r // 2
-                score_passes(bank[:, P * place : P * (place + 1)], c, r, c, b, P)
+                score_passes(bank[:, P * place(r) : P * (place(r) + 1)], tile[0], r, tile[1], b, P)
 
-        def far_scores(a, j):
-            bank = new_bank(("far", a, j), score_banks)
+        def wide_scores(j):
+            bank = new_bank(("wide", j), score_banks)
             for e in range(2):
-                score_passes(bank[:, 2 * P * e : 2 * P * (e + 1)], 0, 2 * e + j, 1, 2 * a, 2 * P)
+                score_passes(bank[:, 2 * P * e : 2 * P * (e + 1)], 0, 2 * e + j, 1, 2, 2 * P)
 
-        def weigh_near(c, b):
+        def weigh_block(tile, b):
             nc.vector.tensor_tensor(
-                out=s_words[c, c, b // 2][:, b % 2].rearrange("p (m i) t -> p m t i", i=2),
-                in0=psum["near", c, b][:].rearrange("p (t m i) -> p m t i", t=4, i=2),
-                in1=gain[2 * c][:].rearrange("p (t b m i) -> p b m t i", t=4, b=4, i=2)[:, b],
+                out=s_words[tile + (b // 2,)][:, b % 2].rearrange("p (m i) t -> p m t i", i=2),
+                in0=psum["scores", tile, b][:].rearrange("p (t m i) -> p m t i", t=4, i=2),
+                in1=gain[sum(tile)][:].rearrange("p (t b m i) -> p b m t i", t=4, b=4, i=2)[:, b],
                 op=ALU.mult,
             )
 
-        def weigh_far(a, j):
-            runs = 2 * P // RUN
+        def weigh_wide(j):
             nc.vector.tensor_tensor(
-                out=far_halves[a][:, j].rearrange("p (m i) e -> p m e i", i=RUN),
-                in0=psum["far", a, j][:].rearrange("p (e m i) -> p m e i", e=2, i=RUN),
-                in1=gain_view(FAR)[:, j, runs * a : runs * (a + 1)],
+                out=wide_halves[:, j].rearrange("p (m i) e -> p m e i", i=RUN),
+                in0=psum["wide", j][:].rearrange("p (e m i) -> p m e i", e=2, i=RUN),
+                in1=gain[sum(FAR)][:].rearrange("p (j e a m i) -> p j a m e i", j=2, e=2, a=2, i=RUN)[:, j, 1],
                 op=ALU.mult,
             )
 
-        def join_far(a, on_vector):
-            pairs = far_halves[a][:].rearrange("p j n e -> p j (n e)").bitcast(F32)
-            join_halves(s_words[0, 1, a][:].rearrange("p b i t -> p (b i) t"), pairs, on_vector)
+        def join_wide():
+            pairs = wide_halves[:].rearrange("p j n e -> p j (n e)").bitcast(F32)
+            join_halves(s_words[FAR + (1,)][:].rearrange("p b i t -> p (b i) t"), pairs, on_vector=True)
 
         def quantise_scores(tile, a, lo=0, hi=2):
             key = tile + (a,)
@@ -265,51 +248,41 @@ def tile_simplifiedretnet_pa_kernel(tc, q, k, v_bytes, v_scale, decay, out):
                 copy_result(0, b, CHUNK * h)
             store(0, b, 0, 2 * CHUNK)
 
-        def emit_half(c, b, h, on_vector=False):
-            copy_result(c, b, CHUNK * h, CHUNK, on_vector)
-            store(c, b, CHUNK * h, CHUNK)
+        def mix_and_emit(b, h):
+            mix(1, b, h)
+            copy_result(1, b, CHUNK * h)
+            store(1, b, CHUNK * h, CHUNK)
 
-        def warm_tensor(x, c, b, width):
-            nc.tensor.matmul(psum["warm"][:, :width], raw[x, c, b][:, :P], raw[x, c, b][:, :width], start=True, stop=True)
-
-        def turn_copy(x, c, b, on_vector=False):
+        def turn_copy(x, c, b):
             turn(x, c, b)
-            copy_turned(x, c, b, on_vector)
+            copy_turned(x, c, b)
 
         load_rate(0, nc.scalar)
-        load_scale(0, nc.sync)
-        load_v(0, 0, 1)
-        load_v(0, 1, 2)
-        load_rows("q", 0, 0, 1)
-        load_rows("k", 0, 0, 1)
-        load_v(0, 2, 3)
-        load_rows("k", 0, 1, 2)
-        load_v(0, 3, 4)
-        load_rows("k", 0, 2, 3)
-        load_rows("k", 0, 3, 4)
-        load_rows("q", 0, 1, 2)
-        load_rows("q", 0, 2, 3)
-        load_rows("q", 0, 3, 4)
-        load_rows("q", 1, 0, 1)
+        load_scale(0)
+        for r in range(2):
+            load_v(0, r, r + 1)
+        load_rows("q", 0, 0)
+        for r in range(2):
+            load_rows("k", 0, r)
+            load_v(0, 2 + r, 3 + r)
+        for x, c, b in [("k", 0, 2), ("k", 0, 3), ("q", 0, 1), ("q", 0, 2), ("q", 0, 3), ("q", 1, 0)]:
+            load_rows(x, c, b)
         load_v(1, 0, 2)
         load_rate(1, nc.sync)
-        load_scale(1, nc.sync)
-        load_rows("q", 1, 1, 2)
-        load_rows("k", 1, 0, 1)
+        load_scale(1)
+        load_rows("q", 1, 1)
+        load_rows("k", 1, 0)
         load_v(1, 2, 4)
-        load_rows("k", 1, 1, 2)
-        load_rows("k", 1, 2, 3)
-        load_rows("k", 1, 3, 4)
-        load_rows("q", 1, 2, 3)
-        load_rows("q", 1, 3, 4)
+        for x, b in [("k", 1), ("k", 2), ("k", 3), ("q", 2), ("q", 3)]:
+            load_rows(x, 1, b)
 
         nc.vector.memset(warm_in[:], 0.0)
         nc.scalar.activation(out=warm_out[:], in_=warm_in[:], func=ACT.Exp)
 
         nc.gpsimd.iota(dist[:], pattern=[[1, CHUNK + 4]], base=-3, channel_multiplier=-4, allow_small_or_imprecise_dtypes=True)
-        nc.vector.scalar_tensor_tensor(out=causal_dist[:], in0=dist[:], scalar=-MASKED, in1=dist[:], op0=ALU.mult, op1=ALU.max)
         negate_rate(0)
         nc.scalar.activation(out=far_bias[:], in_=rate[0][:], func=ACT.Copy, scale=-float(CHUNK), bias=LOG_SCALE)
+        nc.vector.scalar_tensor_tensor(out=causal_dist[:], in0=dist[:], scalar=-MASKED, in1=dist[:], op0=ALU.mult, op1=ALU.max)
         nc.vector.tensor_scalar(out=ident[:], in0=dist[:, 3 : 3 + CHUNK : 4], scalar1=0.0, scalar2=None, op0=ALU.is_equal)
 
         gains = [(tile, r) for tile in (NEAR0, FAR, NEAR1) for r in (0, 2, 1, 3)]
@@ -318,150 +291,109 @@ def tile_simplifiedretnet_pa_kernel(tc, q, k, v_bytes, v_scale, decay, out):
             for tile, r in gains[lo:hi]:
                 make_gain(tile, r)
 
-        make_gains(0, 1)
-        make_gains(1, 2)
-        make_gains(2, 3)
-        make_gains(3, 4)
-        widen_v(0, 0, True)
-        widen_v(0, 1, True)
-        widen_v(0, 2, True)
-        widen_v(0, 3, True)
-        turn("q", 0, 0)
-        copy_turned("q", 0, 0, False)
+        make_gains(0, 4)
+        for r in range(4):
+            widen_v(0, r)
+        turn_copy("q", 0, 0)
         make_gains(4, 5)
-        turn("k", 0, 0)
-        copy_turned("k", 0, 0, False)
-        make_gains(5, 6)
-        turn("k", 0, 1)
-        copy_turned("k", 0, 1, False)
         quantise_block("q", 0, 0)
-        join_v(0, 0, True)
-        join_v(0, 1, True)
+        for h in range(2):
+            join_v(0, h, on_vector=True)
         quantise_v(0, 0)
-        quantise_rows("k", 0, 0)
-        turn("k", 0, 2)
-        copy_turned("k", 0, 2, False)
-        turn("k", 0, 3)
-        copy_turned("k", 0, 3, False)
-        quantise_rows("k", 0, 1)
-        turn("q", 0, 1)
-        copy_turned("q", 0, 1, False)
+        for a in range(2):
+            for r in range(2 * a, 2 * a + 2):
+                turn_copy("k", 0, r)
+            quantise_rows("k", 0, a)
+        turn_copy("q", 0, 1)
         quantise_block("q", 0, 1)
         quantise_v(0, 1)
-        turn("q", 0, 2)
-        copy_turned("q", 0, 2, False)
-        widen_v(1, 0, True)
-        turn("q", 0, 3)
-        copy_turned("q", 0, 3, False)
+        for b in range(2, 4):
+            turn_copy("q", 0, b)
         turn("q", 1, 0)
         negate_rate(1)
-        make_gains(6, 7)
-        copy_turned("q", 1, 0, False)
-        near_scores(0, 0)
-        near_scores(0, 1)
+        make_gains(5, 6)
+        copy_turned("q", 1, 0)
+
+        block_scores(NEAR0, 0)
+        block_scores(NEAR0, 1)
+        widen_v(1, 0)
         quantise_rows("q", 0, 1)
-        weigh_near(0, 0)
-        widen_v(1, 1, True)
-        weigh_near(0, 1)
-        make_gains(7, 8)
-        make_gains(8, 9)
-        make_gains(9, 10)
-        make_gains(10, 11)
-        turn("q", 1, 1)
-        copy_turned("q", 1, 1, False)
-        turn("k", 1, 0)
-        copy_turned("k", 1, 0, False)
-        turn("k", 1, 1)
-        copy_turned("k", 1, 1, False)
-        widen_v(1, 2, True)
+        for b in range(2):
+            weigh_block(NEAR0, b)
+            widen_v(1, 1 + b)
+        make_gains(6, 10)
+        for x, b in [("q", 1), ("k", 0), ("k", 1)]:
+            turn_copy(x, 1, b)
         quantise_scores(NEAR0, 0)
-        near_scores(0, 2)
-        near_scores(0, 3)
-        weigh_near(0, 2)
         quantise_rows("q", 1, 0)
-        widen_v(1, 3, True)
-        weigh_near(0, 3)
+        block_scores(NEAR0, 2)
+        block_scores(NEAR0, 3)
+        weigh_block(NEAR0, 2)
+        widen_v(1, 3)
+        weigh_block(NEAR0, 3)
         quantise_rows("k", 1, 0)
-        make_gains(11, 12)
-        turn("k", 1, 2)
-        copy_turned("k", 1, 2, False)
-        turn("k", 1, 3)
-        copy_turned("k", 1, 3, False)
-        turn("q", 1, 2)
-        copy_turned("q", 1, 2, False)
-        turn("q", 1, 3)
-        copy_turned("q", 1, 3, False)
-        mix(0, 0, 0)
-        mix(0, 0, 1)
-        far_scores(0, 0)
-        far_scores(0, 1)
+        make_gains(10, 12)
+        for r in range(2, 4):
+            turn_copy("k", 1, r)
+
+        for h in range(2):
+            mix(0, 0, h)
+        for b in range(2):
+            block_scores(FAR, b)
         emit_rows(0)
+        join_v(1, 0, on_vector=False)
+        for b in range(2, 4):
+            turn_copy("q", 1, b)
         quantise_scores(NEAR0, 1)
         quantise_rows("k", 1, 1)
-        weigh_far(0, 0)
-        weigh_far(0, 1)
-        mix(0, 1, 0)
-        mix(0, 1, 1)
-        join_v(1, 0, False)
+        for b in range(2):
+            weigh_block(FAR, b)
+        for h in range(2):
+            mix(0, 1, h)
         emit_rows(1)
-        join_v(1, 1, False)
-        mix(0, 2, 0)
+        block_scores(NEAR1, 0)
+        mix(0, 2, 0, score_banks)
         mix(0, 2, 1)
-        near_scores(1, 0)
-        quantise_rows("q", 1, 1)
-        join_far(0, True)
         quantise_v(1, 0)
         quantise_scores(FAR, 0)
+        quantise_rows("q", 1, 1)
         emit_rows(2)
-        near_scores(1, 1)
-        weigh_near(1, 0)
-        weigh_near(1, 1)
-        mix(0, 3, 0)
-        mix(0, 3, 1)
-        far_scores(1, 0)
-        far_scores(1, 1)
+        join_v(1, 1, on_vector=False)
+        block_scores(NEAR1, 1)
+        for b in range(2):
+            weigh_block(NEAR1, b)
+        for h in range(2):
+            mix(0, 3, h)
+        for j in range(2):
+            wide_scores(j)
         emit_rows(3)
-        weigh_far(1, 0)
+        weigh_wide(0)
         quantise_scores(NEAR1, 0)
         quantise_v(1, 1)
-        weigh_far(1, 1)
-        near_scores(1, 2)
-        mix(1, 0, 0)
-        emit_half(1, 0, 0, False)
-        mix(1, 1, 0)
-        emit_half(1, 1, 0, False)
-        mix(1, 0, 1)
-        emit_half(1, 0, 1, False)
-        near_scores(1, 3)
-        mix(1, 1, 1)
-        emit_half(1, 1, 1, False)
-        weigh_near(1, 2)
-        join_far(1, True)
+        weigh_wide(1)
+
+        block_scores(NEAR1, 2)
+        mix_and_emit(0, 0)
+        mix_and_emit(1, 0)
+        mix_and_emit(0, 1)
+        block_scores(NEAR1, 3)
+        mix_and_emit(1, 1)
+
+        weigh_block(NEAR1, 2)
+        join_wide()
         quantise_scores(NEAR1, 1, 0, 1)
         quantise_scores(FAR, 1)
-        weigh_near(1, 3)
+        weigh_block(NEAR1, 3)
         quantise_scores(NEAR1, 1, 1, 2)
-        mix(1, 2, 0)
-        emit_half(1, 2, 0, False)
-        mix(1, 2, 1)
-        emit_half(1, 2, 1, False)
-        new_bank(("mix", 1, 3, 256 * 0), score_banks)
-        mix_pass(1, 3, 256 * 0, 256, 0)
-        new_bank(("mix", 1, 3, 256 * 1), score_banks)
-        mix_pass(1, 3, 256 * 1, 256, 0)
-        new_bank(("mix", 1, 3, 256 * 2), score_banks)
-        mix_pass(1, 3, 256 * 2, 256, 0)
-        new_bank(("mix", 1, 3, 256 * 3), score_banks)
-        mix_pass(1, 3, 256 * 3, 256, 0)
-        mix_pass(1, 3, 256 * 0, 256, 1)
-        mix_pass(1, 3, 256 * 1, 256, 1)
-        mix_pass(1, 3, 256 * 2, 256, 1)
-        mix_pass(1, 3, 256 * 3, 256, 1)
-        copy_result(1, 3, 256 * 0, 256, False)
-        store(1, 3, 256 * 0, 256)
-        copy_result(1, 3, 256 * 1, 256, True)
-        store(1, 3, 256 * 1, 256)
-        copy_result(1, 3, 256 * 2, 256, False)
-        store(1, 3, 256 * 2, 256)
-        copy_result(1, 3, 256 * 3, 256, True)
-        store(1, 3, 256 * 3, 256)
+        for h in range(2):
+            mix_and_emit(2, h)
+
+        quarters = range(0, 2 * CHUNK, QUARTER)
+        for lo in quarters:
+            new_bank(("mix", 1, 3, lo), score_banks)
+            mix_pass(1, 3, lo, QUARTER, 0)
+        for lo in quarters:
+            mix_pass(1, 3, lo, QUARTER, 1)
+        for lo in quarters:
+            copy_result(1, 3, lo, QUARTER, on_vector=lo % CHUNK > 0)
+            store(1, 3, lo, QUARTER)

@@ -48,7 +48,8 @@ def tile_simplifiedretnet_pa_kernel(tc, q, k, v_bytes, v_scale, decay, out):
         x_codes = {key: sb("x_codes_%s_%s_%s" % key, [P, 512], U32) for key in row_pairs}
         x_scales = {key: sb("x_scales_%s_%s_%s" % key, [P, 512], U8) for key in row_pairs}
         v_wide = [sb("v_wide_%s" % (g,), [P, 2, 1024, 2], BF16) for g in range(2)]
-        v_words = {key: sb("v_words_%s_%s" % key, [P, CHUNK, 4], BF16) for key in v_halves}
+        v_words = {key: sb("v_words_%s_%s" % key, [P, CHUNK, 4], BF16)[:] for key in v_halves[:3]}
+        v_words[1, 1] = turned["q", 1, 1][:].rearrange("p s m u -> p (s m u)").bitcast(BF16).rearrange("p (n t) -> p n t", t=4)
         v_codes = {key: sb("v_codes_%s_%s" % key, [P, CHUNK], U32) for key in v_halves}
         v_scales = {key: sb("v_scales_%s_%s" % key, [P, CHUNK], U8) for key in v_halves}
         gain = [sb("gain_%s" % (table,), [P, 4 * CHUNK], F32) for table in range(3)]
@@ -145,6 +146,10 @@ def tile_simplifiedretnet_pa_kernel(tc, q, k, v_bytes, v_scale, decay, out):
         def join_v(g, h, on_vector):
             pairs = v_wide[g][:].rearrange("p j n e -> p j (n e)").bitcast(F32)
             join_halves(v_words[g, h][:], pairs[:, :, CHUNK * h : CHUNK * (h + 1)], on_vector)
+
+        def join_v_on_gpsimd(g, h):
+            pairs = v_wide[g][:].rearrange("p j n e -> p j (n e)").bitcast(U32)[:, :, CHUNK * h : CHUNK * (h + 1)]
+            nc.gpsimd.tensor_copy(out=v_words[g, h].bitcast(U32), in_=pairs.rearrange("p j n -> p n j"))
 
         def quantise_v(g, h):
             nc.vector.quantize_mx(
@@ -358,7 +363,7 @@ def tile_simplifiedretnet_pa_kernel(tc, q, k, v_bytes, v_scale, decay, out):
         quantise_scores(FAR, 0)
         quantise_rows("q", 1, 1)
         emit_rows(2)
-        join_v(1, 1, on_vector=False)
+        join_v_on_gpsimd(1, 1)
         block_scores(NEAR1, 1)
         for b in range(2):
             weigh_block(NEAR1, b)

@@ -16,11 +16,14 @@ FLOPS = 2 * 1024 * (512 * 512 + 512 * 1024) * 2
 P = 128
 CHUNK = 512
 QUARTER = 256
-RUN = 4
 MASKED = 2.0**100
 LEAST_RATE = 2.0**-90
 LOG_SCALE = -5.0 * math.log(2.0)
 NEAR0, FAR, NEAR1 = (0, 0), (0, 1), (1, 1)
+SCORE_BANKS = 4
+WIDE_TILES = [(FAR, 0), (FAR, 1)]
+WOVEN = []
+REUSED = {}
 
 
 def tile_simplifiedretnet_pa_kernel(tc, q, k, v_bytes, v_scale, decay, out):
@@ -34,8 +37,8 @@ def tile_simplifiedretnet_pa_kernel(tc, q, k, v_bytes, v_scale, decay, out):
 
     with ExitStack() as ctx:
         keep = ctx.enter_context(tc.tile_pool(name="keep", bufs=1))
-        score_banks = ctx.enter_context(tc.psum_pool(name="score_banks", bufs=4))
-        other_banks = ctx.enter_context(tc.psum_pool(name="other_banks", bufs=4))
+        score_banks = ctx.enter_context(tc.psum_pool(name="score_banks", bufs=SCORE_BANKS))
+        other_banks = ctx.enter_context(tc.psum_pool(name="other_banks", bufs=8 - SCORE_BANKS))
         ctx.enter_context(tc.manual_schedule())
 
         def sb(name, shape, dtype):
@@ -44,17 +47,18 @@ def tile_simplifiedretnet_pa_kernel(tc, q, k, v_bytes, v_scale, decay, out):
         row_pairs = [(x, c, a) for x in "qk" for c in range(2) for a in range(2)]
         v_halves = [(g, h) for g in range(2) for h in range(2)]
         score_pairs = [(g, c, a) for g, c in (NEAR0, FAR, NEAR1) for a in range(2)]
-        turned = {key: sb("turned_%s_%s_%s" % key, [P, 4, P, 2], F32) for key in row_pairs}
+        turned = {key: sb("turned_%s_%s_%s" % key, [P, 2 * CHUNK], F32) for key in row_pairs}
         x_codes = {key: sb("x_codes_%s_%s_%s" % key, [P, 512], U32) for key in row_pairs}
         x_scales = {key: sb("x_scales_%s_%s_%s" % key, [P, 512], U8) for key in row_pairs}
-        v_wide = [sb("v_wide_%s" % (g,), [P, 2, 1024, 2], BF16) for g in range(2)]
-        v_words = {key: sb("v_words_%s_%s" % key, [P, CHUNK, 4], BF16)[:] for key in v_halves[:3]}
-        v_words[1, 1] = turned["q", 1, 1][:].rearrange("p s m u -> p (s m u)").bitcast(BF16).rearrange("p (n t) -> p n t", t=4)
+        v_wide = [sb("v_wide_%s" % (g,), [P, 4 * 1024], BF16) for g in range(2)]
+        v_words = {key: sb("v_words_%s_%s" % key, [P, 4 * CHUNK], BF16) for key in v_halves if key not in REUSED}
+        for key, rows in REUSED.items():
+            v_words[key] = turned[rows][:].bitcast(BF16)
         v_codes = {key: sb("v_codes_%s_%s" % key, [P, CHUNK], U32) for key in v_halves}
         v_scales = {key: sb("v_scales_%s_%s" % key, [P, CHUNK], U8) for key in v_halves}
         gain = [sb("gain_%s" % (table,), [P, 4 * CHUNK], F32) for table in range(3)]
-        s_words = {key: sb("s_words_%s_%s_%s" % key, [P, 2, P, 4], BF16) for key in score_pairs}
-        wide_halves = sb("wide_halves", [P, 2, 2 * P, 2], BF16)
+        s_words = {key: sb("s_words_%s_%s_%s" % key, [P, 2 * CHUNK], BF16) for key in score_pairs}
+        halves = {key: sb("halves_%s_%s" % (sum(key[0]), key[1]), [P, 2 * CHUNK], BF16) for key in WIDE_TILES}
         s_codes = {key: sb("s_codes_%s_%s_%s" % key, [P, 2 * P], U32) for key in score_pairs}
         s_scales = {key: sb("s_scales_%s_%s_%s" % key, [P, 2 * P], U8) for key in score_pairs}
         result = {(c, b): sb("result_%s_%s" % (c, b), [P, 1024], F32) for c in range(2) for b in range(4)}
@@ -86,24 +90,21 @@ def tile_simplifiedretnet_pa_kernel(tc, q, k, v_bytes, v_scale, decay, out):
         def load_rate(g, queue):
             queue.dma_start(out=rate[g][:], in_=decay.rearrange("(g p r) -> g p r", g=2, r=4)[g])
 
-        def load_scale(g):
-            nc.sync.dma_start(out=key_scale[g][:], in_=v_scale.rearrange("o (g p r) i -> (o g) p (r i)", g=2, r=4)[g])
+        def load_scale(g, queue):
+            queue.dma_start(out=key_scale[g][:], in_=v_scale.rearrange("o (g p r) i -> (o g) p (r i)", g=2, r=4)[g])
 
         def negate_rate(g):
             nc.scalar.activation(out=neg_rate[g][:], in_=rate[g][:], func=ACT.Copy, scale=-1.0, bias=-LEAST_RATE)
 
-        def new_bank(key, pool):
-            psum[key] = pool.tile([P, CHUNK], F32, name="bank")
+        def new_bank(key, pool, dtype=F32, width=CHUNK):
+            psum[key] = pool.tile([P, width], dtype, name="bank")
             return psum[key]
 
-        def turn(x, c, b):
-            bank = new_bank(("turn", x, c, b), other_banks)[:].rearrange("p (f u m) -> p f u m", f=2, u=2)
+        def turn(x, c, b, pool=other_banks):
+            bank = new_bank(("turn", x, c, b), pool)[:].rearrange("p (f u m) -> p f u m", f=2, u=2)
             for f in range(2):
                 for u in range(2):
                     nc.tensor.transpose(bank[:, f, u, :], words[x, c, b][:, f, u, :], ident[:])
-
-        def slot(b, f):
-            return 2 * f + b % 2
 
         def copy(out, in_, on_vector):
             if on_vector:
@@ -111,118 +112,117 @@ def tile_simplifiedretnet_pa_kernel(tc, q, k, v_bytes, v_scale, decay, out):
             else:
                 nc.scalar.copy(out, in_)
 
-        def copy_turned(x, c, b):
-            src = psum["turn", x, c, b][:].rearrange("p (f u m) -> p f m u", f=2, u=2)
-            nc.scalar.copy(turned[x, c, b // 2][:, b % 2 :: 2], src)
+        def slot(x, c, b, f):
+            return 2 * f + b % 2
 
-        def quantise_rows(x, c, a):
+        def copy_turned(x, c, b, on_vector=False):
+            src = psum["turn", x, c, b][:].rearrange("p (f u m) -> p f m u", f=2, u=2)
+            slots = turned[x, c, b // 2][:].rearrange("p (n m u) -> p n m u", n=4, u=2)
+            lo, hi = slot(x, c, b, 0), slot(x, c, b, 1)
+            copy(slots[:, lo : hi + 1 : hi - lo], src, on_vector)
+
+        def quantise_rows(x, c, a, lo=0, hi=2):
             nc.vector.quantize_mx(
-                out=x_codes[x, c, a][:].bitcast(FP8X4),
-                scales=x_scales[x, c, a][:],
-                in_=turned[x, c, a][:].rearrange("p s m u -> p (s m u)").bitcast(BF16),
+                out=x_codes[x, c, a][:, 2 * P * lo : 2 * P * hi].bitcast(FP8X4),
+                scales=x_scales[x, c, a][:, 2 * P * lo : 2 * P * hi],
+                in_=turned[x, c, a][:, CHUNK * lo : CHUNK * hi].bitcast(BF16),
             )
 
         def quantise_block(x, c, b):
             for f in range(2):
-                n = slot(b, f)
+                n = slot(x, c, b, f)
                 nc.vector.quantize_mx(
                     out=x_codes[x, c, b // 2][:, P * n : P * (n + 1)].bitcast(FP8X4),
                     scales=x_scales[x, c, b // 2][:, P * n : P * (n + 1)],
-                    in_=turned[x, c, b // 2][:, n].rearrange("p m u -> p (m u)").bitcast(BF16),
+                    in_=turned[x, c, b // 2][:, 2 * P * n : 2 * P * (n + 1)].bitcast(BF16),
                 )
 
-        def widen_v(g, r):
-            nc.vector.tensor_scalar(
-                out=v_wide[g][:, r % 2, :, r // 2],
-                in0=fp8[g, r].bitcast(E4M3FN),
-                scalar1=key_scale[g][:, r : r + 1],
-                scalar2=None,
-                op0=ALU.mult,
-            )
+        def widen_v(g, r, on_vector=True):
+            if g in WOVEN:
+                plane = v_wide[g][:, 1024 * r : 1024 * (r + 1)]
+            else:
+                plane = v_wide[g][:].rearrange("p (j n e) -> p j e n", j=2, e=2)[:, r // 2, r % 2]
+            if on_vector:
+                nc.vector.tensor_scalar(out=plane, in0=fp8[g, r].bitcast(E4M3FN), scalar1=key_scale[g][:, r : r + 1], scalar2=None, op0=ALU.mult)
+            else:
+                nc.scalar.activation(out=plane, in_=fp8[g, r].bitcast(E4M3FN), func=ACT.Copy, scale=key_scale[g][:, r : r + 1])
 
-        def join_halves(dst, pairs, on_vector):
-            copy(dst.bitcast(F32), pairs.rearrange("p j n -> p n j"), on_vector)
+        def join_on_gpsimd(g, h):
+            pairs = v_wide[g][:].bitcast(U32).rearrange("p (j n) -> p n j", j=2)[:, CHUNK * h : CHUNK * (h + 1), :]
+            nc.gpsimd.tensor_copy(out=v_words[g, h][:].bitcast(U32).rearrange("p (n j) -> p n j", j=2), in_=pairs)
 
         def join_v(g, h, on_vector):
-            pairs = v_wide[g][:].rearrange("p j n e -> p j (n e)").bitcast(F32)
-            join_halves(v_words[g, h][:], pairs[:, :, CHUNK * h : CHUNK * (h + 1)], on_vector)
-
-        def join_v_on_gpsimd(g, h):
-            pairs = v_wide[g][:].rearrange("p j n e -> p j (n e)").bitcast(U32)[:, :, CHUNK * h : CHUNK * (h + 1)]
-            nc.gpsimd.tensor_copy(out=v_words[g, h].bitcast(U32), in_=pairs.rearrange("p j n -> p n j"))
+            pairs = v_wide[g][:].bitcast(F32).rearrange("p (j n) -> p n j", j=2)[:, CHUNK * h : CHUNK * (h + 1), :]
+            copy(v_words[g, h][:].bitcast(F32).rearrange("p (n j) -> p n j", j=2), pairs, on_vector)
 
         def quantise_v(g, h):
-            nc.vector.quantize_mx(
-                out=v_codes[g, h][:].bitcast(FP8X4),
-                scales=v_scales[g, h][:],
-                in_=v_words[g, h][:].rearrange("p n t -> p (n t)"),
-            )
-
-        def place(r):
-            return 2 * (r % 2) + r // 2
+            nc.vector.quantize_mx(out=v_codes[g, h][:].bitcast(FP8X4), scales=v_scales[g, h][:], in_=v_words[g, h][:])
 
         def make_gain(tile, r):
             table = dist if tile == FAR else causal_dist
             nc.scalar.activation(
-                out=gain[sum(tile)][:, CHUNK * place(r) : CHUNK * (place(r) + 1)],
+                out=gain[sum(tile)][:, CHUNK * r : CHUNK * (r + 1)],
                 in_=table[:, 3 - r : 3 - r + CHUNK],
                 func=ACT.Exp,
                 bias=far_bias[:, r : r + 1] if tile == FAR else LOG_SCALE,
                 scale=neg_rate[tile[0]][:, r : r + 1],
             )
 
-        def score_passes(out_cols, g, r, c, b, width):
-            a = b // 2
+        def score_passes(out_cols, tile, r, b, width):
+            g, c = tile
             for f in range(2):
-                keys = slice(P * slot(r, f), P * slot(r, f) + P)
-                cols = slice(P * slot(b, f), P * slot(b, f) + width)
+                keys = slice(P * slot("k", g, r, f), P * slot("k", g, r, f) + P)
+                cols = slice(P * slot("q", c, b, f), P * slot("q", c, b, f) + width)
                 nc.tensor.matmul_mx(
                     out=out_cols,
                     lhsT=x_codes["k", g, r // 2][:, keys].bitcast(FP8X4),
                     lhsT_scale=x_scales["k", g, r // 2][:, keys],
-                    rhs=x_codes["q", c, a][:, cols].bitcast(FP8X4),
-                    rhs_scale=x_scales["q", c, a][:, cols],
+                    rhs=x_codes["q", c, b // 2][:, cols].bitcast(FP8X4),
+                    rhs_scale=x_scales["q", c, b // 2][:, cols],
                     start=(f == 0),
                     stop=(f == 1),
                 )
 
-        def block_scores(tile, b):
-            bank = new_bank(("scores", tile, b), score_banks)
+        def scores(tile, b, pool=score_banks):
+            bank = new_bank(("scores", tile, b), pool)
             for r in range(4):
-                score_passes(bank[:, P * place(r) : P * (place(r) + 1)], tile[0], r, tile[1], b, P)
+                score_passes(bank[:, P * r : P * (r + 1)], tile, r, b, P)
 
-        def wide_scores(j):
-            bank = new_bank(("wide", j), score_banks)
+        def wide_scores(tile, a, j, pool=score_banks):
+            bank = new_bank(("wide", tile, a, j), pool)
             for e in range(2):
-                score_passes(bank[:, 2 * P * e : 2 * P * (e + 1)], 0, 2 * e + j, 1, 2, 2 * P)
+                score_passes(bank[:, 2 * P * e : 2 * P * (e + 1)], tile, 2 * j + e, 2 * a, 2 * P)
 
-        def weigh_block(tile, b):
+        def weigh_wide(tile, a, j):
             nc.vector.tensor_tensor(
-                out=s_words[tile + (b // 2,)][:, b % 2].rearrange("p (m i) t -> p m t i", i=2),
+                out=halves[tile, a][:, CHUNK * j : CHUNK * (j + 1)].rearrange("p (m i e) -> p m e i", i=4, e=2),
+                in0=psum["wide", tile, a, j][:].rearrange("p (e m i) -> p m e i", e=2, i=4),
+                in1=gain[sum(tile)][:].rearrange("p (j e a m i) -> p j a m e i", j=2, e=2, a=2, i=4)[:, j, a],
+                op=ALU.mult,
+            )
+
+        def join_wide(tile, a, on_vector):
+            pairs = halves[tile, a][:].bitcast(F32).rearrange("p (j n) -> p n j", j=2)
+            copy(s_words[tile + (a,)][:].bitcast(F32).rearrange("p (n j) -> p n j", j=2), pairs, on_vector)
+
+        def weigh(tile, b):
+            nc.vector.tensor_tensor(
+                out=s_words[tile + (b // 2,)][:, CHUNK * (b % 2) : CHUNK * (b % 2 + 1)].rearrange("p (m i t) -> p m t i", i=2, t=4),
                 in0=psum["scores", tile, b][:].rearrange("p (t m i) -> p m t i", t=4, i=2),
                 in1=gain[sum(tile)][:].rearrange("p (t b m i) -> p b m t i", t=4, b=4, i=2)[:, b],
                 op=ALU.mult,
             )
-
-        def weigh_wide(j):
-            nc.vector.tensor_tensor(
-                out=wide_halves[:, j].rearrange("p (m i) e -> p m e i", i=RUN),
-                in0=psum["wide", j][:].rearrange("p (e m i) -> p m e i", e=2, i=RUN),
-                in1=gain[sum(FAR)][:].rearrange("p (j e a m i) -> p j a m e i", j=2, e=2, a=2, i=RUN)[:, j, 1],
-                op=ALU.mult,
-            )
-
-        def join_wide():
-            pairs = wide_halves[:].rearrange("p j n e -> p j (n e)").bitcast(F32)
-            join_halves(s_words[FAR + (1,)][:].rearrange("p b i t -> p (b i) t"), pairs, on_vector=True)
 
         def quantise_scores(tile, a, lo=0, hi=2):
             key = tile + (a,)
             nc.vector.quantize_mx(
                 out=s_codes[key][:, P * lo : P * hi].bitcast(FP8X4),
                 scales=s_scales[key][:, P * lo : P * hi],
-                in_=s_words[key][:, lo:hi].rearrange("p b i t -> p (b i t)"),
+                in_=s_words[key][:, CHUNK * lo : CHUNK * hi],
             )
+
+        def quantise_score_block(tile, b):
+            quantise_scores(tile, b // 2, b % 2, b % 2 + 1)
 
         def mix_pass(c, b, lo, width, g):
             rows = slice(P * (b % 2), P * (b % 2 + 1))
@@ -242,163 +242,221 @@ def tile_simplifiedretnet_pa_kernel(tc, q, k, v_bytes, v_scale, decay, out):
             for g in range(c + 1):
                 mix_pass(c, b, CHUNK * h, CHUNK, g)
 
-        def store(c, b, lo, width):
+        def store(c, b, lo=0, width=2 * CHUNK):
             nc.sync.dma_start(out=out_rows[c][:, b, lo : lo + width], in_=result[c, b][:, lo : lo + width])
 
         def copy_result(c, b, lo, width=CHUNK, on_vector=False):
             copy(result[c, b][:, lo : lo + width], psum["mix", c, b, lo][:, :width], on_vector)
 
-        def emit_rows(b):
-            for h in range(2):
-                copy_result(0, b, CHUNK * h)
-            store(0, b, 0, 2 * CHUNK)
+        def warm_up():
+            nc.vector.memset(warm_in[:], 0.0)
+            nc.scalar.activation(out=warm_out[:], in_=warm_in[:], func=ACT.Exp)
 
-        def mix_and_emit(b, h):
-            mix(1, b, h)
-            copy_result(1, b, CHUNK * h)
-            store(1, b, CHUNK * h, CHUNK)
+        def make_dist():
+            nc.gpsimd.iota(dist[:], pattern=[[1, CHUNK + 4]], base=-3, channel_multiplier=-4, allow_small_or_imprecise_dtypes=True)
 
-        def turn_copy(x, c, b):
-            turn(x, c, b)
-            copy_turned(x, c, b)
+        def make_far_bias():
+            nc.scalar.activation(out=far_bias[:], in_=rate[0][:], func=ACT.Copy, scale=-float(CHUNK), bias=LOG_SCALE)
+
+        def make_ident():
+            nc.vector.tensor_scalar(out=ident[:], in0=dist[:, 3 : 3 + CHUNK : 4], scalar1=0.0, scalar2=None, op0=ALU.is_equal)
+
+        def make_causal():
+            nc.vector.scalar_tensor_tensor(out=causal_dist[:], in0=dist[:], scalar=-MASKED, in1=dist[:], op0=ALU.mult, op1=ALU.max)
+
+        def mix_far(b, lo, width=CHUNK, pool=other_banks):
+            new_bank(("mix", 1, b, lo), pool)
+            mix_pass(1, b, lo, width, 0)
+
+        def mix_near(b, lo, width=CHUNK):
+            mix_pass(1, b, lo, width, 1)
 
         load_rate(0, nc.scalar)
-        load_scale(0)
-        for r in range(2):
-            load_v(0, r, r + 1)
+        warm_up()
+        make_dist()
+        load_scale(0, nc.sync)
+        load_v(0, 0, 1)
+        load_v(0, 2, 3)
         load_rows("q", 0, 0)
-        for r in range(2):
-            load_rows("k", 0, r)
-            load_v(0, 2 + r, 3 + r)
-        for x, c, b in [("k", 0, 2), ("k", 0, 3), ("q", 0, 1), ("q", 0, 2), ("q", 0, 3), ("q", 1, 0)]:
-            load_rows(x, c, b)
+        load_rows("k", 0, 0)
+        load_v(0, 1, 2)
+        load_rows("k", 0, 1)
+        load_v(0, 3, 4)
+        load_rows("k", 0, 2)
+        load_rows("k", 0, 3)
+        load_rows("q", 0, 1)
+        load_rows("q", 0, 2)
+        load_rows("q", 0, 3)
+        load_rows("q", 1, 0)
         load_v(1, 0, 2)
         load_rate(1, nc.sync)
-        load_scale(1)
+        load_scale(1, nc.sync)
         load_rows("q", 1, 1)
         load_rows("k", 1, 0)
         load_v(1, 2, 4)
-        for x, b in [("k", 1), ("k", 2), ("k", 3), ("q", 2), ("q", 3)]:
-            load_rows(x, 1, b)
-
-        nc.vector.memset(warm_in[:], 0.0)
-        nc.scalar.activation(out=warm_out[:], in_=warm_in[:], func=ACT.Exp)
-
-        nc.gpsimd.iota(dist[:], pattern=[[1, CHUNK + 4]], base=-3, channel_multiplier=-4, allow_small_or_imprecise_dtypes=True)
+        load_rows("k", 1, 1)
+        load_rows("k", 1, 2)
+        load_rows("k", 1, 3)
+        load_rows("q", 1, 2)
+        load_rows("q", 1, 3)
+        make_causal()
+        make_ident()
+        widen_v(0, 0)
+        widen_v(0, 2)
+        widen_v(0, 1)
+        widen_v(0, 3)
         negate_rate(0)
-        nc.scalar.activation(out=far_bias[:], in_=rate[0][:], func=ACT.Copy, scale=-float(CHUNK), bias=LOG_SCALE)
-        nc.vector.scalar_tensor_tensor(out=causal_dist[:], in0=dist[:], scalar=-MASKED, in1=dist[:], op0=ALU.mult, op1=ALU.max)
-        nc.vector.tensor_scalar(out=ident[:], in0=dist[:, 3 : 3 + CHUNK : 4], scalar1=0.0, scalar2=None, op0=ALU.is_equal)
-
-        gains = [(tile, r) for tile in (NEAR0, FAR, NEAR1) for r in (0, 2, 1, 3)]
-
-        def make_gains(lo, hi):
-            for tile, r in gains[lo:hi]:
-                make_gain(tile, r)
-
-        make_gains(0, 4)
-        for r in range(4):
-            widen_v(0, r)
-        turn_copy("q", 0, 0)
-        make_gains(4, 5)
+        make_far_bias()
+        make_gain(NEAR0, 0)
+        make_gain(NEAR0, 1)
+        make_gain(NEAR0, 2)
+        make_gain(NEAR0, 3)
+        turn("q", 0, 0)
+        turn("k", 0, 0)
+        turn("k", 0, 1)
+        turn("k", 0, 2)
+        copy_turned("q", 0, 0)
+        make_gain(FAR, 0)
+        copy_turned("k", 0, 0)
+        copy_turned("k", 0, 1)
+        copy_turned("k", 0, 2)
+        turn("k", 0, 3)
+        turn("q", 0, 1)
+        turn("q", 0, 2)
+        turn("q", 0, 3)
         quantise_block("q", 0, 0)
-        for h in range(2):
-            join_v(0, h, on_vector=True)
+        join_v(0, 0, True)
+        join_v(0, 1, True)
         quantise_v(0, 0)
-        for a in range(2):
-            for r in range(2 * a, 2 * a + 2):
-                turn_copy("k", 0, r)
-            quantise_rows("k", 0, a)
-        turn_copy("q", 0, 1)
+        quantise_rows("k", 0, 0)
+        copy_turned("k", 0, 3)
+        copy_turned("q", 0, 1)
+        copy_turned("q", 0, 2)
+        copy_turned("q", 0, 3)
+        negate_rate(1)
+        make_gain(FAR, 1)
+        turn("q", 1, 0)
+        quantise_rows("k", 0, 1)
         quantise_block("q", 0, 1)
         quantise_v(0, 1)
-        for b in range(2, 4):
-            turn_copy("q", 0, b)
-        turn("q", 1, 0)
-        negate_rate(1)
-        make_gains(5, 6)
-        copy_turned("q", 1, 0)
-
-        block_scores(NEAR0, 0)
-        block_scores(NEAR0, 1)
         widen_v(1, 0)
         quantise_rows("q", 0, 1)
-        for b in range(2):
-            weigh_block(NEAR0, b)
-            widen_v(1, 1 + b)
-        make_gains(6, 10)
-        for x, b in [("q", 1), ("k", 0), ("k", 1)]:
-            turn_copy(x, 1, b)
+        copy_turned("q", 1, 0)
+        make_gain(FAR, 2)
+        make_gain(FAR, 3)
+        make_gain(NEAR1, 0)
+        make_gain(NEAR1, 1)
+        scores(NEAR0, 0)
+        scores(NEAR0, 1)
+        turn("q", 1, 1)
+        turn("k", 1, 0)
+        turn("k", 1, 1)
+        scores(NEAR0, 2)
+        scores(NEAR0, 3)
+        turn("k", 1, 2)
+        weigh(NEAR0, 0)
+        widen_v(1, 1)
+        weigh(NEAR0, 1)
+        widen_v(1, 2)
         quantise_scores(NEAR0, 0)
+        copy_turned("q", 1, 1)
+        copy_turned("k", 1, 0)
+        copy_turned("k", 1, 1)
+        make_gain(NEAR1, 2)
+        copy_turned("k", 1, 2)
+        turn("k", 1, 3)
+        mix(0, 0, 0)
+        mix(0, 0, 1)
         quantise_rows("q", 1, 0)
-        block_scores(NEAR0, 2)
-        block_scores(NEAR0, 3)
-        weigh_block(NEAR0, 2)
-        widen_v(1, 3)
-        weigh_block(NEAR0, 3)
         quantise_rows("k", 1, 0)
-        make_gains(10, 12)
-        for r in range(2, 4):
-            turn_copy("k", 1, r)
-
-        for h in range(2):
-            mix(0, 0, h)
-        for b in range(2):
-            block_scores(FAR, b)
-        emit_rows(0)
-        join_v(1, 0, on_vector=False)
-        for b in range(2, 4):
-            turn_copy("q", 1, b)
-        quantise_scores(NEAR0, 1)
+        widen_v(1, 3)
+        copy_turned("k", 1, 3)
+        copy_result(0, 0, 0, 512)
+        copy_result(0, 0, 512, 512)
+        make_gain(NEAR1, 3)
+        wide_scores(FAR, 0, 0)
+        wide_scores(FAR, 0, 1)
+        turn("q", 1, 2)
+        turn("q", 1, 3)
+        mix(0, 1, 0)
+        mix(0, 1, 1)
+        join_on_gpsimd(1, 1)
+        store(0, 0)
         quantise_rows("k", 1, 1)
-        for b in range(2):
-            weigh_block(FAR, b)
-        for h in range(2):
-            mix(0, 1, h)
-        emit_rows(1)
-        block_scores(NEAR1, 0)
-        mix(0, 2, 0, score_banks)
+        weigh(NEAR0, 2)
+        weigh(NEAR0, 3)
+        weigh_wide(FAR, 0, 0)
+        weigh_wide(FAR, 0, 1)
+        quantise_scores(NEAR0, 1)
+        copy_turned("q", 1, 2)
+        copy_turned("q", 1, 3)
+        join_v(1, 0, False)
+        copy_result(0, 1, 0, 512)
+        join_wide(FAR, 0, False)
+        copy_result(0, 1, 512, 512)
+        scores(NEAR1, 0)
+        scores(NEAR1, 1)
+        mix(0, 2, 0)
         mix(0, 2, 1)
+        store(0, 1)
+        quantise_rows("q", 1, 1)
+        weigh(NEAR1, 0)
+        weigh(NEAR1, 1)
         quantise_v(1, 0)
         quantise_scores(FAR, 0)
-        quantise_rows("q", 1, 1)
-        emit_rows(2)
-        join_v_on_gpsimd(1, 1)
-        block_scores(NEAR1, 1)
-        for b in range(2):
-            weigh_block(NEAR1, b)
-        for h in range(2):
-            mix(0, 3, h)
-        for j in range(2):
-            wide_scores(j)
-        emit_rows(3)
-        weigh_wide(0)
         quantise_scores(NEAR1, 0)
         quantise_v(1, 1)
-        weigh_wide(1)
-
-        block_scores(NEAR1, 2)
-        mix_and_emit(0, 0)
-        mix_and_emit(1, 0)
-        mix_and_emit(0, 1)
-        block_scores(NEAR1, 3)
-        mix_and_emit(1, 1)
-
-        weigh_block(NEAR1, 2)
-        join_wide()
-        quantise_scores(NEAR1, 1, 0, 1)
+        copy_result(0, 2, 0, 512)
+        copy_result(0, 2, 512, 512)
+        wide_scores(FAR, 1, 0)
+        wide_scores(FAR, 1, 1)
+        mix(0, 3, 0)
+        scores(NEAR1, 2)
+        mix(0, 3, 1)
+        mix(1, 0, 0)
+        mix(1, 1, 0)
+        scores(NEAR1, 3)
+        store(0, 2)
+        weigh_wide(FAR, 1, 0)
+        weigh_wide(FAR, 1, 1)
+        weigh(NEAR1, 2)
+        join_wide(FAR, 1, True)
+        quantise_score_block(NEAR1, 2)
         quantise_scores(FAR, 1)
-        weigh_block(NEAR1, 3)
-        quantise_scores(NEAR1, 1, 1, 2)
-        for h in range(2):
-            mix_and_emit(2, h)
-
-        quarters = range(0, 2 * CHUNK, QUARTER)
-        for lo in quarters:
-            new_bank(("mix", 1, 3, lo), score_banks)
-            mix_pass(1, 3, lo, QUARTER, 0)
-        for lo in quarters:
-            mix_pass(1, 3, lo, QUARTER, 1)
-        for lo in quarters:
-            copy_result(1, 3, lo, QUARTER, on_vector=lo % CHUNK > 0)
-            store(1, 3, lo, QUARTER)
+        weigh(NEAR1, 3)
+        quantise_score_block(NEAR1, 3)
+        copy_result(0, 3, 0, 512)
+        copy_result(0, 3, 512, 512)
+        copy_result(1, 0, 0, 512)
+        copy_result(1, 1, 0, 512)
+        mix(1, 0, 1)
+        mix(1, 1, 1)
+        mix(1, 2, 0)
+        mix(1, 2, 1)
+        mix_far(3, 0, 256, pool=score_banks)
+        mix_far(3, 256, 256, pool=score_banks)
+        mix_far(3, 512, 256, pool=score_banks)
+        mix_far(3, 768, 256, pool=score_banks)
+        mix_near(3, 0, 256)
+        mix_near(3, 256, 256)
+        mix_near(3, 512, 256)
+        mix_near(3, 768, 256)
+        store(0, 3)
+        store(1, 0, 0, 512)
+        store(1, 1, 0, 512)
+        copy_result(1, 3, 256, 256, True)
+        copy_result(1, 3, 768, 256, True)
+        copy_result(1, 0, 512, 512)
+        copy_result(1, 1, 512, 512)
+        copy_result(1, 2, 0, 512)
+        copy_result(1, 2, 512, 512)
+        copy_result(1, 3, 0, 256)
+        copy_result(1, 3, 512, 256)
+        store(1, 0, 512, 512)
+        store(1, 1, 512, 512)
+        store(1, 2, 0, 512)
+        store(1, 2, 512, 512)
+        store(1, 3, 0, 256)
+        store(1, 3, 256, 256)
+        store(1, 3, 512, 256)
+        store(1, 3, 768, 256)

@@ -23,7 +23,7 @@ NEAR0, FAR, NEAR1 = (0, 0), (0, 1), (1, 1)
 SCORE_BANKS = 4
 WIDE_TILES = [(FAR, 0), (FAR, 1)]
 WOVEN = []
-REUSED = {}
+REUSED = {(1, 1): ("q", 1, 1)}
 
 
 def tile_simplifiedretnet_pa_kernel(tc, q, k, v_bytes, v_scale, decay, out):
@@ -326,26 +326,23 @@ def tile_simplifiedretnet_pa_kernel(tc, q, k, v_bytes, v_scale, decay, out):
         turn("q", 0, 3)
         quantise_block("q", 0, 0)
         join_v(0, 0, True)
-        join_v(0, 1, True)
-        quantise_v(0, 0)
         quantise_rows("k", 0, 0)
+        quantise_v(0, 0)
         copy_turned("k", 0, 3)
         copy_turned("q", 0, 1)
         copy_turned("q", 0, 2)
         copy_turned("q", 0, 3)
+        join_v(0, 1, False)
         negate_rate(1)
-        make_gain(FAR, 1)
         turn("q", 1, 0)
         quantise_rows("k", 0, 1)
         quantise_block("q", 0, 1)
-        quantise_v(0, 1)
         widen_v(1, 0)
         quantise_rows("q", 0, 1)
+        widen_v(1, 1)
         copy_turned("q", 1, 0)
+        make_gain(FAR, 1)
         make_gain(FAR, 2)
-        make_gain(FAR, 3)
-        make_gain(NEAR1, 0)
-        make_gain(NEAR1, 1)
         scores(NEAR0, 0)
         scores(NEAR0, 1)
         turn("q", 1, 1)
@@ -355,44 +352,46 @@ def tile_simplifiedretnet_pa_kernel(tc, q, k, v_bytes, v_scale, decay, out):
         scores(NEAR0, 3)
         turn("k", 1, 2)
         weigh(NEAR0, 0)
-        widen_v(1, 1)
+        quantise_v(0, 1)
         weigh(NEAR0, 1)
         widen_v(1, 2)
         quantise_scores(NEAR0, 0)
         copy_turned("q", 1, 1)
         copy_turned("k", 1, 0)
         copy_turned("k", 1, 1)
-        make_gain(NEAR1, 2)
+        make_gain(FAR, 3)
+        make_gain(NEAR1, 0)
         copy_turned("k", 1, 2)
         turn("k", 1, 3)
         mix(0, 0, 0)
         mix(0, 0, 1)
         quantise_rows("q", 1, 0)
         quantise_rows("k", 1, 0)
+        weigh(NEAR0, 2)
         widen_v(1, 3)
         copy_turned("k", 1, 3)
         copy_result(0, 0, 0, 512)
         copy_result(0, 0, 512, 512)
-        make_gain(NEAR1, 3)
+        make_gain(NEAR1, 1)
         wide_scores(FAR, 0, 0)
         wide_scores(FAR, 0, 1)
         turn("q", 1, 2)
         turn("q", 1, 3)
         mix(0, 1, 0)
         mix(0, 1, 1)
-        join_on_gpsimd(1, 1)
+        join_on_gpsimd(1, 0)
         store(0, 0)
         quantise_rows("k", 1, 1)
-        weigh(NEAR0, 2)
         weigh(NEAR0, 3)
         weigh_wide(FAR, 0, 0)
         weigh_wide(FAR, 0, 1)
         quantise_scores(NEAR0, 1)
         copy_turned("q", 1, 2)
         copy_turned("q", 1, 3)
-        join_v(1, 0, False)
-        copy_result(0, 1, 0, 512)
+        make_gain(NEAR1, 2)
+        make_gain(NEAR1, 3)
         join_wide(FAR, 0, False)
+        copy_result(0, 1, 0, 512)
         copy_result(0, 1, 512, 512)
         scores(NEAR1, 0)
         scores(NEAR1, 1)
@@ -400,12 +399,9 @@ def tile_simplifiedretnet_pa_kernel(tc, q, k, v_bytes, v_scale, decay, out):
         mix(0, 2, 1)
         store(0, 1)
         quantise_rows("q", 1, 1)
+        quantise_v(1, 0)
         weigh(NEAR1, 0)
         weigh(NEAR1, 1)
-        quantise_v(1, 0)
-        quantise_scores(FAR, 0)
-        quantise_scores(NEAR1, 0)
-        quantise_v(1, 1)
         copy_result(0, 2, 0, 512)
         copy_result(0, 2, 512, 512)
         wide_scores(FAR, 1, 0)
@@ -413,24 +409,31 @@ def tile_simplifiedretnet_pa_kernel(tc, q, k, v_bytes, v_scale, decay, out):
         mix(0, 3, 0)
         scores(NEAR1, 2)
         mix(0, 3, 1)
-        mix(1, 0, 0)
-        mix(1, 1, 0)
-        scores(NEAR1, 3)
+        join_on_gpsimd(1, 1)
         store(0, 2)
         weigh_wide(FAR, 1, 0)
+        quantise_scores(FAR, 0)
+        quantise_scores(NEAR1, 0)
+        quantise_v(1, 1)
         weigh_wide(FAR, 1, 1)
         weigh(NEAR1, 2)
         join_wide(FAR, 1, True)
         quantise_score_block(NEAR1, 2)
         quantise_scores(FAR, 1)
-        weigh(NEAR1, 3)
-        quantise_score_block(NEAR1, 3)
         copy_result(0, 3, 0, 512)
         copy_result(0, 3, 512, 512)
+        mix(1, 0, 0)
+        mix(1, 1, 0)
+        mix(1, 0, 1)
+        scores(NEAR1, 3)
+        mix(1, 1, 1)
+        store(0, 3)
+        weigh(NEAR1, 3)
+        quantise_score_block(NEAR1, 3)
         copy_result(1, 0, 0, 512)
         copy_result(1, 1, 0, 512)
-        mix(1, 0, 1)
-        mix(1, 1, 1)
+        copy_result(1, 0, 512, 512)
+        copy_result(1, 1, 512, 512)
         mix(1, 2, 0)
         mix(1, 2, 1)
         mix_far(3, 0, 256, pool=score_banks)
@@ -441,19 +444,16 @@ def tile_simplifiedretnet_pa_kernel(tc, q, k, v_bytes, v_scale, decay, out):
         mix_near(3, 256, 256)
         mix_near(3, 512, 256)
         mix_near(3, 768, 256)
-        store(0, 3)
         store(1, 0, 0, 512)
         store(1, 1, 0, 512)
+        store(1, 0, 512, 512)
+        store(1, 1, 512, 512)
         copy_result(1, 3, 256, 256, True)
         copy_result(1, 3, 768, 256, True)
-        copy_result(1, 0, 512, 512)
-        copy_result(1, 1, 512, 512)
         copy_result(1, 2, 0, 512)
         copy_result(1, 2, 512, 512)
         copy_result(1, 3, 0, 256)
         copy_result(1, 3, 512, 256)
-        store(1, 0, 512, 512)
-        store(1, 1, 512, 512)
         store(1, 2, 0, 512)
         store(1, 2, 512, 512)
         store(1, 3, 0, 256)

import math
from contextlib import ExitStack

import concourse.mybir as mybir

F32 = mybir.dt.float32
BF16 = mybir.dt.bfloat16
U32 = mybir.dt.uint32
U8 = mybir.dt.uint8
E4M3FN = mybir.dt.float8_e4m3fn
FP8X4 = mybir.dt.float8_e4m3fn_x4
ALU = mybir.AluOpType
ACT = mybir.ActivationFunctionType

FLOPS = 2 * 1024 * (512 * 512 + 512 * 1024) * 2
P = 128
CHUNK = 512
QUARTER = 256
MASKED = 2.0**100
LEAST_RATE = 2.0**-90
LOG_SCALE = -5.0 * math.log(2.0)
NEAR0, FAR, NEAR1 = (0, 0), (0, 1), (1, 1)
SCORE_BANKS = 4
WIDE_TILES = [(FAR, 0), (FAR, 1)]
WOVEN = []
REUSED = {(1, 1): ("q", 1, 1)}


def tile_simplifiedretnet_pa_kernel(tc, q, k, v_bytes, v_scale, decay, out):
    nc = tc.nc
    rows_of = {
        "q": q.rearrange("o (c b m) f -> (o c) m b f", c=2, b=4),
        "k": k.rearrange("o (c m b) f -> (o c) m b f", c=2, b=4),
    }
    v_planes = v_bytes.rearrange("o (g p r) n -> (o g) p r n", g=2, r=4)
    out_rows = out.rearrange("o (c b m) n -> (o c) m b n", c=2, b=4)

    with ExitStack() as ctx:
        keep = ctx.enter_context(tc.tile_pool(name="keep", bufs=1))
        score_banks = ctx.enter_context(tc.psum_pool(name="score_banks", bufs=SCORE_BANKS))
        other_banks = ctx.enter_context(tc.psum_pool(name="other_banks", bufs=8 - SCORE_BANKS))
        ctx.enter_context(tc.manual_schedule())

        def sb(name, shape, dtype):
            return keep.tile(shape, dtype, name=name, align_bytes=64)

        row_pairs = [(x, c, a) for x in "qk" for c in range(2) for a in range(2)]
        v_halves = [(g, h) for g in range(2) for h in range(2)]
        score_pairs = [(g, c, a) for g, c in (NEAR0, FAR, NEAR1) for a in range(2)]
        turned = {key: sb("turned_%s_%s_%s" % key, [P, 2 * CHUNK], F32) for key in row_pairs}
        x_codes = {key: sb("x_codes_%s_%s_%s" % key, [P, 512], U32) for key in row_pairs}
        x_scales = {key: sb("x_scales_%s_%s_%s" % key, [P, 512], U8) for key in row_pairs}
        v_wide = [sb("v_wide_%s" % (g,), [P, 4 * 1024], BF16) for g in range(2)]
        v_words = {key: sb("v_words_%s_%s" % key, [P, 4 * CHUNK], BF16) for key in v_halves if key not in REUSED}
        for key, rows in REUSED.items():
            v_words[key] = turned[rows][:].bitcast(BF16)
        v_codes = {key: sb("v_codes_%s_%s" % key, [P, CHUNK], U32) for key in v_halves}
        v_scales = {key: sb("v_scales_%s_%s" % key, [P, CHUNK], U8) for key in v_halves}
        gain = [sb("gain_%s" % (table,), [P, 4 * CHUNK], F32) for table in range(3)]
        s_words = {key: sb("s_words_%s_%s_%s" % key, [P, 2 * CHUNK], BF16) for key in score_pairs}
        halves = {key: sb("halves_%s_%s" % (sum(key[0]), key[1]), [P, 2 * CHUNK], BF16) for key in WIDE_TILES}
        s_codes = {key: sb("s_codes_%s_%s_%s" % key, [P, 2 * P], U32) for key in score_pairs}
        s_scales = {key: sb("s_scales_%s_%s_%s" % key, [P, 2 * P], U8) for key in score_pairs}
        result = {(c, b): sb("result_%s_%s" % (c, b), [P, 1024], F32) for c in range(2) for b in range(4)}
        ident = sb("ident", [P, P], F32)
        dist = sb("dist", [P, CHUNK + 4], F32)
        causal_dist = sb("causal_dist", [P, CHUNK + 4], F32)
        far_bias = sb("far_bias", [P, 4], F32)
        rate = [sb("rate_%s" % (g,), [P, 4], BF16) for g in range(2)]
        neg_rate = [sb("neg_rate_%s" % (g,), [P, 4], F32) for g in range(2)]
        key_scale = [sb("key_scale_%s" % (g,), [P, 4], F32) for g in range(2)]
        warm_in = sb("warm_in", [P, 8], F32)
        warm_out = sb("warm_out", [P, 8], F32)

        words = {}
        fp8 = {}
        psum = {}

        def load_rows(x, c, b):
            rows = sb("raw_%s_%s_%s" % (x, c, b), [P, 1024], BF16)
            nc.sync.dma_start(out=rows[:], in_=rows_of[x][c][:, b, :])
            words[x, c, b] = rows[:].bitcast(F32).rearrange("p (f m u) -> p f u m", f=2, u=2)

        def load_v(g, lo, hi):
            planes = sb("fp8_%s_%s" % (g, lo), [P, hi - lo, 1024], U8)
            nc.sync.dma_start(out=planes[:], in_=v_planes[g][:, lo:hi, :])
            for r in range(lo, hi):
                fp8[g, r] = planes[:, r - lo, :]

        def load_rate(g, queue):
            queue.dma_start(out=rate[g][:], in_=decay.rearrange("(g p r) -> g p r", g=2, r=4)[g])

        def load_scale(g, queue):
            queue.dma_start(out=key_scale[g][:], in_=v_scale.rearrange("o (g p r) i -> (o g) p (r i)", g=2, r=4)[g])

        def negate_rate(g):
            nc.scalar.activation(out=neg_rate[g][:], in_=rate[g][:], func=ACT.Copy, scale=-1.0, bias=-LEAST_RATE)

        def new_bank(key, pool, dtype=F32, width=CHUNK):
            psum[key] = pool.tile([P, width], dtype, name="bank")
            return psum[key]

        def turn(x, c, b, pool=other_banks):
            bank = new_bank(("turn", x, c, b), pool)[:].rearrange("p (f u m) -> p f u m", f=2, u=2)
            for f in range(2):
                for u in range(2):
                    nc.tensor.transpose(bank[:, f, u, :], words[x, c, b][:, f, u, :], ident[:])

        def copy(out, in_, on_vector):
            if on_vector:
                nc.vector.tensor_copy(out=out, in_=in_)
            else:
                nc.scalar.copy(out, in_)

        def slot(x, c, b, f):
            return 2 * f + b % 2

        def copy_turned(x, c, b, on_vector=False):
            src = psum["turn", x, c, b][:].rearrange("p (f u m) -> p f m u", f=2, u=2)
            slots = turned[x, c, b // 2][:].rearrange("p (n m u) -> p n m u", n=4, u=2)
            lo, hi = slot(x, c, b, 0), slot(x, c, b, 1)
            copy(slots[:, lo : hi + 1 : hi - lo], src, on_vector)

        def quantise_rows(x, c, a, lo=0, hi=2):
            nc.vector.quantize_mx(
                out=x_codes[x, c, a][:, 2 * P * lo : 2 * P * hi].bitcast(FP8X4),
                scales=x_scales[x, c, a][:, 2 * P * lo : 2 * P * hi],
                in_=turned[x, c, a][:, CHUNK * lo : CHUNK * hi].bitcast(BF16),
            )

        def quantise_block(x, c, b):
            for f in range(2):
                n = slot(x, c, b, f)
                nc.vector.quantize_mx(
                    out=x_codes[x, c, b // 2][:, P * n : P * (n + 1)].bitcast(FP8X4),
                    scales=x_scales[x, c, b // 2][:, P * n : P * (n + 1)],
                    in_=turned[x, c, b // 2][:, 2 * P * n : 2 * P * (n + 1)].bitcast(BF16),
                )

        def widen_v(g, r, on_vector=True):
            if g in WOVEN:
                plane = v_wide[g][:, 1024 * r : 1024 * (r + 1)]
            else:
                plane = v_wide[g][:].rearrange("p (j n e) -> p j e n", j=2, e=2)[:, r // 2, r % 2]
            if on_vector:
                nc.vector.tensor_scalar(out=plane, in0=fp8[g, r].bitcast(E4M3FN), scalar1=key_scale[g][:, r : r + 1], scalar2=None, op0=ALU.mult)
            else:
                nc.scalar.activation(out=plane, in_=fp8[g, r].bitcast(E4M3FN), func=ACT.Copy, scale=key_scale[g][:, r : r + 1])

        def join_on_gpsimd(g, h):
            pairs = v_wide[g][:].bitcast(U32).rearrange("p (j n) -> p n j", j=2)[:, CHUNK * h : CHUNK * (h + 1), :]
            nc.gpsimd.tensor_copy(out=v_words[g, h][:].bitcast(U32).rearrange("p (n j) -> p n j", j=2), in_=pairs)

        def join_v(g, h, on_vector):
            pairs = v_wide[g][:].bitcast(F32).rearrange("p (j n) -> p n j", j=2)[:, CHUNK * h : CHUNK * (h + 1), :]
            copy(v_words[g, h][:].bitcast(F32).rearrange("p (n j) -> p n j", j=2), pairs, on_vector)

        def quantise_v(g, h):
            nc.vector.quantize_mx(out=v_codes[g, h][:].bitcast(FP8X4), scales=v_scales[g, h][:], in_=v_words[g, h][:])

        def make_gain(tile, r):
            table = dist if tile == FAR else causal_dist
            nc.scalar.activation(
                out=gain[sum(tile)][:, CHUNK * r : CHUNK * (r + 1)],
                in_=table[:, 3 - r : 3 - r + CHUNK],
                func=ACT.Exp,
                bias=far_bias[:, r : r + 1] if tile == FAR else LOG_SCALE,
                scale=neg_rate[tile[0]][:, r : r + 1],
            )

        def score_passes(out_cols, tile, r, b, width):
            g, c = tile
            for f in range(2):
                keys = slice(P * slot("k", g, r, f), P * slot("k", g, r, f) + P)
                cols = slice(P * slot("q", c, b, f), P * slot("q", c, b, f) + width)
                nc.tensor.matmul_mx(
                    out=out_cols,
                    lhsT=x_codes["k", g, r // 2][:, keys].bitcast(FP8X4),
                    lhsT_scale=x_scales["k", g, r // 2][:, keys],
                    rhs=x_codes["q", c, b // 2][:, cols].bitcast(FP8X4),
                    rhs_scale=x_scales["q", c, b // 2][:, cols],
                    start=(f == 0),
                    stop=(f == 1),
                )

        def scores(tile, b, pool=score_banks):
            bank = new_bank(("scores", tile, b), pool)
            for r in range(4):
                score_passes(bank[:, P * r : P * (r + 1)], tile, r, b, P)

        def wide_scores(tile, a, j, pool=score_banks):
            bank = new_bank(("wide", tile, a, j), pool)
            for e in range(2):
                score_passes(bank[:, 2 * P * e : 2 * P * (e + 1)], tile, 2 * j + e, 2 * a, 2 * P)

        def weigh_wide(tile, a, j):
            nc.vector.tensor_tensor(
                out=halves[tile, a][:, CHUNK * j : CHUNK * (j + 1)].rearrange("p (m i e) -> p m e i", i=4, e=2),
                in0=psum["wide", tile, a, j][:].rearrange("p (e m i) -> p m e i", e=2, i=4),
                in1=gain[sum(tile)][:].rearrange("p (j e a m i) -> p j a m e i", j=2, e=2, a=2, i=4)[:, j, a],
                op=ALU.mult,
            )

        def join_wide(tile, a, on_vector):
            pairs = halves[tile, a][:].bitcast(F32).rearrange("p (j n) -> p n j", j=2)
            copy(s_words[tile + (a,)][:].bitcast(F32).rearrange("p (n j) -> p n j", j=2), pairs, on_vector)

        def weigh(tile, b):
            nc.vector.tensor_tensor(
                out=s_words[tile + (b // 2,)][:, CHUNK * (b % 2) : CHUNK * (b % 2 + 1)].rearrange("p (m i t) -> p m t i", i=2, t=4),
                in0=psum["scores", tile, b][:].rearrange("p (t m i) -> p m t i", t=4, i=2),
                in1=gain[sum(tile)][:].rearrange("p (t b m i) -> p b m t i", t=4, b=4, i=2)[:, b],
                op=ALU.mult,
            )

        def quantise_scores(tile, a, lo=0, hi=2):
            key = tile + (a,)
            nc.vector.quantize_mx(
                out=s_codes[key][:, P * lo : P * hi].bitcast(FP8X4),
                scales=s_scales[key][:, P * lo : P * hi],
                in_=s_words[key][:, CHUNK * lo : CHUNK * hi],
            )

        def quantise_score_block(tile, b):
            quantise_scores(tile, b // 2, b % 2, b % 2 + 1)

        def mix_pass(c, b, lo, width, g):
            rows = slice(P * (b % 2), P * (b % 2 + 1))
            h, cols = lo // CHUNK, slice(lo % CHUNK, lo % CHUNK + width)
            nc.tensor.matmul_mx(
                out=psum["mix", c, b, lo][:, :width],
                lhsT=s_codes[g, c, b // 2][:, rows].bitcast(FP8X4),
                lhsT_scale=s_scales[g, c, b // 2][:, rows],
                rhs=v_codes[g, h][:, cols].bitcast(FP8X4),
                rhs_scale=v_scales[g, h][:, cols],
                start=(g == 0),
                stop=(g == c),
            )

        def mix(c, b, h, pool=other_banks):
            new_bank(("mix", c, b, CHUNK * h), pool)
            for g in range(c + 1):
                mix_pass(c, b, CHUNK * h, CHUNK, g)

        def store(c, b, lo=0, width=2 * CHUNK):
            nc.sync.dma_start(out=out_rows[c][:, b, lo : lo + width], in_=result[c, b][:, lo : lo + width])

        def copy_result(c, b, lo, width=CHUNK, on_vector=False):
            copy(result[c, b][:, lo : lo + width], psum["mix", c, b, lo][:, :width], on_vector)

        def warm_up():
            nc.vector.memset(warm_in[:], 0.0)
            nc.scalar.activation(out=warm_out[:], in_=warm_in[:], func=ACT.Exp)

        def make_dist():
            nc.gpsimd.iota(dist[:], pattern=[[1, CHUNK + 4]], base=-3, channel_multiplier=-4, allow_small_or_imprecise_dtypes=True)

        def make_far_bias():
            nc.scalar.activation(out=far_bias[:], in_=rate[0][:], func=ACT.Copy, scale=-float(CHUNK), bias=LOG_SCALE)

        def make_ident():
            nc.vector.tensor_scalar(out=ident[:], in0=dist[:, 3 : 3 + CHUNK : 4], scalar1=0.0, scalar2=None, op0=ALU.is_equal)

        def make_causal():
            nc.vector.scalar_tensor_tensor(out=causal_dist[:], in0=dist[:], scalar=-MASKED, in1=dist[:], op0=ALU.mult, op1=ALU.max)

        def mix_far(b, lo, width=CHUNK, pool=other_banks):
            new_bank(("mix", 1, b, lo), pool)
            mix_pass(1, b, lo, width, 0)

        def mix_near(b, lo, width=CHUNK):
            mix_pass(1, b, lo, width, 1)

        load_rate(0, nc.scalar)
        warm_up()
        make_dist()
        load_scale(0, nc.sync)
        load_v(0, 0, 1)
        load_v(0, 2, 3)
        load_rows("q", 0, 0)
        load_rows("k", 0, 0)
        load_v(0, 1, 2)
        load_rows("k", 0, 1)
        load_v(0, 3, 4)
        load_rows("k", 0, 2)
        load_rows("k", 0, 3)
        load_rows("q", 0, 1)
        load_rows("q", 0, 2)
        load_rows("q", 0, 3)
        load_rows("q", 1, 0)
        load_v(1, 0, 2)
        load_rate(1, nc.sync)
        load_scale(1, nc.sync)
        load_rows("q", 1, 1)
        load_rows("k", 1, 0)
        load_v(1, 2, 4)
        load_rows("k", 1, 1)
        load_rows("k", 1, 2)
        load_rows("k", 1, 3)
        load_rows("q", 1, 2)
        load_rows("q", 1, 3)
        make_causal()
        make_ident()
        widen_v(0, 0)
        widen_v(0, 2)
        widen_v(0, 1)
        widen_v(0, 3)
        negate_rate(0)
        make_far_bias()
        make_gain(NEAR0, 0)
        make_gain(NEAR0, 1)
        make_gain(NEAR0, 2)
        make_gain(NEAR0, 3)
        turn("q", 0, 0)
        turn("k", 0, 0)
        turn("k", 0, 1)
        turn("k", 0, 2)
        copy_turned("q", 0, 0)
        make_gain(FAR, 0)
        copy_turned("k", 0, 0)
        copy_turned("k", 0, 1)
        copy_turned("k", 0, 2)
        turn("k", 0, 3)
        turn("q", 0, 1)
        turn("q", 0, 2)
        turn("q", 0, 3)
        quantise_block("q", 0, 0)
        join_v(0, 0, True)
        quantise_rows("k", 0, 0)
        quantise_v(0, 0)
        copy_turned("k", 0, 3)
        copy_turned("q", 0, 1)
        copy_turned("q", 0, 2)
        copy_turned("q", 0, 3)
        join_v(0, 1, False)
        negate_rate(1)
        turn("q", 1, 0)
        quantise_rows("k", 0, 1)
        quantise_block("q", 0, 1)
        widen_v(1, 0)
        quantise_rows("q", 0, 1)
        widen_v(1, 1)
        copy_turned("q", 1, 0)
        make_gain(FAR, 1)
        make_gain(FAR, 2)
        scores(NEAR0, 0)
        scores(NEAR0, 1)
        turn("q", 1, 1)
        turn("k", 1, 0)
        turn("k", 1, 1)
        scores(NEAR0, 2)
        scores(NEAR0, 3)
        turn("k", 1, 2)
        weigh(NEAR0, 0)
        quantise_v(0, 1)
        weigh(NEAR0, 1)
        widen_v(1, 2)
        quantise_scores(NEAR0, 0)
        copy_turned("q", 1, 1)
        copy_turned("k", 1, 0)
        copy_turned("k", 1, 1)
        make_gain(FAR, 3)
        make_gain(NEAR1, 0)
        copy_turned("k", 1, 2)
        turn("k", 1, 3)
        mix(0, 0, 0)
        mix(0, 0, 1)
        quantise_rows("q", 1, 0)
        quantise_rows("k", 1, 0)
        weigh(NEAR0, 2)
        widen_v(1, 3)
        copy_turned("k", 1, 3)
        copy_result(0, 0, 0, 512)
        copy_result(0, 0, 512, 512)
        make_gain(NEAR1, 1)
        wide_scores(FAR, 0, 0)
        wide_scores(FAR, 0, 1)
        turn("q", 1, 2)
        turn("q", 1, 3)
        mix(0, 1, 0)
        mix(0, 1, 1)
        join_on_gpsimd(1, 0)
        store(0, 0)
        quantise_rows("k", 1, 1)
        weigh(NEAR0, 3)
        weigh_wide(FAR, 0, 0)
        weigh_wide(FAR, 0, 1)
        quantise_scores(NEAR0, 1)
        copy_turned("q", 1, 2)
        copy_turned("q", 1, 3)
        make_gain(NEAR1, 2)
        make_gain(NEAR1, 3)
        join_wide(FAR, 0, False)
        copy_result(0, 1, 0, 512)
        copy_result(0, 1, 512, 512)
        scores(NEAR1, 0)
        scores(NEAR1, 1)
        mix(0, 2, 0)
        mix(0, 2, 1)
        store(0, 1)
        quantise_rows("q", 1, 1)
        quantise_v(1, 0)
        weigh(NEAR1, 0)
        weigh(NEAR1, 1)
        copy_result(0, 2, 0, 512)
        copy_result(0, 2, 512, 512)
        wide_scores(FAR, 1, 0)
        wide_scores(FAR, 1, 1)
        mix(0, 3, 0)
        scores(NEAR1, 2)
        mix(0, 3, 1)
        join_on_gpsimd(1, 1)
        store(0, 2)
        weigh_wide(FAR, 1, 0)
        quantise_scores(FAR, 0)
        quantise_scores(NEAR1, 0)
        quantise_v(1, 1)
        weigh_wide(FAR, 1, 1)
        weigh(NEAR1, 2)
        join_wide(FAR, 1, True)
        quantise_score_block(NEAR1, 2)
        quantise_scores(FAR, 1)
        copy_result(0, 3, 0, 512)
        copy_result(0, 3, 512, 512)
        mix(1, 0, 0)
        mix(1, 1, 0)
        mix(1, 0, 1)
        scores(NEAR1, 3)
        mix(1, 1, 1)
        store(0, 3)
        weigh(NEAR1, 3)
        quantise_score_block(NEAR1, 3)
        copy_result(1, 0, 0, 512)
        copy_result(1, 1, 0, 512)
        copy_result(1, 0, 512, 512)
        copy_result(1, 1, 512, 512)
        mix(1, 2, 0)
        mix(1, 2, 1)
        mix_far(3, 0, 256, pool=score_banks)
        mix_far(3, 256, 256, pool=score_banks)
        mix_far(3, 512, 256, pool=score_banks)
        mix_far(3, 768, 256, pool=score_banks)
        mix_near(3, 0, 256)
        mix_near(3, 256, 256)
        mix_near(3, 512, 256)
        mix_near(3, 768, 256)
        store(1, 0, 0, 512)
        store(1, 1, 0, 512)
        store(1, 0, 512, 512)
        store(1, 1, 512, 512)
        copy_result(1, 3, 256, 256, True)
        copy_result(1, 3, 768, 256, True)
        copy_result(1, 2, 0, 512)
        copy_result(1, 2, 512, 512)
        copy_result(1, 3, 0, 256)
        copy_result(1, 3, 512, 256)
        store(1, 2, 0, 512)
        store(1, 2, 512, 512)
        store(1, 3, 0, 256)
        store(1, 3, 256, 256)
        store(1, 3, 512, 256)
        store(1, 3, 768, 256)
